import numpy as np
import ml_dtypes


def mxq(x, axis, fmt="e4m3"):
    dtype, down = {"e4m3": (ml_dtypes.float8_e4m3fn, 7), "e5m2": (ml_dtypes.float8_e5m2, 14)}[fmt]
    v = np.moveaxis(np.asarray(x, np.float32).astype(ml_dtypes.bfloat16).astype(np.float64), axis, -1)
    blocks = v.reshape(v.shape[:-1] + (-1, 32))
    amax = np.abs(blocks).max(-1, keepdims=True)
    byte = np.maximum(np.where(amax > 0, np.frexp(amax)[1] - 1 + 127, 0) - down, 1)
    scale = np.exp2(byte - 127.0)
    codes = (blocks / scale).astype(np.float32).astype(dtype).astype(np.float64)
    return np.moveaxis((codes * scale).reshape(v.shape), -1, axis)


WIDE = False


def mx_kscale(k):
    if not WIDE:
        return np.ones(k)
    levels = np.array([10, -10, 5, -5, 0])
    a = np.random.permutation(np.resize(levels, k // 512 * 4)).reshape(k // 512, 4)
    idx = np.arange(k)
    return np.exp2(a[idx // 512, idx % 128 // 32])


BF16 = ml_dtypes.bfloat16


def bf(x):
    return np.asarray(x, np.float32).astype(BF16)


def f64(x):
    return np.asarray(x).astype(np.float64)


E2M1 = np.array([0.0, 0.5, 1.0, 1.5, 2.0, 3.0, 4.0, 6.0, -0.0, -0.5, -1.0, -1.5, -2.0, -3.0, -4.0, -6.0])


def pack_weight(w, fmt):
    k, n = w.shape
    w = f64(bf(w)).reshape(k // 32, 32, n)
    amax = np.abs(w).max(1)
    if fmt == "e4m3":
        byte = np.frexp(amax)[1] - 1 + 127 - 7
    else:
        mant, ex = np.frexp(amax / 6.0)
        byte = np.where(mant > 0.5, ex, ex - 1) + 127
    byte = np.clip(np.where(amax > 0, byte, 1), 1, 254)
    scaled = (w * np.exp2(127.0 - byte)[:, None, :]).reshape(k, n).astype(np.float32)
    by_word = np.ascontiguousarray(scaled.reshape(k // 512, 128, 4, n).transpose(0, 1, 3, 2))
    if fmt == "e4m3":
        words = by_word.astype(ml_dtypes.float8_e4m3fn).view(np.uint8)
    else:
        c = by_word.astype(ml_dtypes.float4_e2m1fn).view(np.uint8) & 0xF
        words = c[..., 0::2] | (c[..., 1::2] << 4)
    return np.ascontiguousarray(words), np.ascontiguousarray(byte.astype(np.uint8).reshape(k // 512, 16, n))


def unpack_weight(words, scales, fmt):
    g, p, n, _ = words.shape
    if fmt == "e4m3":
        vals = np.ascontiguousarray(words).view(ml_dtypes.float8_e4m3fn).astype(np.float64)
    else:
        nib = np.empty((g, p, n, 4), np.uint8)
        nib[..., 0::2] = words & 0xF
        nib[..., 1::2] = words >> 4
        vals = E2M1[nib]
    vals = vals * np.repeat(np.exp2(scales.astype(np.float64) - 127.0), 8, axis=1)[..., None]
    return vals.transpose(0, 1, 3, 2).reshape(g * 512, n)

def pack4(w):
    words, scales = pack_weight(w, "e2m1")
    return words.reshape(words.shape[0], 128, -1), scales


def unpack4(words, scales):
    return unpack_weight(words.reshape(words.shape[0], 128, -1, 2), scales, "e2m1")


B, N, D, H, NS, SK1, SK2 = 1, 2048, 1024, 16, 10, 512, 1024
HD = D // H
D4 = np.array([0.4829629131445341, 0.8365163037378079, 0.2241438680420134, -0.1294095225512604])
TAPS = len(D4)
SPARSE_DILATIONS = (SK1, SK2)


def softmax(v, axis):
    e = np.exp(v - v.max(axis, keepdims=True))
    return e / e.sum(axis, keepdims=True)


def sigmoid(v):
    return 1.0 / (1.0 + np.exp(-v))


def shift_right(t, s):
    if s == 0:
        return t
    return np.pad(t, ((0, 0), (0, 0), (s, 0), (0, 0)))[:, :, :N, :]


def to_heads(t):
    return t.reshape(B, N, H, HD).transpose(0, 2, 1, 3)


def setup_inputs():
    s = mx_kscale(D)
    x = bf(np.random.standard_normal((B, N, D)) * s)
    Wkv_words, Wkv_scales = pack4(np.random.standard_normal((D, D + D)) * D ** -0.5 / s[:, None])
    return {"x": x,
            "Wkv_words": Wkv_words,
            "Wkv_scales": Wkv_scales,
            "bkv": bf(np.random.standard_normal(D + D) * 0.2),
            "scale_gain": bf(np.random.standard_normal((NS, H)) * 0.5),
            "skip_w": bf(-1.0 + np.random.standard_normal(len(SPARSE_DILATIONS)) * 0.3)}


def reference(x, Wkv_words, Wkv_scales, bkv, scale_gain, skip_w):
    kv = (mxq(f64(x), 2, "e4m3") @ unpack4(Wkv_words, Wkv_scales)) + f64(bkv)
    k, v = to_heads(kv[..., :D]), to_heads(kv[..., D:])
    k_mag = np.sqrt((k * k).sum(-1, keepdims=True))
    field = v * k_mag
    gains = softmax(f64(scale_gain), 0)
    acc = np.zeros_like(field)
    for j in range(NS):
        d = 1 << j
        y = sum(D4[t] * shift_right(field, (TAPS - 1 - t) * d) for t in range(TAPS))
        acc = acc + gains[j][None, :, None, None] * y
    field = acc
    sw = sigmoid(f64(skip_w))
    skip = sum(sw[i] * shift_right(field, d) for i, d in enumerate(SPARSE_DILATIONS))
    return field + skip

@@ -1,0 +1,350 @@
+from contextlib import ExitStack
+
+import concourse.mybir as mybir
+from concourse.masks import make_identity
+
+F32 = mybir.dt.float32
+BF16 = mybir.dt.bfloat16
+I32 = mybir.dt.int32
+U32 = mybir.dt.uint32
+U8 = mybir.dt.uint8
+FP8X4 = mybir.dt.float8_e4m3fn_x4
+FP4X4 = mybir.dt.float4_e2m1fn_x4
+ALU = mybir.AluOpType
+ACT = mybir.ActivationFunctionType
+AXIS = mybir.AxisListType
+
+P = 128
+TOKENS = 2048
+DIM = 1024
+HEADS = 16
+HEAD_DIM = 64
+PAIRS = HEADS // 2
+SCALES = 10
+D4 = (0.4829629131445341, 0.8365163037378079, 0.2241438680420134, -0.1294095225512604)
+SKIPS = (512, 1024)
+K_PASS = 512
+K_PASSES = DIM // K_PASS
+BANK = 512
+
+STRIDE = 8
+CLASS_LEN = TOKENS // STRIDE
+BLOCKS = CLASS_LEN // P
+ROWS_PER_BANK = BANK // CLASS_LEN
+BANKS = TOKENS // BANK
+PAD = 8
+PERIOD = CLASS_LEN + P
+
+FLOPS = 2 * TOKENS * DIM * 2 * DIM
+
+
+def tap_terms():
+    terms = {}
+    for j in range(SCALES):
+        for t in range(3):
+            shift = (3 - t) * 2**j
+            if shift not in terms:
+                terms[shift] = []
+            terms[shift].append((j, D4[t]))
+    return terms
+
+
+def tile_causalwaveletfieldattentionh_pa_kernel(tc, x, Wkv_words, Wkv_scales, bkv, scale_gain, skip_w, out):
+    nc = tc.nc
+    terms = tap_terms()
+    long_shifts = [s for s in sorted(terms) if s % STRIDE == 0]
+    short_shifts = [s for s in sorted(terms) if s % STRIDE != 0]
+    hop = SKIPS[0] // STRIDE
+
+    with ExitStack() as ctx:
+        const = ctx.enter_context(tc.tile_pool(name="const", bufs=1))
+        setup = ctx.enter_context(tc.tile_pool(name="setup", bufs=1))
+        x_pool = ctx.enter_context(tc.tile_pool(name="x_pool", bufs=BANKS))
+        grouped_pool = ctx.enter_context(tc.tile_pool(name="grouped_pool", bufs=2))
+        single = ctx.enter_context(tc.tile_pool(name="single", bufs=1))
+        double = ctx.enter_context(tc.tile_pool(name="double", bufs=2))
+        psum_mx = ctx.enter_context(tc.psum_pool(name="psum_mx", bufs=3))
+        psum_tr = ctx.enter_context(tc.psum_pool(name="psum_tr", bufs=2))
+        psum_sum = ctx.enter_context(tc.psum_pool(name="psum_sum", bufs=2))
+        psum_small = ctx.enter_context(tc.psum_pool(name="psum_small", bufs=1))
+
+        w_scales = const.tile([P, K_PASSES, 2 * DIM], U8, name="w_scales", align_bytes=64)
+        nc.vector.memset(w_scales[:].bitcast(I32), 0)
+        for g in range(K_PASSES):
+            for quad in range(4):
+                nc.sync.dma_start(
+                    out=w_scales[32 * quad : 32 * quad + 4, g, :].bitcast(I32),
+                    in_=Wkv_scales[g, 4 * quad : 4 * quad + 4, :].bitcast(I32),
+                )
+
+        x_view = x.flatten_outer_dims().rearrange("(b p a) k -> p b a k", b=BLOCKS, p=P, a=STRIDE)
+        x_rows = []
+        w_words = const.tile([P, K_PASSES, 4 * DIM], U8, name="w_words", align_bytes=64)
+        for j in range(BANKS):
+            rows = x_pool.tile([P, BLOCKS, ROWS_PER_BANK, DIM], BF16, name="x_rows")
+            nc.sync.dma_start(out=rows[:], in_=x_view[:, :, ROWS_PER_BANK * j : ROWS_PER_BANK * (j + 1), :])
+            x_rows.append(rows)
+            if j == 0:
+                for g in range(K_PASSES):
+                    nc.sync.dma_start(out=w_words[:, g, :].bitcast(I32), in_=Wkv_words[g].bitcast(I32))
+
+        gain_bf = setup.tile([P, SCALES * HEADS], BF16, name="gain_bf")
+        nc.scalar.dma_start(out=gain_bf[:], in_=scale_gain.rearrange("j h -> (j h)").partition_broadcast(P))
+        skip_bf = setup.tile([P, len(SKIPS)], BF16, name="skip_bf")
+        nc.scalar.dma_start(out=skip_bf[:], in_=skip_w.partition_broadcast(P))
+        bias_bf = setup.tile([2 * PAIRS, P], BF16, name="bias_bf")
+        nc.scalar.dma_start(out=bias_bf[:], in_=bkv.rearrange("(t c) -> t c", c=P))
+
+        ident = const.tile([P, P], F32, name="ident")
+        make_identity(nc, ident[:])
+        coef_row = setup.tile([P, HEADS, PERIOD], F32, name="coef_row")
+        nc.gpsimd.memset(coef_row[:], 0.0)
+        head_sel = const.tile([P, 2], F32, name="head_sel")
+        nc.vector.memset(head_sel[:], 0.0)
+        nc.vector.memset(head_sel[0:HEAD_DIM, 0:1], 1.0)
+        nc.vector.memset(head_sel[HEAD_DIM:P, 1:2], 1.0)
+        field_t_tiles = []
+        for i in range(2):
+            field_tile = const.tile([P, STRIDE, PAD + CLASS_LEN], F32, name="field_t%d" % i)
+            nc.vector.memset(field_tile[:, :, 0:PAD], 0.0)
+            field_t_tiles.append(field_tile)
+
+        bias_rows = setup.tile([P, P], F32, name="bias_rows")
+        nc.vector.memset(bias_rows[:], 0.0)
+        nc.vector.tensor_copy(out=bias_rows[0 : 2 * PAIRS, :], in_=bias_bf[:])
+        bias_ps = psum_small.tile([P, P], F32, name="bias_ps", tag="small")
+        nc.tensor.transpose(bias_ps[:], bias_rows[:], ident[:])
+        bias_col = const.tile([P, 2 * PAIRS], F32, name="bias_col")
+        nc.vector.tensor_copy(out=bias_col[:], in_=bias_ps[:, 0 : 2 * PAIRS])
+
+        x_codes = const.tile([P, K_PASSES, TOKENS], U32, name="x_codes", align_bytes=64)
+        x_scales = const.tile([P, K_PASSES, TOKENS], U8, name="x_scales", align_bytes=64)
+        for j in range(BANKS):
+            for g in range(K_PASSES):
+                grouped = grouped_pool.tile([P, 4 * BANK], BF16, name="grouped", align_bytes=64)
+                grouped_words = grouped[:].bitcast(F32)
+                for half in range(2):
+                    xt = psum_mx.tile([P, 2, BANK // 2], F32, name="xt", tag="acc")
+                    for i in range(2):
+                        a_local, b = divmod(2 * half + i, BLOCKS)
+                        words = x_rows[j][:, b, a_local, :].bitcast(F32)
+                        for u in range(2):
+                            nc.tensor.transpose(
+                                xt[:, u, P * i : P * (i + 1)], words[:, 256 * g + u : 256 * (g + 1) : 2], ident[:]
+                            )
+                    dest = grouped_words[:, BANK * half : BANK * (half + 1)].rearrange("p (t u) -> p t u", u=2)
+                    if half == 0:
+                        nc.vector.tensor_copy(out=dest, in_=xt[:].rearrange("p u t -> p t u"))
+                    else:
+                        nc.scalar.copy(out=dest, in_=xt[:].rearrange("p u t -> p t u"))
+                cols = slice(BANK * j, BANK * (j + 1))
+                nc.vector.quantize_mx(out=x_codes[:, g, cols].bitcast(FP8X4), scales=x_scales[:, g, cols], in_=grouped[:])
+
+        gains = setup.tile([P, SCALES, HEADS], F32, name="gains")
+        nc.vector.tensor_copy(out=gains[:].rearrange("p j h -> p (j h)"), in_=gain_bf[:])
+        top = setup.tile([P, HEADS], F32, name="top")
+        nc.vector.tensor_reduce(out=top[:], in_=gains[:].rearrange("p j h -> p h j"), axis=AXIS.X, op=ALU.max)
+        nc.vector.tensor_tensor(
+            out=gains[:], in0=gains[:], in1=top[:].unsqueeze(1).to_broadcast([P, SCALES, HEADS]), op=ALU.subtract
+        )
+        nc.scalar.activation(out=gains[:], in_=gains[:], func=ACT.Exp)
+        total = setup.tile([P, HEADS], F32, name="total")
+        nc.vector.tensor_reduce(out=total[:], in_=gains[:].rearrange("p j h -> p h j"), axis=AXIS.X, op=ALU.add)
+        inverse = setup.tile([P, HEADS], F32, name="inverse")
+        nc.vector.reciprocal(out=inverse[:], in_=total[:])
+        nc.vector.tensor_tensor(
+            out=gains[:], in0=gains[:], in1=inverse[:].unsqueeze(1).to_broadcast([P, SCALES, HEADS]), op=ALU.mult
+        )
+        skip_f32 = setup.tile([P, len(SKIPS)], F32, name="skip_f32")
+        nc.vector.tensor_copy(out=skip_f32[:], in_=skip_bf[:])
+        skip_gate = const.tile([P, len(SKIPS)], F32, name="skip_gate")
+        nc.scalar.activation(out=skip_gate[:], in_=skip_f32[:], func=ACT.Sigmoid)
+
+        def write_coefficient(dest, shift):
+            for i, (j, weight) in enumerate(terms[shift]):
+                if i == 0:
+                    nc.vector.tensor_scalar_mul(out=dest, in0=gains[:, j, :], scalar1=weight)
+                else:
+                    nc.vector.scalar_tensor_tensor(
+                        out=dest, in0=gains[:, j, :], scalar=weight, in1=dest, op0=ALU.mult, op1=ALU.add
+                    )
+
+        def add_skips(rows):
+            for block in range(CLASS_LEN // hop - 1, 0, -1):
+                for i in range(len(SKIPS)):
+                    source = block - SKIPS[i] // SKIPS[0]
+                    if source >= 0:
+                        nc.vector.scalar_tensor_tensor(
+                            out=rows[:, :, hop * block : hop * (block + 1)],
+                            in0=rows[:, :, hop * source : hop * (source + 1)],
+                            scalar=skip_gate[:, i : i + 1],
+                            in1=rows[:, :, hop * block : hop * (block + 1)],
+                            op0=ALU.mult,
+                            op1=ALU.add,
+                        )
+
+        short_all = setup.tile([P, len(short_shifts), HEADS], F32, name="short_all")
+        for i, shift in enumerate(short_shifts):
+            write_coefficient(short_all[:, i, :], shift)
+        short_coef = const.tile([P, PAIRS, len(short_shifts)], F32, name="short_coef")
+        for half in range(2):
+            rows = slice(HEAD_DIM * half, HEAD_DIM * (half + 1))
+            by_pair = short_all[rows, :, :].rearrange("p s (c w) -> p c s w", w=2)
+            nc.vector.tensor_copy(out=short_coef[rows, :, :], in_=by_pair[:, :, :, half])
+
+        gain_sum = setup.tile([P, HEADS], F32, name="gain_sum")
+        nc.vector.tensor_reduce(out=gain_sum[:], in_=gains[:].rearrange("p j h -> p h j"), axis=AXIS.X, op=ALU.add)
+        nc.vector.tensor_scalar_mul(out=coef_row[:, :, 0], in0=gain_sum[:], scalar1=D4[3])
+        for shift in long_shifts:
+            write_coefficient(coef_row[:, :, shift // STRIDE], shift)
+        add_skips(coef_row)
+        scratch = out.rearrange("o h n e -> (o h n e)")[0 : HEADS * P * PERIOD]
+        nc.gpsimd.dma_start(out=scratch.rearrange("(h r i) -> r h i", h=HEADS, r=P), in_=coef_row[:])
+        toeplitz = const.tile([P, HEADS, CLASS_LEN], F32, name="toeplitz")
+        skewed = scratch.rearrange("(h z) -> h z", h=HEADS)[:, 0 : P * (PERIOD - 1)].rearrange("h (r w) -> r h w", r=P)
+        nc.gpsimd.dma_start(out=toeplitz[:], in_=skewed[:, :, 0:CLASS_LEN])
+
+        k_square, v_t, mag_rep, mag_t, field_q, short_t, result = {}, {}, {}, {}, {}, {}, {}
+
+        def project(column_block, j, func, dest):
+            cols = slice(BANK * j, BANK * (j + 1))
+            acc = psum_mx.tile([P, BANK], F32, name="acc")
+            for g in range(K_PASSES):
+                nc.tensor.matmul_mx(
+                    out=acc[:],
+                    lhsT=w_words[:, g, 2 * P * column_block : 2 * P * (column_block + 1)].bitcast(FP4X4),
+                    lhsT_scale=w_scales[:, g, P * column_block : P * (column_block + 1)],
+                    rhs=x_codes[:, g, cols].bitcast(FP8X4),
+                    rhs_scale=x_scales[:, g, cols],
+                    start=(g == 0),
+                    stop=(g == K_PASSES - 1),
+                )
+            nc.scalar.activation(out=dest[:, cols], in_=acc[:], func=func, bias=bias_col[:, column_block : column_block + 1])
+
+        def project_and_norm(pair):
+            k_square[pair] = single.tile([P, TOKENS], F32, name="k_square")
+            v_t[pair] = double.tile([P, TOKENS], F32, name="v_t")
+            for j in range(BANKS):
+                project(pair, j, ACT.Square, k_square[pair])
+            norm_ps = psum_small.tile([P, 2 * TOKENS // P], F32, name="norm_ps", tag="small")
+            for j in range(BANKS):
+                project(PAIRS + pair, j, ACT.Identity, v_t[pair])
+                for t in range(4 * j, 4 * j + 4):
+                    nc.tensor.matmul(
+                        out=norm_ps[:, 2 * t : 2 * t + 2],
+                        lhsT=k_square[pair][:, P * t : P * (t + 1)],
+                        rhs=head_sel[:],
+                        start=True,
+                        stop=True,
+                    )
+            mag_rep[pair] = single.tile([P, TOKENS], F32, name="mag_rep")
+            nc.scalar.activation(
+                out=mag_rep[pair][:].rearrange("p (g e) -> p g e", e=HEAD_DIM),
+                in_=norm_ps[:].unsqueeze(2).to_broadcast([P, 2 * TOKENS // P, HEAD_DIM]),
+                func=ACT.Sqrt,
+            )
+
+        def turn_mag(pair, j):
+            if j == 0:
+                mag_t[pair] = double.tile([P, TOKENS], F32, name="mag_t")
+            turned = psum_tr.tile([P, BANK], F32, name="turned")
+            for i in range(4):
+                t = 4 * j + i
+                nc.tensor.transpose(turned[:, P * i : P * (i + 1)], mag_rep[pair][:, P * t : P * (t + 1)], ident[:])
+            nc.scalar.copy(out=mag_t[pair][:, BANK * j : BANK * (j + 1)], in_=turned[:])
+
+        def shifted_field(field_t, shift, row0, row1):
+            steps, residue = divmod(shift, STRIDE)
+            if row0 >= residue:
+                source, back = row0 - residue, steps
+            else:
+                source, back = row0 - residue + STRIDE, steps + 1
+            return field_t[:, source : source + row1 - row0, PAD - back : PAD - back + CLASS_LEN]
+
+        def field_and_short_shifts(pair):
+            field_t = field_t_tiles[pair % 2]
+            nc.vector.tensor_tensor(
+                out=field_t[:, :, PAD:],
+                in0=v_t[pair][:].rearrange("p (a q) -> p a q", a=STRIDE),
+                in1=mag_t[pair][:].rearrange("p (a q) -> p a q", a=STRIDE),
+                op=ALU.mult,
+            )
+            short_t[pair] = double.tile([P, STRIDE, CLASS_LEN], F32, name="short_t")
+            for i, shift in enumerate(short_shifts):
+                residue = shift % STRIDE
+                for row0, row1 in ((residue, STRIDE), (0, residue)):
+                    if i == 0:
+                        nc.vector.tensor_scalar_mul(
+                            out=short_t[pair][:, row0:row1, :],
+                            in0=shifted_field(field_t, shift, row0, row1),
+                            scalar1=short_coef[:, pair, i : i + 1],
+                        )
+                    else:
+                        nc.vector.scalar_tensor_tensor(
+                            out=short_t[pair][:, row0:row1, :],
+                            in0=shifted_field(field_t, shift, row0, row1),
+                            scalar=short_coef[:, pair, i : i + 1],
+                            in1=short_t[pair][:, row0:row1, :],
+                            op0=ALU.mult,
+                            op1=ALU.add,
+                        )
+            add_skips(short_t[pair])
+
+        def turn_field(pair, j):
+            if j == 0:
+                field_q[pair] = double.tile([P, BLOCKS, 2, STRIDE, HEAD_DIM], F32, name="field_q")
+            b, group = divmod(j, STRIDE // 4)
+            turned = psum_tr.tile([P, BANK], F32, name="turned")
+            for i in range(4):
+                nc.tensor.transpose(
+                    turned[:, P * i : P * (i + 1)],
+                    field_t_tiles[pair % 2][:, 4 * group + i, PAD + P * b : PAD + P * (b + 1)],
+                    ident[:],
+                )
+            nc.scalar.copy(
+                out=field_q[pair][:, b, :, 4 * group : 4 * group + 4, :],
+                in_=turned[:].rearrange("p (a h e) -> p h a e", a=4, h=2),
+            )
+
+        def sum_and_store(pair, j):
+            if j == 0:
+                result[pair] = double.tile([P, BLOCKS, 2, STRIDE, HEAD_DIM], F32, name="result")
+            b, group = divmod(j, STRIDE // 4)
+            rows = slice(4 * group, 4 * group + 4)
+            summed = psum_sum.tile([P, 4, 2, HEAD_DIM], F32, name="summed")
+            for half in range(2):
+                for source in range(b + 1):
+                    nc.tensor.matmul(
+                        out=summed[:, :, half, :],
+                        lhsT=toeplitz[:, 2 * pair + half, P * (b - source) : P * (b - source + 1)],
+                        rhs=field_q[pair][:, source, half, rows, :],
+                        start=(half == 0 and source == 0),
+                        stop=False,
+                    )
+            for i in range(4):
+                nc.tensor.matmul(
+                    out=summed[:, i, :, :],
+                    lhsT=short_t[pair][:, 4 * group + i, P * b : P * (b + 1)],
+                    rhs=ident[:].rearrange("p (h e) -> p h e", h=2),
+                    is_transpose=True,
+                    start=False,
+                    stop=(i == 3),
+                )
+            nc.scalar.copy(out=result[pair][:, b, :, rows, :], in_=summed[:].rearrange("p a h e -> p h a e"))
+            if group == STRIDE // 4 - 1:
+                out_view = out[0, 2 * pair : 2 * pair + 2].rearrange("h (b p a) e -> b p h (a e)", b=BLOCKS, p=P, a=STRIDE)
+                nc.sync.dma_start(out=out_view[b], in_=result[pair][:, b].rearrange("p h a e -> p h (a e)"))
+
+        with tc.manual_schedule():
+            for step in range(PAIRS + 2):
+                if step < PAIRS:
+                    project_and_norm(step)
+                if 1 <= step <= PAIRS:
+                    field_and_short_shifts(step - 1)
+                for j in range(BANKS):
+                    if step >= 2:
+                        sum_and_store(step - 2, j)
+                    if step < PAIRS:
+                        turn_mag(step, j)
+                    if 1 <= step <= PAIRS:
+                        turn_field(step - 1, j)

@@ -53,7 +53,7 @@ def tile_causalwaveletfieldattentionh_pa_kernel(tc, x, Wkv_words, Wkv_scales, bk
     nc = tc.nc
     terms = tap_terms()
     long_shifts = [s for s in sorted(terms) if s % STRIDE == 0]
-    short_shifts = [s for s in sorted(terms) if s % STRIDE != 0]
+    short_shifts = sorted([s for s in terms if s % STRIDE != 0], key=lambda s: (s % STRIDE, s))
     hop = SKIPS[0] // STRIDE
 
     with ExitStack() as ctx:
@@ -67,6 +67,14 @@ def tile_causalwaveletfieldattentionh_pa_kernel(tc, x, Wkv_words, Wkv_scales, bk
         psum_tr = ctx.enter_context(tc.psum_pool(name="psum_tr", bufs=2))
         psum_sum = ctx.enter_context(tc.psum_pool(name="psum_sum", bufs=2))
         psum_small = ctx.enter_context(tc.psum_pool(name="psum_small", bufs=1))
+        ctx.enter_context(tc.manual_schedule())
+
+        gain_bf = setup.tile([P, SCALES * HEADS], BF16, name="gain_bf")
+        nc.scalar.dma_start(out=gain_bf[:], in_=scale_gain.rearrange("j h -> (j h)").partition_broadcast(P))
+        skip_bf = setup.tile([P, len(SKIPS)], BF16, name="skip_bf")
+        nc.scalar.dma_start(out=skip_bf[:], in_=skip_w.partition_broadcast(P))
+        bias_bf = setup.tile([2 * PAIRS, P], BF16, name="bias_bf")
+        nc.scalar.dma_start(out=bias_bf[:], in_=bkv.rearrange("(t c) -> t c", c=P))
 
         w_scales = const.tile([P, K_PASSES, 2 * DIM], U8, name="w_scales", align_bytes=64)
         nc.vector.memset(w_scales[:].bitcast(I32), 0)
@@ -88,13 +96,6 @@ def tile_causalwaveletfieldattentionh_pa_kernel(tc, x, Wkv_words, Wkv_scales, bk
                 for g in range(K_PASSES):
                     nc.sync.dma_start(out=w_words[:, g, :].bitcast(I32), in_=Wkv_words[g].bitcast(I32))
 
-        gain_bf = setup.tile([P, SCALES * HEADS], BF16, name="gain_bf")
-        nc.scalar.dma_start(out=gain_bf[:], in_=scale_gain.rearrange("j h -> (j h)").partition_broadcast(P))
-        skip_bf = setup.tile([P, len(SKIPS)], BF16, name="skip_bf")
-        nc.scalar.dma_start(out=skip_bf[:], in_=skip_w.partition_broadcast(P))
-        bias_bf = setup.tile([2 * PAIRS, P], BF16, name="bias_bf")
-        nc.scalar.dma_start(out=bias_bf[:], in_=bkv.rearrange("(t c) -> t c", c=P))
-
         ident = const.tile([P, P], F32, name="ident")
         make_identity(nc, ident[:])
         coef_row = setup.tile([P, HEADS, PERIOD], F32, name="coef_row")
@@ -103,11 +104,14 @@ def tile_causalwaveletfieldattentionh_pa_kernel(tc, x, Wkv_words, Wkv_scales, bk
         nc.vector.memset(head_sel[:], 0.0)
         nc.vector.memset(head_sel[0:HEAD_DIM, 0:1], 1.0)
         nc.vector.memset(head_sel[HEAD_DIM:P, 1:2], 1.0)
-        field_t_tiles = []
-        for i in range(2):
+        field_tiles = []
+        for i in range(3):
             field_tile = const.tile([P, STRIDE, PAD + CLASS_LEN], F32, name="field_t%d" % i)
             nc.vector.memset(field_tile[:, :, 0:PAD], 0.0)
-            field_t_tiles.append(field_tile)
+            field_tiles.append(field_tile)
+
+        mag_q = const.tile([P, P], F32, name="mag_q")
+        nc.vector.memset(mag_q[:], 0.0)
 
         bias_rows = setup.tile([P, P], F32, name="bias_rows")
         nc.vector.memset(bias_rows[:], 0.0)
@@ -117,9 +121,30 @@ def tile_causalwaveletfieldattentionh_pa_kernel(tc, x, Wkv_words, Wkv_scales, bk
         bias_col = const.tile([P, 2 * PAIRS], F32, name="bias_col")
         nc.vector.tensor_copy(out=bias_col[:], in_=bias_ps[:, 0 : 2 * PAIRS])
 
+        gains = setup.tile([P, SCALES, HEADS], F32, name="gains")
+        nc.vector.tensor_copy(out=gains[:].rearrange("p j h -> p (j h)"), in_=gain_bf[:])
+        top = setup.tile([P, HEADS], F32, name="top")
+        nc.vector.tensor_reduce(out=top[:], in_=gains[:].rearrange("p j h -> p h j"), axis=AXIS.X, op=ALU.max)
+        nc.vector.tensor_tensor(
+            out=gains[:], in0=gains[:], in1=top[:].unsqueeze(1).to_broadcast([P, SCALES, HEADS]), op=ALU.subtract
+        )
+        nc.scalar.activation(out=gains[:], in_=gains[:], func=ACT.Exp)
+        skip_f32 = setup.tile([P, len(SKIPS)], F32, name="skip_f32")
+        nc.vector.tensor_copy(out=skip_f32[:], in_=skip_bf[:])
+        skip_gate = const.tile([P, len(SKIPS)], F32, name="skip_gate")
+        nc.scalar.activation(out=skip_gate[:], in_=skip_f32[:], func=ACT.Sigmoid)
+        total = setup.tile([P, HEADS], F32, name="total")
+        nc.vector.tensor_reduce(out=total[:], in_=gains[:].rearrange("p j h -> p h j"), axis=AXIS.X, op=ALU.add)
+        inverse = setup.tile([P, HEADS], F32, name="inverse")
+        nc.vector.reciprocal(out=inverse[:], in_=total[:])
+        nc.vector.tensor_tensor(
+            out=gains[:], in0=gains[:], in1=inverse[:].unsqueeze(1).to_broadcast([P, SCALES, HEADS]), op=ALU.mult
+        )
+
         x_codes = const.tile([P, K_PASSES, TOKENS], U32, name="x_codes", align_bytes=64)
         x_scales = const.tile([P, K_PASSES, TOKENS], U8, name="x_scales", align_bytes=64)
-        for j in range(BANKS):
+
+        def quantise_bank(j):
             for g in range(K_PASSES):
                 grouped = grouped_pool.tile([P, 4 * BANK], BF16, name="grouped", align_bytes=64)
                 grouped_words = grouped[:].bitcast(F32)
@@ -139,26 +164,6 @@ def tile_causalwaveletfieldattentionh_pa_kernel(tc, x, Wkv_words, Wkv_scales, bk
                         nc.scalar.copy(out=dest, in_=xt[:].rearrange("p u t -> p t u"))
                 cols = slice(BANK * j, BANK * (j + 1))
                 nc.vector.quantize_mx(out=x_codes[:, g, cols].bitcast(FP8X4), scales=x_scales[:, g, cols], in_=grouped[:])
-
-        gains = setup.tile([P, SCALES, HEADS], F32, name="gains")
-        nc.vector.tensor_copy(out=gains[:].rearrange("p j h -> p (j h)"), in_=gain_bf[:])
-        top = setup.tile([P, HEADS], F32, name="top")
-        nc.vector.tensor_reduce(out=top[:], in_=gains[:].rearrange("p j h -> p h j"), axis=AXIS.X, op=ALU.max)
-        nc.vector.tensor_tensor(
-            out=gains[:], in0=gains[:], in1=top[:].unsqueeze(1).to_broadcast([P, SCALES, HEADS]), op=ALU.subtract
-        )
-        nc.scalar.activation(out=gains[:], in_=gains[:], func=ACT.Exp)
-        total = setup.tile([P, HEADS], F32, name="total")
-        nc.vector.tensor_reduce(out=total[:], in_=gains[:].rearrange("p j h -> p h j"), axis=AXIS.X, op=ALU.add)
-        inverse = setup.tile([P, HEADS], F32, name="inverse")
-        nc.vector.reciprocal(out=inverse[:], in_=total[:])
-        nc.vector.tensor_tensor(
-            out=gains[:], in0=gains[:], in1=inverse[:].unsqueeze(1).to_broadcast([P, SCALES, HEADS]), op=ALU.mult
-        )
-        skip_f32 = setup.tile([P, len(SKIPS)], F32, name="skip_f32")
-        nc.vector.tensor_copy(out=skip_f32[:], in_=skip_bf[:])
-        skip_gate = const.tile([P, len(SKIPS)], F32, name="skip_gate")
-        nc.scalar.activation(out=skip_gate[:], in_=skip_f32[:], func=ACT.Sigmoid)
 
         def write_coefficient(dest, shift):
             for i, (j, weight) in enumerate(terms[shift]):
@@ -183,28 +188,30 @@ def tile_causalwaveletfieldattentionh_pa_kernel(tc, x, Wkv_words, Wkv_scales, bk
                             op1=ALU.add,
                         )
 
-        short_all = setup.tile([P, len(short_shifts), HEADS], F32, name="short_all")
-        for i, shift in enumerate(short_shifts):
-            write_coefficient(short_all[:, i, :], shift)
+        out_flat = out.rearrange("o h n e -> (o h n e)")
         short_coef = const.tile([P, PAIRS, len(short_shifts)], F32, name="short_coef")
-        for half in range(2):
-            rows = slice(HEAD_DIM * half, HEAD_DIM * (half + 1))
-            by_pair = short_all[rows, :, :].rearrange("p s (c w) -> p c s w", w=2)
-            nc.vector.tensor_copy(out=short_coef[rows, :, :], in_=by_pair[:, :, :, half])
-
-        gain_sum = setup.tile([P, HEADS], F32, name="gain_sum")
-        nc.vector.tensor_reduce(out=gain_sum[:], in_=gains[:].rearrange("p j h -> p h j"), axis=AXIS.X, op=ALU.add)
-        nc.vector.tensor_scalar_mul(out=coef_row[:, :, 0], in0=gain_sum[:], scalar1=D4[3])
-        for shift in long_shifts:
-            write_coefficient(coef_row[:, :, shift // STRIDE], shift)
-        add_skips(coef_row)
-        scratch = out.rearrange("o h n e -> (o h n e)")[0 : HEADS * P * PERIOD]
-        nc.gpsimd.dma_start(out=scratch.rearrange("(h r i) -> r h i", h=HEADS, r=P), in_=coef_row[:])
         toeplitz = const.tile([P, HEADS, CLASS_LEN], F32, name="toeplitz")
-        skewed = scratch.rearrange("(h z) -> h z", h=HEADS)[:, 0 : P * (PERIOD - 1)].rearrange("h (r w) -> r h w", r=P)
-        nc.gpsimd.dma_start(out=toeplitz[:], in_=skewed[:, :, 0:CLASS_LEN])
 
-        k_square, v_t, mag_rep, mag_t, field_q, short_t, result = {}, {}, {}, {}, {}, {}, {}
+        def filter_weights():
+            short_all = setup.tile([P, len(short_shifts), HEADS], F32, name="short_all")
+            for i, shift in enumerate(short_shifts):
+                write_coefficient(short_all[:, i, :], shift)
+            for half in range(2):
+                rows = slice(HEAD_DIM * half, HEAD_DIM * (half + 1))
+                by_pair = short_all[rows, :, :].rearrange("p s (c w) -> p c s w", w=2)
+                nc.vector.tensor_copy(out=short_coef[rows, :, :], in_=by_pair[:, :, :, half])
+            gain_sum = setup.tile([P, HEADS], F32, name="gain_sum")
+            nc.vector.tensor_reduce(out=gain_sum[:], in_=gains[:].rearrange("p j h -> p h j"), axis=AXIS.X, op=ALU.add)
+            nc.vector.tensor_scalar_mul(out=coef_row[:, :, 0], in0=gain_sum[:], scalar1=D4[3])
+            for shift in long_shifts:
+                write_coefficient(coef_row[:, :, shift // STRIDE], shift)
+            add_skips(coef_row)
+            scratch = out_flat[0 : HEADS * P * PERIOD]
+            nc.gpsimd.dma_start(out=scratch.rearrange("(h r i) -> r h i", h=HEADS, r=P), in_=coef_row[:])
+            skewed = scratch.rearrange("(h z) -> h z", h=HEADS)[:, 0 : P * (PERIOD - 1)].rearrange("h (r w) -> r h w", r=P)
+            nc.gpsimd.dma_start(out=toeplitz[:], in_=skewed[:, :, 0:CLASS_LEN])
+
+        k_square, norm_ps, mag_t, field_q, short_t, result = {}, {}, {}, {}, {}, {}
 
         def project(column_block, j, func, dest):
             cols = slice(BANK * j, BANK * (j + 1))
@@ -219,39 +226,48 @@ def tile_causalwaveletfieldattentionh_pa_kernel(tc, x, Wkv_words, Wkv_scales, bk
                     start=(g == 0),
                     stop=(g == K_PASSES - 1),
                 )
-            nc.scalar.activation(out=dest[:, cols], in_=acc[:], func=func, bias=bias_col[:, column_block : column_block + 1])
-
-        def project_and_norm(pair):
-            k_square[pair] = single.tile([P, TOKENS], F32, name="k_square")
-            v_t[pair] = double.tile([P, TOKENS], F32, name="v_t")
-            for j in range(BANKS):
-                project(pair, j, ACT.Square, k_square[pair])
-            norm_ps = psum_small.tile([P, 2 * TOKENS // P], F32, name="norm_ps", tag="small")
-            for j in range(BANKS):
-                project(PAIRS + pair, j, ACT.Identity, v_t[pair])
-                for t in range(4 * j, 4 * j + 4):
-                    nc.tensor.matmul(
-                        out=norm_ps[:, 2 * t : 2 * t + 2],
-                        lhsT=k_square[pair][:, P * t : P * (t + 1)],
-                        rhs=head_sel[:],
-                        start=True,
-                        stop=True,
-                    )
-            mag_rep[pair] = single.tile([P, TOKENS], F32, name="mag_rep")
             nc.scalar.activation(
-                out=mag_rep[pair][:].rearrange("p (g e) -> p g e", e=HEAD_DIM),
-                in_=norm_ps[:].unsqueeze(2).to_broadcast([P, 2 * TOKENS // P, HEAD_DIM]),
-                func=ACT.Sqrt,
+                out=dest,
+                in_=acc[:].rearrange("p (a q) -> p a q", a=ROWS_PER_BANK),
+                func=func,
+                bias=bias_col[:, column_block : column_block + 1],
             )
 
-        def turn_mag(pair, j):
+        def project_k_v(pair, j):
             if j == 0:
-                mag_t[pair] = double.tile([P, TOKENS], F32, name="mag_t")
-            turned = psum_tr.tile([P, BANK], F32, name="turned")
-            for i in range(4):
-                t = 4 * j + i
-                nc.tensor.transpose(turned[:, P * i : P * (i + 1)], mag_rep[pair][:, P * t : P * (t + 1)], ident[:])
-            nc.scalar.copy(out=mag_t[pair][:, BANK * j : BANK * (j + 1)], in_=turned[:])
+                k_square[pair] = single.tile([P, STRIDE, CLASS_LEN], F32, name="k_square")
+            rows = slice(ROWS_PER_BANK * j, ROWS_PER_BANK * (j + 1))
+            project(pair, j, ACT.Square, k_square[pair][:, rows, :])
+            project(PAIRS + pair, j, ACT.Identity, field_tiles[pair % 3][:, rows, PAD:])
+
+        def key_norms(pair, j):
+            if j == 0:
+                norm_ps[pair] = psum_small.tile([P, 2 * TOKENS // P], F32, name="norm_ps", tag="small")
+            squares = k_square[pair][:].rearrange("p a q -> p (a q)")
+            for t in range(4 * j, 4 * j + 4):
+                nc.tensor.matmul(
+                    out=norm_ps[pair][:, 2 * t : 2 * t + 2],
+                    lhsT=squares[:, P * t : P * (t + 1)],
+                    rhs=head_sel[:],
+                    start=True,
+                    stop=True,
+                )
+            if j == BANKS - 1:
+                nc.scalar.activation(out=mag_q[:, 0 : 2 * TOKENS // P], in_=norm_ps[pair][:], func=ACT.Sqrt)
+
+        def spread_mag(pair):
+            turned = psum_tr.tile([P, P], F32, name="turned")
+            nc.tensor.transpose(turned[:], mag_q[:], ident[:])
+            mag_rows = single.tile([2 * TOKENS // P, P], F32, name="mag_rows")
+            nc.scalar.copy(out=mag_rows[:], in_=turned[0 : 2 * TOKENS // P, :])
+            parked = out_flat[out_flat.shape[0] - 2 * TOKENS * (pair + 1) : out_flat.shape[0] - 2 * TOKENS * pair]
+            nc.sync.dma_start(out=parked.rearrange("(r q) -> r q", q=P), in_=mag_rows[:])
+            mag_t[pair] = double.tile([P, TOKENS], F32, name="mag_t")
+            for half in range(2):
+                nc.sync.dma_start(
+                    out=mag_t[pair][HEAD_DIM * half : HEAD_DIM * (half + 1), :].rearrange("p (t q) -> p t q", q=P),
+                    in_=parked.rearrange("(t h q) -> h t q", h=2, q=P)[half].partition_broadcast(HEAD_DIM),
+                )
 
         def shifted_field(field_t, shift, row0, row1):
             steps, residue = divmod(shift, STRIDE)
@@ -262,10 +278,10 @@ def tile_causalwaveletfieldattentionh_pa_kernel(tc, x, Wkv_words, Wkv_scales, bk
             return field_t[:, source : source + row1 - row0, PAD - back : PAD - back + CLASS_LEN]
 
         def field_and_short_shifts(pair):
-            field_t = field_t_tiles[pair % 2]
+            field_t = field_tiles[pair % 3]
             nc.vector.tensor_tensor(
                 out=field_t[:, :, PAD:],
-                in0=v_t[pair][:].rearrange("p (a q) -> p a q", a=STRIDE),
+                in0=field_t[:, :, PAD:],
                 in1=mag_t[pair][:].rearrange("p (a q) -> p a q", a=STRIDE),
                 op=ALU.mult,
             )
@@ -298,7 +314,7 @@ def tile_causalwaveletfieldattentionh_pa_kernel(tc, x, Wkv_words, Wkv_scales, bk
             for i in range(4):
                 nc.tensor.transpose(
                     turned[:, P * i : P * (i + 1)],
-                    field_t_tiles[pair % 2][:, 4 * group + i, PAD + P * b : PAD + P * (b + 1)],
+                    field_tiles[pair % 3][:, 4 * group + i, PAD + P * b : PAD + P * (b + 1)],
                     ident[:],
                 )
             nc.scalar.copy(
@@ -335,16 +351,23 @@ def tile_causalwaveletfieldattentionh_pa_kernel(tc, x, Wkv_words, Wkv_scales, bk
                 out_view = out[0, 2 * pair : 2 * pair + 2].rearrange("h (b p a) e -> b p h (a e)", b=BLOCKS, p=P, a=STRIDE)
                 nc.sync.dma_start(out=out_view[b], in_=result[pair][:, b].rearrange("p h a e -> p h (a e)"))
 
-        with tc.manual_schedule():
-            for step in range(PAIRS + 2):
+        quantise_bank(0)
+        quantise_bank(1)
+        for step in range(PAIRS + 3):
+            if 2 <= step < PAIRS + 2:
+                field_and_short_shifts(step - 2)
+            for j in range(BANKS):
                 if step < PAIRS:
-                    project_and_norm(step)
-                if 1 <= step <= PAIRS:
-                    field_and_short_shifts(step - 1)
-                for j in range(BANKS):
-                    if step >= 2:
-                        sum_and_store(step - 2, j)
-                    if step < PAIRS:
-                        turn_mag(step, j)
-                    if 1 <= step <= PAIRS:
-                        turn_field(step - 1, j)
+                    project_k_v(step, j)
+                if 3 <= step:
+                    sum_and_store(step - 3, j)
+                if step < PAIRS:
+                    key_norms(step, j)
+                if 1 <= step < PAIRS + 1 and j == 0:
+                    spread_mag(step - 1)
+                if 2 <= step < PAIRS + 2:
+                    turn_field(step - 2, j)
+                if step == 0 and j + 2 < BANKS:
+                    quantise_bank(j + 2)
+            if step == 0:
+                filter_weights()

@@ -63,9 +63,8 @@ def tile_causalwaveletfieldattentionh_pa_kernel(tc, x, Wkv_words, Wkv_scales, bk
         grouped_pool = ctx.enter_context(tc.tile_pool(name="grouped_pool", bufs=2))
         single = ctx.enter_context(tc.tile_pool(name="single", bufs=1))
         double = ctx.enter_context(tc.tile_pool(name="double", bufs=2))
-        psum_mx = ctx.enter_context(tc.psum_pool(name="psum_mx", bufs=3))
+        psum_ring = ctx.enter_context(tc.psum_pool(name="psum_ring", bufs=5))
         psum_tr = ctx.enter_context(tc.psum_pool(name="psum_tr", bufs=2))
-        psum_sum = ctx.enter_context(tc.psum_pool(name="psum_sum", bufs=2))
         psum_small = ctx.enter_context(tc.psum_pool(name="psum_small", bufs=1))
         ctx.enter_context(tc.manual_schedule())
 
@@ -110,6 +109,12 @@ def tile_causalwaveletfieldattentionh_pa_kernel(tc, x, Wkv_words, Wkv_scales, bk
             nc.vector.memset(field_tile[:, :, 0:PAD], 0.0)
             field_tiles.append(field_tile)
 
+        gated = [
+            const.tile([P, STRIDE, CLASS_LEN], F32, name="gated0"),
+            const.tile([P, STRIDE, CLASS_LEN - 2 * hop], F32, name="gated1"),
+        ]
+        nc.vector.memset(gated[0][:, :, 0:hop], 0.0)
+
         mag_q = const.tile([P, P], F32, name="mag_q")
         nc.vector.memset(mag_q[:], 0.0)
 
@@ -149,7 +154,7 @@ def tile_causalwaveletfieldattentionh_pa_kernel(tc, x, Wkv_words, Wkv_scales, bk
                 grouped = grouped_pool.tile([P, 4 * BANK], BF16, name="grouped", align_bytes=64)
                 grouped_words = grouped[:].bitcast(F32)
                 for half in range(2):
-                    xt = psum_mx.tile([P, 2, BANK // 2], F32, name="xt", tag="acc")
+                    xt = psum_ring.tile([P, 2, BANK // 2], F32, name="xt", tag="ring")
                     for i in range(2):
                         a_local, b = divmod(2 * half + i, BLOCKS)
                         words = x_rows[j][:, b, a_local, :].bitcast(F32)
@@ -158,10 +163,7 @@ def tile_causalwaveletfieldattentionh_pa_kernel(tc, x, Wkv_words, Wkv_scales, bk
                                 xt[:, u, P * i : P * (i + 1)], words[:, 256 * g + u : 256 * (g + 1) : 2], ident[:]
                             )
                     dest = grouped_words[:, BANK * half : BANK * (half + 1)].rearrange("p (t u) -> p t u", u=2)
-                    if half == 0:
-                        nc.vector.tensor_copy(out=dest, in_=xt[:].rearrange("p u t -> p t u"))
-                    else:
-                        nc.scalar.copy(out=dest, in_=xt[:].rearrange("p u t -> p t u"))
+                    nc.scalar.copy(out=dest, in_=xt[:].rearrange("p u t -> p t u"))
                 cols = slice(BANK * j, BANK * (j + 1))
                 nc.vector.quantize_mx(out=x_codes[:, g, cols].bitcast(FP8X4), scales=x_scales[:, g, cols], in_=grouped[:])
 
@@ -211,11 +213,11 @@ def tile_causalwaveletfieldattentionh_pa_kernel(tc, x, Wkv_words, Wkv_scales, bk
             skewed = scratch.rearrange("(h z) -> h z", h=HEADS)[:, 0 : P * (PERIOD - 1)].rearrange("h (r w) -> r h w", r=P)
             nc.gpsimd.dma_start(out=toeplitz[:], in_=skewed[:, :, 0:CLASS_LEN])
 
-        k_square, norm_ps, mag_t, field_q, short_t, result = {}, {}, {}, {}, {}, {}
+        k_square, norm_ps, mag_t, field_q, short_t, summed, result = {}, {}, {}, {}, {}, {}, {}
 
         def project(column_block, j, func, dest):
             cols = slice(BANK * j, BANK * (j + 1))
-            acc = psum_mx.tile([P, BANK], F32, name="acc")
+            acc = psum_ring.tile([P, BANK], F32, name="acc", tag="ring")
             for g in range(K_PASSES):
                 nc.tensor.matmul_mx(
                     out=acc[:],
@@ -304,7 +306,15 @@ def tile_causalwaveletfieldattentionh_pa_kernel(tc, x, Wkv_words, Wkv_scales, bk
                             op0=ALU.mult,
                             op1=ALU.add,
                         )
-            add_skips(short_t[pair])
+
+        def gate_short_part(pair):
+            for i, dest in enumerate((gated[0][:, :, hop:], gated[1][:])):
+                nc.scalar.activation(
+                    out=dest,
+                    in_=short_t[pair][:, :, 0 : CLASS_LEN - hop * (i + 1)],
+                    func=ACT.Copy,
+                    scale=skip_gate[:, i : i + 1],
+                )
 
         def turn_field(pair, j):
             if j == 0:
@@ -322,31 +332,39 @@ def tile_causalwaveletfieldattentionh_pa_kernel(tc, x, Wkv_words, Wkv_scales, bk
                 in_=turned[:].rearrange("p (a h e) -> p h a e", a=4, h=2),
             )
 
-        def sum_and_store(pair, j):
-            if j == 0:
-                result[pair] = double.tile([P, BLOCKS, 2, STRIDE, HEAD_DIM], F32, name="result")
+        def long_sums(pair, j):
             b, group = divmod(j, STRIDE // 4)
-            rows = slice(4 * group, 4 * group + 4)
-            summed = psum_sum.tile([P, 4, 2, HEAD_DIM], F32, name="summed")
+            summed[pair, j] = psum_ring.tile([P, 4, 2, HEAD_DIM], F32, name="summed", tag="ring")
             for half in range(2):
                 for source in range(b + 1):
                     nc.tensor.matmul(
-                        out=summed[:, :, half, :],
+                        out=summed[pair, j][:, :, half, :],
                         lhsT=toeplitz[:, 2 * pair + half, P * (b - source) : P * (b - source + 1)],
-                        rhs=field_q[pair][:, source, half, rows, :],
+                        rhs=field_q[pair][:, source, half, 4 * group : 4 * group + 4, :],
                         start=(half == 0 and source == 0),
                         stop=False,
                     )
-            for i in range(4):
-                nc.tensor.matmul(
-                    out=summed[:, i, :, :],
-                    lhsT=short_t[pair][:, 4 * group + i, P * b : P * (b + 1)],
-                    rhs=ident[:].rearrange("p (h e) -> p h e", h=2),
-                    is_transpose=True,
-                    start=False,
-                    stop=(i == 3),
-                )
-            nc.scalar.copy(out=result[pair][:, b, :, rows, :], in_=summed[:].rearrange("p a h e -> p h a e"))
+
+        def add_short_part_and_store(pair, j):
+            if j == 0:
+                result[pair] = double.tile([P, BLOCKS, 2, STRIDE, HEAD_DIM], F32, name="result")
+            b, group = divmod(j, STRIDE // 4)
+            parts = [short_t[pair][:, :, P * b : P * (b + 1)], gated[0][:, :, P * b : P * (b + 1)]]
+            if b > 0:
+                parts.append(gated[1][:, :, P * (b - 1) : P * b])
+            for n, part in enumerate(parts):
+                for i in range(4):
+                    nc.tensor.matmul(
+                        out=summed[pair, j][:, i, :, :],
+                        lhsT=part[:, 4 * group + i, :],
+                        rhs=ident[:].rearrange("p (h e) -> p h e", h=2),
+                        is_transpose=True,
+                        start=False,
+                        stop=(n == len(parts) - 1 and i == 3),
+                    )
+            nc.scalar.copy(
+                out=result[pair][:, b, :, 4 * group : 4 * group + 4, :], in_=summed[pair, j][:].rearrange("p a h e -> p h a e")
+            )
             if group == STRIDE // 4 - 1:
                 out_view = out[0, 2 * pair : 2 * pair + 2].rearrange("h (b p a) e -> b p h (a e)", b=BLOCKS, p=P, a=STRIDE)
                 nc.sync.dma_start(out=out_view[b], in_=result[pair][:, b].rearrange("p h a e -> p h (a e)"))
@@ -356,11 +374,18 @@ def tile_causalwaveletfieldattentionh_pa_kernel(tc, x, Wkv_words, Wkv_scales, bk
         for step in range(PAIRS + 3):
             if 2 <= step < PAIRS + 2:
                 field_and_short_shifts(step - 2)
+            if 3 <= step:
+                gate_short_part(step - 3)
+            if step == PAIRS + 2:
+                for j in range(BANKS):
+                    long_sums(step - 3, j)
             for j in range(BANKS):
                 if step < PAIRS:
                     project_k_v(step, j)
+                if 3 <= step < PAIRS + 2:
+                    long_sums(step - 3, j)
                 if 3 <= step:
-                    sum_and_store(step - 3, j)
+                    add_short_part_and_store(step - 3, j)
                 if step < PAIRS:
                     key_norms(step, j)
                 if 1 <= step < PAIRS + 1 and j == 0:

@@ -38,22 +38,21 @@ PERIOD = CLASS_LEN + P
 FLOPS = 2 * TOKENS * DIM * 2 * DIM
 
 
-def tap_terms():
-    terms = {}
-    for j in range(SCALES):
-        for t in range(3):
-            shift = (3 - t) * 2**j
-            if shift not in terms:
-                terms[shift] = []
-            terms[shift].append((j, D4[t]))
-    return terms
+def tap_places():
+    places = {}
+    for m in range(SCALES + 1):
+        places[2**m] = (0, m)
+    for m in range(SCALES):
+        places[3 * 2**m] = (1, m)
+    return places
 
 
 def tile_causalwaveletfieldattentionh_pa_kernel(tc, x, Wkv_words, Wkv_scales, bkv, scale_gain, skip_w, out):
     nc = tc.nc
-    terms = tap_terms()
-    long_shifts = [s for s in sorted(terms) if s % STRIDE == 0]
-    short_shifts = sorted([s for s in terms if s % STRIDE != 0], key=lambda s: (s % STRIDE, s))
+    places = tap_places()
+    long_shifts = [s for s in sorted(places) if s % STRIDE == 0]
+    short_shifts = sorted([s for s in places if s % STRIDE != 0], key=lambda s: (s % STRIDE, s))
+    short_powers = 1 + max(places[s][1] for s in short_shifts)
     hop = SKIPS[0] // STRIDE
 
     with ExitStack() as ctx:
@@ -87,39 +86,40 @@ def tile_causalwaveletfieldattentionh_pa_kernel(tc, x, Wkv_words, Wkv_scales, bk
         x_view = x.flatten_outer_dims().rearrange("(b p a) k -> p b a k", b=BLOCKS, p=P, a=STRIDE)
         x_rows = []
         w_words = const.tile([P, K_PASSES, 4 * DIM], U8, name="w_words", align_bytes=64)
+
+        def load_weight_blocks(first, last):
+            for g in range(K_PASSES):
+                columns = slice(2 * P * first, 2 * P * last)
+                nc.sync.dma_start(out=w_words[:, g, columns].bitcast(I32), in_=Wkv_words[g, :, columns].bitcast(I32))
+
+        load_weight_blocks(0, 1)
+        load_weight_blocks(PAIRS, PAIRS + 1)
         for j in range(BANKS):
             rows = x_pool.tile([P, BLOCKS, ROWS_PER_BANK, DIM], BF16, name="x_rows")
             nc.sync.dma_start(out=rows[:], in_=x_view[:, :, ROWS_PER_BANK * j : ROWS_PER_BANK * (j + 1), :])
             x_rows.append(rows)
-            if j == 0:
-                for g in range(K_PASSES):
-                    nc.sync.dma_start(out=w_words[:, g, :].bitcast(I32), in_=Wkv_words[g].bitcast(I32))
+        load_weight_blocks(1, PAIRS)
+        load_weight_blocks(PAIRS + 1, 2 * PAIRS)
 
         ident = const.tile([P, P], F32, name="ident")
         make_identity(nc, ident[:])
-        coef_row = setup.tile([P, HEADS, PERIOD], F32, name="coef_row")
-        nc.gpsimd.memset(coef_row[:], 0.0)
         head_sel = const.tile([P, 2], F32, name="head_sel")
-        nc.vector.memset(head_sel[:], 0.0)
-        nc.vector.memset(head_sel[0:HEAD_DIM, 0:1], 1.0)
-        nc.vector.memset(head_sel[HEAD_DIM:P, 1:2], 1.0)
+        nc.gpsimd.memset(head_sel[:], 0.0)
+        nc.gpsimd.memset(head_sel[0:HEAD_DIM, 0:1], 1.0)
+        nc.gpsimd.memset(head_sel[HEAD_DIM:P, 1:2], 1.0)
         field_tiles = []
         for i in range(3):
             field_tile = const.tile([P, STRIDE, PAD + CLASS_LEN], F32, name="field_t%d" % i)
-            nc.vector.memset(field_tile[:, :, 0:PAD], 0.0)
+            nc.gpsimd.memset(field_tile[:, :, 0:PAD], 0.0)
             field_tiles.append(field_tile)
 
-        gated = [
-            const.tile([P, STRIDE, CLASS_LEN], F32, name="gated0"),
-            const.tile([P, STRIDE, CLASS_LEN - 2 * hop], F32, name="gated1"),
-        ]
-        nc.vector.memset(gated[0][:, :, 0:hop], 0.0)
-
         mag_q = const.tile([P, P], F32, name="mag_q")
-        nc.vector.memset(mag_q[:], 0.0)
+        nc.gpsimd.memset(mag_q[:], 0.0)
 
         bias_rows = setup.tile([P, P], F32, name="bias_rows")
-        nc.vector.memset(bias_rows[:], 0.0)
+        nc.gpsimd.memset(bias_rows[:], 0.0)
+        coef_row = setup.tile([P, HEADS, PERIOD], F32, name="coef_row")
+        nc.gpsimd.memset(coef_row[:], 0.0)
         nc.vector.tensor_copy(out=bias_rows[0 : 2 * PAIRS, :], in_=bias_bf[:])
         bias_ps = psum_small.tile([P, P], F32, name="bias_ps", tag="small")
         nc.tensor.transpose(bias_ps[:], bias_rows[:], ident[:])
@@ -163,18 +163,12 @@ def tile_causalwaveletfieldattentionh_pa_kernel(tc, x, Wkv_words, Wkv_scales, bk
                                 xt[:, u, P * i : P * (i + 1)], words[:, 256 * g + u : 256 * (g + 1) : 2], ident[:]
                             )
                     dest = grouped_words[:, BANK * half : BANK * (half + 1)].rearrange("p (t u) -> p t u", u=2)
-                    nc.scalar.copy(out=dest, in_=xt[:].rearrange("p u t -> p t u"))
+                    if half == 0:
+                        nc.vector.tensor_copy(out=dest, in_=xt[:].rearrange("p u t -> p t u"))
+                    else:
+                        nc.scalar.copy(out=dest, in_=xt[:].rearrange("p u t -> p t u"))
                 cols = slice(BANK * j, BANK * (j + 1))
                 nc.vector.quantize_mx(out=x_codes[:, g, cols].bitcast(FP8X4), scales=x_scales[:, g, cols], in_=grouped[:])
-
-        def write_coefficient(dest, shift):
-            for i, (j, weight) in enumerate(terms[shift]):
-                if i == 0:
-                    nc.vector.tensor_scalar_mul(out=dest, in0=gains[:, j, :], scalar1=weight)
-                else:
-                    nc.vector.scalar_tensor_tensor(
-                        out=dest, in0=gains[:, j, :], scalar=weight, in1=dest, op0=ALU.mult, op1=ALU.add
-                    )
 
         def add_skips(rows):
             for block in range(CLASS_LEN // hop - 1, 0, -1):
@@ -191,27 +185,38 @@ def tile_causalwaveletfieldattentionh_pa_kernel(tc, x, Wkv_words, Wkv_scales, bk
                         )
 
         out_flat = out.rearrange("o h n e -> (o h n e)")
-        short_coef = const.tile([P, PAIRS, len(short_shifts)], F32, name="short_coef")
+        short_coef = const.tile([P, PAIRS, 2, short_powers], F32, name="short_coef")
         toeplitz = const.tile([P, HEADS, CLASS_LEN], F32, name="toeplitz")
 
-        def filter_weights():
-            short_all = setup.tile([P, len(short_shifts), HEADS], F32, name="short_all")
-            for i, shift in enumerate(short_shifts):
-                write_coefficient(short_all[:, i, :], shift)
-            for half in range(2):
-                rows = slice(HEAD_DIM * half, HEAD_DIM * (half + 1))
-                by_pair = short_all[rows, :, :].rearrange("p s (c w) -> p c s w", w=2)
-                nc.vector.tensor_copy(out=short_coef[rows, :, :], in_=by_pair[:, :, :, half])
-            gain_sum = setup.tile([P, HEADS], F32, name="gain_sum")
-            nc.vector.tensor_reduce(out=gain_sum[:], in_=gains[:].rearrange("p j h -> p h j"), axis=AXIS.X, op=ALU.add)
-            nc.vector.tensor_scalar_mul(out=coef_row[:, :, 0], in0=gain_sum[:], scalar1=D4[3])
-            for shift in long_shifts:
-                write_coefficient(coef_row[:, :, shift // STRIDE], shift)
-            add_skips(coef_row)
+        weights = setup.tile([P, 2, SCALES + 1, HEADS], F32, name="weights")
+        nc.vector.tensor_scalar_mul(out=weights[:, 0, 0:SCALES, :], in0=gains[:], scalar1=D4[2])
+        nc.vector.tensor_scalar_mul(out=weights[:, 1, 0:SCALES, :], in0=gains[:], scalar1=D4[0])
+        nc.vector.tensor_scalar_mul(out=weights[:, 0, SCALES, :], in0=gains[:, SCALES - 1, :], scalar1=D4[1])
+        nc.vector.scalar_tensor_tensor(
+            out=weights[:, 0, 1:SCALES, :],
+            in0=gains[:, 0 : SCALES - 1, :],
+            scalar=D4[1],
+            in1=weights[:, 0, 1:SCALES, :],
+            op0=ALU.mult,
+            op1=ALU.add,
+        )
+        for half in range(2):
+            rows = slice(HEAD_DIM * half, HEAD_DIM * (half + 1))
+            by_pair = weights[rows, :, 0:short_powers, :].rearrange("p f m (c w) -> p c f m w", w=2)
+            nc.vector.tensor_copy(out=short_coef[rows], in_=by_pair[:, :, :, :, half])
+        gain_sum = setup.tile([P, HEADS], F32, name="gain_sum")
+        nc.vector.tensor_reduce(out=gain_sum[:], in_=gains[:].rearrange("p j h -> p h j"), axis=AXIS.X, op=ALU.add)
+        nc.vector.tensor_scalar_mul(out=weights[:, 1, SCALES, :], in0=gain_sum[:], scalar1=D4[3])
+        nc.gpsimd.tensor_copy(out=coef_row[:, :, 0], in_=weights[:, 1, SCALES, :])
+        for shift in long_shifts:
+            family, m = places[shift]
+            nc.gpsimd.tensor_copy(out=coef_row[:, :, shift // STRIDE], in_=weights[:, family, m, :])
+
+        def build_toeplitz():
             scratch = out_flat[0 : HEADS * P * PERIOD]
-            nc.gpsimd.dma_start(out=scratch.rearrange("(h r i) -> r h i", h=HEADS, r=P), in_=coef_row[:])
+            nc.sync.dma_start(out=scratch.rearrange("(h r i) -> r h i", h=HEADS, r=P), in_=coef_row[:])
             skewed = scratch.rearrange("(h z) -> h z", h=HEADS)[:, 0 : P * (PERIOD - 1)].rearrange("h (r w) -> r h w", r=P)
-            nc.gpsimd.dma_start(out=toeplitz[:], in_=skewed[:, :, 0:CLASS_LEN])
+            nc.sync.dma_start(out=toeplitz[:], in_=skewed[:, :, 0:CLASS_LEN])
 
         k_square, norm_ps, mag_t, field_q, short_t, summed, result = {}, {}, {}, {}, {}, {}, {}
 
@@ -279,7 +284,7 @@ def tile_causalwaveletfieldattentionh_pa_kernel(tc, x, Wkv_words, Wkv_scales, bk
                 source, back = row0 - residue + STRIDE, steps + 1
             return field_t[:, source : source + row1 - row0, PAD - back : PAD - back + CLASS_LEN]
 
-        def field_and_short_shifts(pair):
+        def make_field(pair):
             field_t = field_tiles[pair % 3]
             nc.vector.tensor_tensor(
                 out=field_t[:, :, PAD:],
@@ -287,34 +292,20 @@ def tile_causalwaveletfieldattentionh_pa_kernel(tc, x, Wkv_words, Wkv_scales, bk
                 in1=mag_t[pair][:].rearrange("p (a q) -> p a q", a=STRIDE),
                 op=ALU.mult,
             )
-            short_t[pair] = double.tile([P, STRIDE, CLASS_LEN], F32, name="short_t")
-            for i, shift in enumerate(short_shifts):
-                residue = shift % STRIDE
-                for row0, row1 in ((residue, STRIDE), (0, residue)):
-                    if i == 0:
-                        nc.vector.tensor_scalar_mul(
-                            out=short_t[pair][:, row0:row1, :],
-                            in0=shifted_field(field_t, shift, row0, row1),
-                            scalar1=short_coef[:, pair, i : i + 1],
-                        )
-                    else:
-                        nc.vector.scalar_tensor_tensor(
-                            out=short_t[pair][:, row0:row1, :],
-                            in0=shifted_field(field_t, shift, row0, row1),
-                            scalar=short_coef[:, pair, i : i + 1],
-                            in1=short_t[pair][:, row0:row1, :],
-                            op0=ALU.mult,
-                            op1=ALU.add,
-                        )
 
-        def gate_short_part(pair):
-            for i, dest in enumerate((gated[0][:, :, hop:], gated[1][:])):
-                nc.scalar.activation(
-                    out=dest,
-                    in_=short_t[pair][:, :, 0 : CLASS_LEN - hop * (i + 1)],
-                    func=ACT.Copy,
-                    scale=skip_gate[:, i : i + 1],
-                )
+        def short_shift(pair, i):
+            shift = short_shifts[i]
+            family, m = places[shift]
+            weight = short_coef[:, pair, family, m : m + 1]
+            if i == 0:
+                short_t[pair] = double.tile([P, STRIDE, CLASS_LEN], F32, name="short_t")
+            for row0, row1 in ((shift % STRIDE, STRIDE), (0, shift % STRIDE)):
+                shifted = shifted_field(field_tiles[pair % 3], shift, row0, row1)
+                rows = short_t[pair][:, row0:row1, :]
+                if i == 0:
+                    nc.scalar.activation(out=rows, in_=shifted, func=ACT.Copy, scale=weight)
+                else:
+                    nc.vector.scalar_tensor_tensor(out=rows, in0=shifted, scalar=weight, in1=rows, op0=ALU.mult, op1=ALU.add)
 
         def turn_field(pair, j):
             if j == 0:
@@ -349,19 +340,15 @@ def tile_causalwaveletfieldattentionh_pa_kernel(tc, x, Wkv_words, Wkv_scales, bk
             if j == 0:
                 result[pair] = double.tile([P, BLOCKS, 2, STRIDE, HEAD_DIM], F32, name="result")
             b, group = divmod(j, STRIDE // 4)
-            parts = [short_t[pair][:, :, P * b : P * (b + 1)], gated[0][:, :, P * b : P * (b + 1)]]
-            if b > 0:
-                parts.append(gated[1][:, :, P * (b - 1) : P * b])
-            for n, part in enumerate(parts):
-                for i in range(4):
-                    nc.tensor.matmul(
-                        out=summed[pair, j][:, i, :, :],
-                        lhsT=part[:, 4 * group + i, :],
-                        rhs=ident[:].rearrange("p (h e) -> p h e", h=2),
-                        is_transpose=True,
-                        start=False,
-                        stop=(n == len(parts) - 1 and i == 3),
-                    )
+            for i in range(4):
+                nc.tensor.matmul(
+                    out=summed[pair, j][:, i, :, :],
+                    lhsT=short_t[pair][:, 4 * group + i, P * b : P * (b + 1)],
+                    rhs=ident[:].rearrange("p (h e) -> p h e", h=2),
+                    is_transpose=True,
+                    start=False,
+                    stop=(i == 3),
+                )
             nc.scalar.copy(
                 out=result[pair][:, b, :, 4 * group : 4 * group + 4, :], in_=summed[pair, j][:].rearrange("p a h e -> p h a e")
             )
@@ -373,9 +360,8 @@ def tile_causalwaveletfieldattentionh_pa_kernel(tc, x, Wkv_words, Wkv_scales, bk
         quantise_bank(1)
         for step in range(PAIRS + 3):
             if 2 <= step < PAIRS + 2:
-                field_and_short_shifts(step - 2)
-            if 3 <= step:
-                gate_short_part(step - 3)
+                for i in range(1, len(short_shifts)):
+                    short_shift(step - 2, i)
             if step == PAIRS + 2:
                 for j in range(BANKS):
                     long_sums(step - 3, j)
@@ -390,9 +376,16 @@ def tile_causalwaveletfieldattentionh_pa_kernel(tc, x, Wkv_words, Wkv_scales, bk
                     key_norms(step, j)
                 if 1 <= step < PAIRS + 1 and j == 0:
                     spread_mag(step - 1)
+                    make_field(step - 1)
+                if 2 <= step < PAIRS + 2 and j == 0:
+                    add_skips(short_t[step - 2])
+                if step == 1 and j == 0:
+                    build_toeplitz()
                 if 2 <= step < PAIRS + 2:
                     turn_field(step - 2, j)
                 if step == 0 and j + 2 < BANKS:
                     quantise_bank(j + 2)
+            if 1 <= step < PAIRS + 1:
+                short_shift(step - 1, 0)
             if step == 0:
-                filter_weights()
+                add_skips(coef_row)

@@ -65,7 +65,6 @@ def tile_causalwaveletfieldattentionh_pa_kernel(tc, x, Wkv_words, Wkv_scales, bk
         psum_ring = ctx.enter_context(tc.psum_pool(name="psum_ring", bufs=5))
         psum_tr = ctx.enter_context(tc.psum_pool(name="psum_tr", bufs=2))
         psum_small = ctx.enter_context(tc.psum_pool(name="psum_small", bufs=1))
-        ctx.enter_context(tc.manual_schedule())
 
         gain_bf = setup.tile([P, SCALES * HEADS], BF16, name="gain_bf")
         nc.scalar.dma_start(out=gain_bf[:], in_=scale_gain.rearrange("j h -> (j h)").partition_broadcast(P))

@@ -34,6 +34,7 @@ ROWS_PER_BANK = BANK // CLASS_LEN
 BANKS = TOKENS // BANK
 PAD = 8
 PERIOD = CLASS_LEN + P
+PARTS = 2
 
 FLOPS = 2 * TOKENS * DIM * 2 * DIM
 
@@ -170,10 +171,11 @@ def tile_causalwaveletfieldattentionh_pa_kernel(tc, x, Wkv_words, Wkv_scales, bk
                 nc.vector.quantize_mx(out=x_codes[:, g, cols].bitcast(FP8X4), scales=x_scales[:, g, cols], in_=grouped[:])
 
         def add_skips(rows):
-            for block in range(CLASS_LEN // hop - 1, 0, -1):
+            blocks = CLASS_LEN // hop
+            for source in range(blocks - 2, -1, -1):
                 for i in range(len(SKIPS)):
-                    source = block - SKIPS[i] // SKIPS[0]
-                    if source >= 0:
+                    block = source + SKIPS[i] // SKIPS[0]
+                    if block < blocks:
                         nc.vector.scalar_tensor_tensor(
                             out=rows[:, :, hop * block : hop * (block + 1)],
                             in0=rows[:, :, hop * source : hop * (source + 1)],
@@ -291,17 +293,19 @@ def tile_causalwaveletfieldattentionh_pa_kernel(tc, x, Wkv_words, Wkv_scales, bk
                 in1=mag_t[pair][:].rearrange("p (a q) -> p a q", a=STRIDE),
                 op=ALU.mult,
             )
+            add_skips(field_t[:, :, PAD:])
 
         def short_shift(pair, i):
             shift = short_shifts[i]
             family, m = places[shift]
             weight = short_coef[:, pair, family, m : m + 1]
-            if i == 0:
-                short_t[pair] = double.tile([P, STRIDE, CLASS_LEN], F32, name="short_t")
+            part = i % PARTS
+            if i < PARTS:
+                short_t[pair, part] = double.tile([P, STRIDE, CLASS_LEN], F32, name="short_t%d" % part)
             for row0, row1 in ((shift % STRIDE, STRIDE), (0, shift % STRIDE)):
                 shifted = shifted_field(field_tiles[pair % 3], shift, row0, row1)
-                rows = short_t[pair][:, row0:row1, :]
-                if i == 0:
+                rows = short_t[pair, part][:, row0:row1, :]
+                if i < PARTS:
                     nc.scalar.activation(out=rows, in_=shifted, func=ACT.Copy, scale=weight)
                 else:
                     nc.vector.scalar_tensor_tensor(out=rows, in0=shifted, scalar=weight, in1=rows, op0=ALU.mult, op1=ALU.add)
@@ -339,15 +343,16 @@ def tile_causalwaveletfieldattentionh_pa_kernel(tc, x, Wkv_words, Wkv_scales, bk
             if j == 0:
                 result[pair] = double.tile([P, BLOCKS, 2, STRIDE, HEAD_DIM], F32, name="result")
             b, group = divmod(j, STRIDE // 4)
-            for i in range(4):
-                nc.tensor.matmul(
-                    out=summed[pair, j][:, i, :, :],
-                    lhsT=short_t[pair][:, 4 * group + i, P * b : P * (b + 1)],
-                    rhs=ident[:].rearrange("p (h e) -> p h e", h=2),
-                    is_transpose=True,
-                    start=False,
-                    stop=(i == 3),
-                )
+            for part in range(PARTS):
+                for i in range(4):
+                    nc.tensor.matmul(
+                        out=summed[pair, j][:, i, :, :],
+                        lhsT=short_t[pair, part][:, 4 * group + i, P * b : P * (b + 1)],
+                        rhs=ident[:].rearrange("p (h e) -> p h e", h=2),
+                        is_transpose=True,
+                        start=False,
+                        stop=(part == PARTS - 1 and i == 3),
+                    )
             nc.scalar.copy(
                 out=result[pair][:, b, :, 4 * group : 4 * group + 4, :], in_=summed[pair, j][:].rearrange("p a h e -> p h a e")
             )
@@ -359,7 +364,7 @@ def tile_causalwaveletfieldattentionh_pa_kernel(tc, x, Wkv_words, Wkv_scales, bk
         quantise_bank(1)
         for step in range(PAIRS + 3):
             if 2 <= step < PAIRS + 2:
-                for i in range(1, len(short_shifts)):
+                for i in range(PARTS, len(short_shifts)):
                     short_shift(step - 2, i)
             if step == PAIRS + 2:
                 for j in range(BANKS):
@@ -376,8 +381,6 @@ def tile_causalwaveletfieldattentionh_pa_kernel(tc, x, Wkv_words, Wkv_scales, bk
                 if 1 <= step < PAIRS + 1 and j == 0:
                     spread_mag(step - 1)
                     make_field(step - 1)
-                if 2 <= step < PAIRS + 2 and j == 0:
-                    add_skips(short_t[step - 2])
                 if step == 1 and j == 0:
                     build_toeplitz()
                 if 2 <= step < PAIRS + 2:
@@ -385,6 +388,5 @@ def tile_causalwaveletfieldattentionh_pa_kernel(tc, x, Wkv_words, Wkv_scales, bk
                 if step == 0 and j + 2 < BANKS:
                     quantise_bank(j + 2)
             if 1 <= step < PAIRS + 1:
-                short_shift(step - 1, 0)
-            if step == 0:
-                add_skips(coef_row)
+                for i in range(PARTS):
+                    short_shift(step - 1, i)

@@ -64,8 +64,7 @@ def tile_causalwaveletfieldattentionh_pa_kernel(tc, x, Wkv_words, Wkv_scales, bk
         single = ctx.enter_context(tc.tile_pool(name="single", bufs=1))
         double = ctx.enter_context(tc.tile_pool(name="double", bufs=2))
         psum_ring = ctx.enter_context(tc.psum_pool(name="psum_ring", bufs=5))
-        psum_tr = ctx.enter_context(tc.psum_pool(name="psum_tr", bufs=2))
-        psum_small = ctx.enter_context(tc.psum_pool(name="psum_small", bufs=1))
+        psum_tr = ctx.enter_context(tc.psum_pool(name="psum_tr", bufs=3))
 
         gain_bf = setup.tile([P, SCALES * HEADS], BF16, name="gain_bf")
         nc.scalar.dma_start(out=gain_bf[:], in_=scale_gain.rearrange("j h -> (j h)").partition_broadcast(P))
@@ -103,10 +102,6 @@ def tile_causalwaveletfieldattentionh_pa_kernel(tc, x, Wkv_words, Wkv_scales, bk
 
         ident = const.tile([P, P], F32, name="ident")
         make_identity(nc, ident[:])
-        head_sel = const.tile([P, 2], F32, name="head_sel")
-        nc.gpsimd.memset(head_sel[:], 0.0)
-        nc.gpsimd.memset(head_sel[0:HEAD_DIM, 0:1], 1.0)
-        nc.gpsimd.memset(head_sel[HEAD_DIM:P, 1:2], 1.0)
         field_tiles = []
         for i in range(3):
             field_tile = const.tile([P, STRIDE, PAD + CLASS_LEN], F32, name="field_t%d" % i)
@@ -121,7 +116,7 @@ def tile_causalwaveletfieldattentionh_pa_kernel(tc, x, Wkv_words, Wkv_scales, bk
         coef_row = setup.tile([P, HEADS, PERIOD], F32, name="coef_row")
         nc.gpsimd.memset(coef_row[:], 0.0)
         nc.vector.tensor_copy(out=bias_rows[0 : 2 * PAIRS, :], in_=bias_bf[:])
-        bias_ps = psum_small.tile([P, P], F32, name="bias_ps", tag="small")
+        bias_ps = psum_tr.tile([P, P], F32, name="bias_ps", tag="turned")
         nc.tensor.transpose(bias_ps[:], bias_rows[:], ident[:])
         bias_col = const.tile([P, 2 * PAIRS], F32, name="bias_col")
         nc.vector.tensor_copy(out=bias_col[:], in_=bias_ps[:, 0 : 2 * PAIRS])
@@ -250,16 +245,17 @@ def tile_causalwaveletfieldattentionh_pa_kernel(tc, x, Wkv_words, Wkv_scales, bk
 
         def key_norms(pair, j):
             if j == 0:
-                norm_ps[pair] = psum_small.tile([P, 2 * TOKENS // P], F32, name="norm_ps", tag="small")
+                norm_ps[pair] = double.tile([P, 2 * TOKENS // P], F32, name="norm_sq")
             squares = k_square[pair][:].rearrange("p a q -> p (a q)")
-            for t in range(4 * j, 4 * j + 4):
-                nc.tensor.matmul(
-                    out=norm_ps[pair][:, 2 * t : 2 * t + 2],
-                    lhsT=squares[:, P * t : P * (t + 1)],
-                    rhs=head_sel[:],
-                    start=True,
-                    stop=True,
-                )
+            turned = psum_tr.tile([P, BANK], F32, name="turned")
+            for i in range(4):
+                nc.tensor.transpose(turned[:, P * i : P * (i + 1)], squares[:, P * (4 * j + i) : P * (4 * j + i + 1)], ident[:])
+            nc.vector.tensor_reduce(
+                out=norm_ps[pair][:, 2 * 4 * j : 2 * 4 * (j + 1)],
+                in_=turned[:].rearrange("p (i e) -> p i e", e=HEAD_DIM),
+                axis=AXIS.X,
+                op=ALU.add,
+            )
             if j == BANKS - 1:
                 nc.scalar.activation(out=mag_q[:, 0 : 2 * TOKENS // P], in_=norm_ps[pair][:], func=ACT.Sqrt)
 

@@ -63,8 +63,8 @@ def tile_causalwaveletfieldattentionh_pa_kernel(tc, x, Wkv_words, Wkv_scales, bk
         grouped_pool = ctx.enter_context(tc.tile_pool(name="grouped_pool", bufs=2))
         single = ctx.enter_context(tc.tile_pool(name="single", bufs=1))
         double = ctx.enter_context(tc.tile_pool(name="double", bufs=2))
-        psum_ring = ctx.enter_context(tc.psum_pool(name="psum_ring", bufs=5))
-        psum_tr = ctx.enter_context(tc.psum_pool(name="psum_tr", bufs=3))
+        psum = ctx.enter_context(tc.psum_pool(name="psum", bufs=8))
+        ctx.enter_context(tc.manual_schedule(engines={mybir.EngineType.PE}))
 
         gain_bf = setup.tile([P, SCALES * HEADS], BF16, name="gain_bf")
         nc.scalar.dma_start(out=gain_bf[:], in_=scale_gain.rearrange("j h -> (j h)").partition_broadcast(P))
@@ -116,7 +116,7 @@ def tile_causalwaveletfieldattentionh_pa_kernel(tc, x, Wkv_words, Wkv_scales, bk
         coef_row = setup.tile([P, HEADS, PERIOD], F32, name="coef_row")
         nc.gpsimd.memset(coef_row[:], 0.0)
         nc.vector.tensor_copy(out=bias_rows[0 : 2 * PAIRS, :], in_=bias_bf[:])
-        bias_ps = psum_tr.tile([P, P], F32, name="bias_ps", tag="turned")
+        bias_ps = psum.tile([P, P], F32, name="bias_ps", tag="bank")
         nc.tensor.transpose(bias_ps[:], bias_rows[:], ident[:])
         bias_col = const.tile([P, 2 * PAIRS], F32, name="bias_col")
         nc.vector.tensor_copy(out=bias_col[:], in_=bias_ps[:, 0 : 2 * PAIRS])
@@ -149,7 +149,7 @@ def tile_causalwaveletfieldattentionh_pa_kernel(tc, x, Wkv_words, Wkv_scales, bk
                 grouped = grouped_pool.tile([P, 4 * BANK], BF16, name="grouped", align_bytes=64)
                 grouped_words = grouped[:].bitcast(F32)
                 for half in range(2):
-                    xt = psum_ring.tile([P, 2, BANK // 2], F32, name="xt", tag="ring")
+                    xt = psum.tile([P, 2, BANK // 2], F32, name="xt", tag="bank")
                     for i in range(2):
                         a_local, b = divmod(2 * half + i, BLOCKS)
                         words = x_rows[j][:, b, a_local, :].bitcast(F32)
@@ -218,7 +218,7 @@ def tile_causalwaveletfieldattentionh_pa_kernel(tc, x, Wkv_words, Wkv_scales, bk
 
         def project(column_block, j, func, dest):
             cols = slice(BANK * j, BANK * (j + 1))
-            acc = psum_ring.tile([P, BANK], F32, name="acc", tag="ring")
+            acc = psum.tile([P, BANK], F32, name="acc", tag="bank")
             for g in range(K_PASSES):
                 nc.tensor.matmul_mx(
                     out=acc[:],
@@ -236,18 +236,19 @@ def tile_causalwaveletfieldattentionh_pa_kernel(tc, x, Wkv_words, Wkv_scales, bk
                 bias=bias_col[:, column_block : column_block + 1],
             )
 
-        def project_k_v(pair, j):
+        def project_k(pair, j):
             if j == 0:
                 k_square[pair] = single.tile([P, STRIDE, CLASS_LEN], F32, name="k_square")
-            rows = slice(ROWS_PER_BANK * j, ROWS_PER_BANK * (j + 1))
-            project(pair, j, ACT.Square, k_square[pair][:, rows, :])
-            project(PAIRS + pair, j, ACT.Identity, field_tiles[pair % 3][:, rows, PAD:])
+            project(pair, j, ACT.Square, k_square[pair][:, ROWS_PER_BANK * j : ROWS_PER_BANK * (j + 1), :])
+
+        def project_v(pair, j):
+            project(PAIRS + pair, j, ACT.Identity, field_tiles[pair % 3][:, ROWS_PER_BANK * j : ROWS_PER_BANK * (j + 1), PAD:])
 
         def key_norms(pair, j):
             if j == 0:
                 norm_ps[pair] = double.tile([P, 2 * TOKENS // P], F32, name="norm_sq")
             squares = k_square[pair][:].rearrange("p a q -> p (a q)")
-            turned = psum_tr.tile([P, BANK], F32, name="turned")
+            turned = psum.tile([P, BANK], F32, name="turned", tag="bank")
             for i in range(4):
                 nc.tensor.transpose(turned[:, P * i : P * (i + 1)], squares[:, P * (4 * j + i) : P * (4 * j + i + 1)], ident[:])
             nc.vector.tensor_reduce(
@@ -260,7 +261,7 @@ def tile_causalwaveletfieldattentionh_pa_kernel(tc, x, Wkv_words, Wkv_scales, bk
                 nc.scalar.activation(out=mag_q[:, 0 : 2 * TOKENS // P], in_=norm_ps[pair][:], func=ACT.Sqrt)
 
         def spread_mag(pair):
-            turned = psum_tr.tile([P, P], F32, name="turned")
+            turned = psum.tile([P, P], F32, name="turned", tag="bank")
             nc.tensor.transpose(turned[:], mag_q[:], ident[:])
             mag_rows = single.tile([2 * TOKENS // P, P], F32, name="mag_rows")
             nc.scalar.copy(out=mag_rows[:], in_=turned[0 : 2 * TOKENS // P, :])
@@ -310,7 +311,7 @@ def tile_causalwaveletfieldattentionh_pa_kernel(tc, x, Wkv_words, Wkv_scales, bk
             if j == 0:
                 field_q[pair] = double.tile([P, BLOCKS, 2, STRIDE, HEAD_DIM], F32, name="field_q")
             b, group = divmod(j, STRIDE // 4)
-            turned = psum_tr.tile([P, BANK], F32, name="turned")
+            turned = psum.tile([P, BANK], F32, name="turned", tag="bank")
             for i in range(4):
                 nc.tensor.transpose(
                     turned[:, P * i : P * (i + 1)],
@@ -324,7 +325,7 @@ def tile_causalwaveletfieldattentionh_pa_kernel(tc, x, Wkv_words, Wkv_scales, bk
 
         def long_sums(pair, j):
             b, group = divmod(j, STRIDE // 4)
-            summed[pair, j] = psum_ring.tile([P, 4, 2, HEAD_DIM], F32, name="summed", tag="ring")
+            summed[pair, j] = psum.tile([P, 4, 2, HEAD_DIM], F32, name="summed", tag="bank")
             for half in range(2):
                 for source in range(b + 1):
                     nc.tensor.matmul(
@@ -356,33 +357,49 @@ def tile_causalwaveletfieldattentionh_pa_kernel(tc, x, Wkv_words, Wkv_scales, bk
                 out_view = out[0, 2 * pair : 2 * pair + 2].rearrange("h (b p a) e -> b p h (a e)", b=BLOCKS, p=P, a=STRIDE)
                 nc.sync.dma_start(out=out_view[b], in_=result[pair][:, b].rearrange("p h a e -> p h (a e)"))
 
+        def live(pair):
+            return 0 <= pair < PAIRS
+
         quantise_bank(0)
         quantise_bank(1)
-        for step in range(PAIRS + 3):
-            if 2 <= step < PAIRS + 2:
-                for i in range(PARTS, len(short_shifts)):
-                    short_shift(step - 2, i)
-            if step == PAIRS + 2:
+        for j in range(BANKS):
+            project_k(0, j)
+            if j + 2 < BANKS:
+                quantise_bank(j + 2)
+            if j >= 1:
+                key_norms(0, j - 1)
+        key_norms(0, BANKS - 1)
+        for j in range(BANKS):
+            project_v(0, j)
+        spread_mag(0)
+        for i in range(-2, PAIRS + 1):
+            if live(i):
+                for t in range(PARTS):
+                    short_shift(i, t)
+            if live(i + 1):
+                make_field(i + 1)
+            if live(i):
+                for t in range(PARTS, len(short_shifts)):
+                    short_shift(i, t)
+            if live(i + 2) and i + 2 > 0:
                 for j in range(BANKS):
-                    long_sums(step - 3, j)
+                    project_v(i + 2, j)
+            if live(i + 3):
+                for j in range(BANKS):
+                    project_k(i + 3, j)
+            if live(i + 2) and i + 2 > 0:
+                spread_mag(i + 2)
+            if i == -1:
+                build_toeplitz()
             for j in range(BANKS):
-                if step < PAIRS:
-                    project_k_v(step, j)
-                if 3 <= step < PAIRS + 2:
-                    long_sums(step - 3, j)
-                if 3 <= step:
-                    add_short_part_and_store(step - 3, j)
-                if step < PAIRS:
-                    key_norms(step, j)
-                if 1 <= step < PAIRS + 1 and j == 0:
-                    spread_mag(step - 1)
-                    make_field(step - 1)
-                if step == 1 and j == 0:
-                    build_toeplitz()
-                if 2 <= step < PAIRS + 2:
-                    turn_field(step - 2, j)
-                if step == 0 and j + 2 < BANKS:
-                    quantise_bank(j + 2)
-            if 1 <= step < PAIRS + 1:
-                for i in range(PARTS):
-                    short_shift(step - 1, i)
+                if live(i - 1):
+                    if i - 1 < PAIRS - 1:
+                        long_sums(i - 1, j)
+                    add_short_part_and_store(i - 1, j)
+                if live(i + 3):
+                    key_norms(i + 3, j)
+                if live(i):
+                    turn_field(i, j)
+            if i == PAIRS - 1:
+                for j in range(BANKS):
+                    long_sums(i, j)

@@ -34,7 +34,14 @@ ROWS_PER_BANK = BANK // CLASS_LEN
 BANKS = TOKENS // BANK
 PAD = 8
 PERIOD = CLASS_LEN + P
-PARTS = 2
+K_AHEAD = 3
+
+
+def parts(pair):
+    return 2 if pair + K_AHEAD >= PAIRS else 1
+
+
+MM_BANKS = 1
 
 FLOPS = 2 * TOKENS * DIM * 2 * DIM
 
@@ -63,6 +70,7 @@ def tile_causalwaveletfieldattentionh_pa_kernel(tc, x, Wkv_words, Wkv_scales, bk
         grouped_pool = ctx.enter_context(tc.tile_pool(name="grouped_pool", bufs=2))
         single = ctx.enter_context(tc.tile_pool(name="single", bufs=1))
         double = ctx.enter_context(tc.tile_pool(name="double", bufs=2))
+        shorts = ctx.enter_context(tc.tile_pool(name="shorts", bufs=4))
         psum = ctx.enter_context(tc.psum_pool(name="psum", bufs=8))
         ctx.enter_context(tc.manual_schedule(engines={mybir.EngineType.PE}))
 
@@ -108,6 +116,11 @@ def tile_causalwaveletfieldattentionh_pa_kernel(tc, x, Wkv_words, Wkv_scales, bk
             nc.gpsimd.memset(field_tile[:, :, 0:PAD], 0.0)
             field_tiles.append(field_tile)
 
+        head_sel = const.tile([P, 2], F32, name="head_sel")
+        nc.gpsimd.memset(head_sel[:], 0.0)
+        nc.gpsimd.memset(head_sel[0:HEAD_DIM, 0:1], 1.0)
+        nc.gpsimd.memset(head_sel[HEAD_DIM:P, 1:2], 1.0)
+        squares = const.tile([P, HEAD_DIM], F32, name="squares")
         mag_q = const.tile([P, P], F32, name="mag_q")
         nc.gpsimd.memset(mag_q[:], 0.0)
 
@@ -216,7 +229,7 @@ def tile_causalwaveletfieldattentionh_pa_kernel(tc, x, Wkv_words, Wkv_scales, bk
 
         k_square, norm_ps, mag_t, field_q, short_t, summed, result = {}, {}, {}, {}, {}, {}, {}
 
-        def project(column_block, j, func, dest):
+        def passes(column_block, j):
             cols = slice(BANK * j, BANK * (j + 1))
             acc = psum.tile([P, BANK], F32, name="acc", tag="bank")
             for g in range(K_PASSES):
@@ -229,34 +242,57 @@ def tile_causalwaveletfieldattentionh_pa_kernel(tc, x, Wkv_words, Wkv_scales, bk
                     start=(g == 0),
                     stop=(g == K_PASSES - 1),
                 )
+            return acc
+
+        def read_k(pair, j, acc):
+            if j == 0:
+                k_square[pair] = single.tile([P, STRIDE, CLASS_LEN], F32, name="k_square")
             nc.scalar.activation(
-                out=dest,
+                out=k_square[pair][:, ROWS_PER_BANK * j : ROWS_PER_BANK * (j + 1), :],
                 in_=acc[:].rearrange("p (a q) -> p a q", a=ROWS_PER_BANK),
-                func=func,
-                bias=bias_col[:, column_block : column_block + 1],
+                func=ACT.Square if j < MM_BANKS else ACT.Identity,
+                bias=bias_col[:, pair : pair + 1],
+            )
+
+        def read_v(pair, j, acc):
+            nc.scalar.activation(
+                out=field_tiles[pair % 3][:, ROWS_PER_BANK * j : ROWS_PER_BANK * (j + 1), PAD:],
+                in_=acc[:].rearrange("p (a q) -> p a q", a=ROWS_PER_BANK),
+                func=ACT.Identity,
+                bias=bias_col[:, PAIRS + pair : PAIRS + pair + 1],
             )
 
         def project_k(pair, j):
-            if j == 0:
-                k_square[pair] = single.tile([P, STRIDE, CLASS_LEN], F32, name="k_square")
-            project(pair, j, ACT.Square, k_square[pair][:, ROWS_PER_BANK * j : ROWS_PER_BANK * (j + 1), :])
+            read_k(pair, j, passes(pair, j))
 
         def project_v(pair, j):
-            project(PAIRS + pair, j, ACT.Identity, field_tiles[pair % 3][:, ROWS_PER_BANK * j : ROWS_PER_BANK * (j + 1), PAD:])
+            read_v(pair, j, passes(PAIRS + pair, j))
 
         def key_norms(pair, j):
             if j == 0:
                 norm_ps[pair] = double.tile([P, 2 * TOKENS // P], F32, name="norm_sq")
-            squares = k_square[pair][:].rearrange("p a q -> p (a q)")
+            keys = k_square[pair][:].rearrange("p a q -> p (a q)")
             turned = psum.tile([P, BANK], F32, name="turned", tag="bank")
-            for i in range(4):
-                nc.tensor.transpose(turned[:, P * i : P * (i + 1)], squares[:, P * (4 * j + i) : P * (4 * j + i + 1)], ident[:])
-            nc.vector.tensor_reduce(
-                out=norm_ps[pair][:, 2 * 4 * j : 2 * 4 * (j + 1)],
-                in_=turned[:].rearrange("p (i e) -> p i e", e=HEAD_DIM),
-                axis=AXIS.X,
-                op=ALU.add,
-            )
+            if j < MM_BANKS:
+                for i in range(4):
+                    nc.tensor.matmul(
+                        out=turned[:, 2 * i : 2 * i + 2],
+                        lhsT=keys[:, P * (4 * j + i) : P * (4 * j + i + 1)],
+                        rhs=head_sel[:],
+                        start=True,
+                        stop=True,
+                    )
+                nc.scalar.copy(out=norm_ps[pair][:, 2 * 4 * j : 2 * 4 * (j + 1)], in_=turned[:, 0 : 2 * 4])
+            else:
+                for i in range(4):
+                    nc.tensor.transpose(turned[:, P * i : P * (i + 1)], keys[:, P * (4 * j + i) : P * (4 * j + i + 1)], ident[:])
+                for i in range(2 * 4):
+                    nc.scalar.activation(
+                        out=squares[:],
+                        in_=turned[:, HEAD_DIM * i : HEAD_DIM * (i + 1)],
+                        func=ACT.Square,
+                        accum_out=norm_ps[pair][:, 2 * 4 * j + i : 2 * 4 * j + i + 1],
+                    )
             if j == BANKS - 1:
                 nc.scalar.activation(out=mag_q[:, 0 : 2 * TOKENS // P], in_=norm_ps[pair][:], func=ACT.Sqrt)
 
@@ -296,13 +332,13 @@ def tile_causalwaveletfieldattentionh_pa_kernel(tc, x, Wkv_words, Wkv_scales, bk
             shift = short_shifts[i]
             family, m = places[shift]
             weight = short_coef[:, pair, family, m : m + 1]
-            part = i % PARTS
-            if i < PARTS:
-                short_t[pair, part] = double.tile([P, STRIDE, CLASS_LEN], F32, name="short_t%d" % part)
+            part = i % parts(pair)
+            if i < parts(pair):
+                short_t[pair, part] = shorts.tile([P, STRIDE, CLASS_LEN], F32, name="short_t")
             for row0, row1 in ((shift % STRIDE, STRIDE), (0, shift % STRIDE)):
                 shifted = shifted_field(field_tiles[pair % 3], shift, row0, row1)
                 rows = short_t[pair, part][:, row0:row1, :]
-                if i < PARTS:
+                if i < parts(pair):
                     nc.scalar.activation(out=rows, in_=shifted, func=ACT.Copy, scale=weight)
                 else:
                     nc.vector.scalar_tensor_tensor(out=rows, in0=shifted, scalar=weight, in1=rows, op0=ALU.mult, op1=ALU.add)
@@ -340,7 +376,7 @@ def tile_causalwaveletfieldattentionh_pa_kernel(tc, x, Wkv_words, Wkv_scales, bk
             if j == 0:
                 result[pair] = double.tile([P, BLOCKS, 2, STRIDE, HEAD_DIM], F32, name="result")
             b, group = divmod(j, STRIDE // 4)
-            for part in range(PARTS):
+            for part in range(parts(pair)):
                 for i in range(4):
                     nc.tensor.matmul(
                         out=summed[pair, j][:, i, :, :],
@@ -348,7 +384,7 @@ def tile_causalwaveletfieldattentionh_pa_kernel(tc, x, Wkv_words, Wkv_scales, bk
                         rhs=ident[:].rearrange("p (h e) -> p h e", h=2),
                         is_transpose=True,
                         start=False,
-                        stop=(part == PARTS - 1 and i == 3),
+                        stop=(part == parts(pair) - 1 and i == 3),
                     )
             nc.scalar.copy(
                 out=result[pair][:, b, :, 4 * group : 4 * group + 4, :], in_=summed[pair, j][:].rearrange("p a h e -> p h a e")
@@ -369,37 +405,40 @@ def tile_causalwaveletfieldattentionh_pa_kernel(tc, x, Wkv_words, Wkv_scales, bk
             if j >= 1:
                 key_norms(0, j - 1)
         key_norms(0, BANKS - 1)
+        waiting = []
         for j in range(BANKS):
-            project_v(0, j)
+            waiting.append(passes(PAIRS, j))
         spread_mag(0)
+        for j in range(BANKS):
+            read_v(0, j, waiting[j])
         for i in range(-2, PAIRS + 1):
             if live(i):
-                for t in range(PARTS):
+                for t in range(parts(i)):
                     short_shift(i, t)
             if live(i + 1):
                 make_field(i + 1)
             if live(i):
-                for t in range(PARTS, len(short_shifts)):
+                for t in range(parts(i), len(short_shifts)):
                     short_shift(i, t)
             if live(i + 2) and i + 2 > 0:
                 for j in range(BANKS):
                     project_v(i + 2, j)
-            if live(i + 3):
+            if live(i + K_AHEAD):
                 for j in range(BANKS):
-                    project_k(i + 3, j)
+                    project_k(i + K_AHEAD, j)
             if live(i + 2) and i + 2 > 0:
                 spread_mag(i + 2)
             if i == -1:
                 build_toeplitz()
             for j in range(BANKS):
                 if live(i - 1):
-                    if i - 1 < PAIRS - 1:
+                    if i - 1 < PAIRS - K_AHEAD:
                         long_sums(i - 1, j)
                     add_short_part_and_store(i - 1, j)
-                if live(i + 3):
-                    key_norms(i + 3, j)
+                if live(i + K_AHEAD):
+                    key_norms(i + K_AHEAD, j)
                 if live(i):
                     turn_field(i, j)
-            if i == PAIRS - 1:
+            if live(i) and i >= PAIRS - K_AHEAD:
                 for j in range(BANKS):
                     long_sums(i, j)

@@ -37,12 +37,6 @@ PERIOD = CLASS_LEN + P
 K_AHEAD = 3
 
 
-def parts(pair):
-    return 2 if pair + K_AHEAD >= PAIRS else 1
-
-
-MM_BANKS = 1
-
 FLOPS = 2 * TOKENS * DIM * 2 * DIM
 
 
@@ -70,9 +64,8 @@ def tile_causalwaveletfieldattentionh_pa_kernel(tc, x, Wkv_words, Wkv_scales, bk
         grouped_pool = ctx.enter_context(tc.tile_pool(name="grouped_pool", bufs=2))
         single = ctx.enter_context(tc.tile_pool(name="single", bufs=1))
         double = ctx.enter_context(tc.tile_pool(name="double", bufs=2))
-        shorts = ctx.enter_context(tc.tile_pool(name="shorts", bufs=4))
         psum = ctx.enter_context(tc.psum_pool(name="psum", bufs=8))
-        ctx.enter_context(tc.manual_schedule(engines={mybir.EngineType.PE}))
+        ctx.enter_context(tc.manual_schedule(engines={mybir.EngineType.PE, mybir.EngineType.SP}))
 
         gain_bf = setup.tile([P, SCALES * HEADS], BF16, name="gain_bf")
         nc.scalar.dma_start(out=gain_bf[:], in_=scale_gain.rearrange("j h -> (j h)").partition_broadcast(P))
@@ -120,7 +113,6 @@ def tile_causalwaveletfieldattentionh_pa_kernel(tc, x, Wkv_words, Wkv_scales, bk
         nc.gpsimd.memset(head_sel[:], 0.0)
         nc.gpsimd.memset(head_sel[0:HEAD_DIM, 0:1], 1.0)
         nc.gpsimd.memset(head_sel[HEAD_DIM:P, 1:2], 1.0)
-        squares = const.tile([P, HEAD_DIM], F32, name="squares")
         mag_q = const.tile([P, P], F32, name="mag_q")
         nc.gpsimd.memset(mag_q[:], 0.0)
 
@@ -250,7 +242,7 @@ def tile_causalwaveletfieldattentionh_pa_kernel(tc, x, Wkv_words, Wkv_scales, bk
             nc.scalar.activation(
                 out=k_square[pair][:, ROWS_PER_BANK * j : ROWS_PER_BANK * (j + 1), :],
                 in_=acc[:].rearrange("p (a q) -> p a q", a=ROWS_PER_BANK),
-                func=ACT.Square if j < MM_BANKS else ACT.Identity,
+                func=ACT.Square,
                 bias=bias_col[:, pair : pair + 1],
             )
 
@@ -268,32 +260,18 @@ def tile_causalwaveletfieldattentionh_pa_kernel(tc, x, Wkv_words, Wkv_scales, bk
         def project_v(pair, j):
             read_v(pair, j, passes(PAIRS + pair, j))
 
-        def key_norms(pair, j):
-            if j == 0:
-                norm_ps[pair] = double.tile([P, 2 * TOKENS // P], F32, name="norm_sq")
-            keys = k_square[pair][:].rearrange("p a q -> p (a q)")
-            turned = psum.tile([P, BANK], F32, name="turned", tag="bank")
-            if j < MM_BANKS:
-                for i in range(4):
-                    nc.tensor.matmul(
-                        out=turned[:, 2 * i : 2 * i + 2],
-                        lhsT=keys[:, P * (4 * j + i) : P * (4 * j + i + 1)],
-                        rhs=head_sel[:],
-                        start=True,
-                        stop=True,
-                    )
-                nc.scalar.copy(out=norm_ps[pair][:, 2 * 4 * j : 2 * 4 * (j + 1)], in_=turned[:, 0 : 2 * 4])
-            else:
-                for i in range(4):
-                    nc.tensor.transpose(turned[:, P * i : P * (i + 1)], keys[:, P * (4 * j + i) : P * (4 * j + i + 1)], ident[:])
-                for i in range(2 * 4):
-                    nc.scalar.activation(
-                        out=squares[:],
-                        in_=turned[:, HEAD_DIM * i : HEAD_DIM * (i + 1)],
-                        func=ACT.Square,
-                        accum_out=norm_ps[pair][:, 2 * 4 * j + i : 2 * 4 * j + i + 1],
-                    )
-            if j == BANKS - 1:
+        def key_norm(pair, t):
+            if t == 0:
+                norm_ps[pair] = psum.tile([P, 2 * TOKENS // P], F32, name="norm_ps", tag="bank")
+            squares = k_square[pair][:].rearrange("p a q -> p (a q)")
+            nc.tensor.matmul(
+                out=norm_ps[pair][:, 2 * t : 2 * t + 2],
+                lhsT=squares[:, P * t : P * (t + 1)],
+                rhs=head_sel[:],
+                start=True,
+                stop=True,
+            )
+            if t == TOKENS // P - 1:
                 nc.scalar.activation(out=mag_q[:, 0 : 2 * TOKENS // P], in_=norm_ps[pair][:], func=ACT.Sqrt)
 
         def spread_mag(pair):
@@ -332,13 +310,12 @@ def tile_causalwaveletfieldattentionh_pa_kernel(tc, x, Wkv_words, Wkv_scales, bk
             shift = short_shifts[i]
             family, m = places[shift]
             weight = short_coef[:, pair, family, m : m + 1]
-            part = i % parts(pair)
-            if i < parts(pair):
-                short_t[pair, part] = shorts.tile([P, STRIDE, CLASS_LEN], F32, name="short_t")
+            if i == 0:
+                short_t[pair] = double.tile([P, STRIDE, CLASS_LEN], F32, name="short_t")
             for row0, row1 in ((shift % STRIDE, STRIDE), (0, shift % STRIDE)):
                 shifted = shifted_field(field_tiles[pair % 3], shift, row0, row1)
-                rows = short_t[pair, part][:, row0:row1, :]
-                if i < parts(pair):
+                rows = short_t[pair][:, row0:row1, :]
+                if i == 0:
                     nc.scalar.activation(out=rows, in_=shifted, func=ACT.Copy, scale=weight)
                 else:
                     nc.vector.scalar_tensor_tensor(out=rows, in0=shifted, scalar=weight, in1=rows, op0=ALU.mult, op1=ALU.add)
@@ -359,33 +336,34 @@ def tile_causalwaveletfieldattentionh_pa_kernel(tc, x, Wkv_words, Wkv_scales, bk
                 in_=turned[:].rearrange("p (a h e) -> p h a e", a=4, h=2),
             )
 
-        def long_sums(pair, j):
+        def long_sum_terms(j):
+            return [(half, source) for half in range(2) for source in range(j // (STRIDE // 4) + 1)]
+
+        def long_sum(pair, j, half, source):
             b, group = divmod(j, STRIDE // 4)
-            summed[pair, j] = psum.tile([P, 4, 2, HEAD_DIM], F32, name="summed", tag="bank")
-            for half in range(2):
-                for source in range(b + 1):
-                    nc.tensor.matmul(
-                        out=summed[pair, j][:, :, half, :],
-                        lhsT=toeplitz[:, 2 * pair + half, P * (b - source) : P * (b - source + 1)],
-                        rhs=field_q[pair][:, source, half, 4 * group : 4 * group + 4, :],
-                        start=(half == 0 and source == 0),
-                        stop=False,
-                    )
+            if half == 0 and source == 0:
+                summed[pair, j] = psum.tile([P, 4, 2, HEAD_DIM], F32, name="summed", tag="bank")
+            nc.tensor.matmul(
+                out=summed[pair, j][:, :, half, :],
+                lhsT=toeplitz[:, 2 * pair + half, P * (b - source) : P * (b - source + 1)],
+                rhs=field_q[pair][:, source, half, 4 * group : 4 * group + 4, :],
+                start=(half == 0 and source == 0),
+                stop=False,
+            )
 
         def add_short_part_and_store(pair, j):
             if j == 0:
                 result[pair] = double.tile([P, BLOCKS, 2, STRIDE, HEAD_DIM], F32, name="result")
             b, group = divmod(j, STRIDE // 4)
-            for part in range(parts(pair)):
-                for i in range(4):
-                    nc.tensor.matmul(
-                        out=summed[pair, j][:, i, :, :],
-                        lhsT=short_t[pair, part][:, 4 * group + i, P * b : P * (b + 1)],
-                        rhs=ident[:].rearrange("p (h e) -> p h e", h=2),
-                        is_transpose=True,
-                        start=False,
-                        stop=(part == parts(pair) - 1 and i == 3),
-                    )
+            for i in range(4):
+                nc.tensor.matmul(
+                    out=summed[pair, j][:, i, :, :],
+                    lhsT=short_t[pair][:, 4 * group + i, P * b : P * (b + 1)],
+                    rhs=ident[:].rearrange("p (h e) -> p h e", h=2),
+                    is_transpose=True,
+                    start=False,
+                    stop=(i == 3),
+                )
             nc.scalar.copy(
                 out=result[pair][:, b, :, 4 * group : 4 * group + 4, :], in_=summed[pair, j][:].rearrange("p a h e -> p h a e")
             )
@@ -403,8 +381,10 @@ def tile_causalwaveletfieldattentionh_pa_kernel(tc, x, Wkv_words, Wkv_scales, bk
             if j + 2 < BANKS:
                 quantise_bank(j + 2)
             if j >= 1:
-                key_norms(0, j - 1)
-        key_norms(0, BANKS - 1)
+                for t in range(4 * (j - 1), 4 * j):
+                    key_norm(0, t)
+        for t in range(4 * (BANKS - 1), 4 * BANKS):
+            key_norm(0, t)
         waiting = []
         for j in range(BANKS):
             waiting.append(passes(PAIRS, j))
@@ -413,12 +393,11 @@ def tile_causalwaveletfieldattentionh_pa_kernel(tc, x, Wkv_words, Wkv_scales, bk
             read_v(0, j, waiting[j])
         for i in range(-2, PAIRS + 1):
             if live(i):
-                for t in range(parts(i)):
-                    short_shift(i, t)
+                short_shift(i, 0)
             if live(i + 1):
                 make_field(i + 1)
             if live(i):
-                for t in range(parts(i), len(short_shifts)):
+                for t in range(1, len(short_shifts)):
                     short_shift(i, t)
             if live(i + 2) and i + 2 > 0:
                 for j in range(BANKS):
@@ -431,14 +410,23 @@ def tile_causalwaveletfieldattentionh_pa_kernel(tc, x, Wkv_words, Wkv_scales, bk
             if i == -1:
                 build_toeplitz()
             for j in range(BANKS):
+                norms = list(range(4 * j, 4 * j + 4)) if live(i + K_AHEAD) else []
+                terms = long_sum_terms(j) if live(i - 1) and i - 1 < PAIRS - K_AHEAD else []
+                share = len(norms) // max(len(terms), 1)
+                for n, (half, source) in enumerate(terms):
+                    long_sum(i - 1, j, half, source)
+                    for t in norms[share * n : share * (n + 1)]:
+                        key_norm(i + K_AHEAD, t)
+                    if n == 0 and live(i):
+                        turn_field(i, j)
+                if not terms:
+                    for t in norms:
+                        key_norm(i + K_AHEAD, t)
+                    if live(i):
+                        turn_field(i, j)
                 if live(i - 1):
-                    if i - 1 < PAIRS - K_AHEAD:
-                        long_sums(i - 1, j)
                     add_short_part_and_store(i - 1, j)
-                if live(i + K_AHEAD):
-                    key_norms(i + K_AHEAD, j)
-                if live(i):
-                    turn_field(i, j)
             if live(i) and i >= PAIRS - K_AHEAD:
                 for j in range(BANKS):
-                    long_sums(i, j)
+                    for half, source in long_sum_terms(j):
+                        long_sum(i, j, half, source)

@@ -37,6 +37,14 @@ PERIOD = CLASS_LEN + P
 K_AHEAD = 3
 
 
+def parts(pair):
+    return 2 if pair + K_AHEAD >= PAIRS else 1
+
+
+def by_scalar(pair, j):
+    return pair > 0 and (j == 1 or (j == 2 and pair > K_AHEAD))
+
+
 FLOPS = 2 * TOKENS * DIM * 2 * DIM
 
 
@@ -64,6 +72,7 @@ def tile_causalwaveletfieldattentionh_pa_kernel(tc, x, Wkv_words, Wkv_scales, bk
         grouped_pool = ctx.enter_context(tc.tile_pool(name="grouped_pool", bufs=2))
         single = ctx.enter_context(tc.tile_pool(name="single", bufs=1))
         double = ctx.enter_context(tc.tile_pool(name="double", bufs=2))
+        shorts = ctx.enter_context(tc.tile_pool(name="shorts", bufs=4))
         psum = ctx.enter_context(tc.psum_pool(name="psum", bufs=8))
         ctx.enter_context(tc.manual_schedule(engines={mybir.EngineType.PE, mybir.EngineType.SP}))
 
@@ -113,6 +122,7 @@ def tile_causalwaveletfieldattentionh_pa_kernel(tc, x, Wkv_words, Wkv_scales, bk
         nc.gpsimd.memset(head_sel[:], 0.0)
         nc.gpsimd.memset(head_sel[0:HEAD_DIM, 0:1], 1.0)
         nc.gpsimd.memset(head_sel[HEAD_DIM:P, 1:2], 1.0)
+        squares_out = const.tile([P, HEAD_DIM], F32, name="squares_out")
         mag_q = const.tile([P, P], F32, name="mag_q")
         nc.gpsimd.memset(mag_q[:], 0.0)
 
@@ -219,7 +229,7 @@ def tile_causalwaveletfieldattentionh_pa_kernel(tc, x, Wkv_words, Wkv_scales, bk
             skewed = scratch.rearrange("(h z) -> h z", h=HEADS)[:, 0 : P * (PERIOD - 1)].rearrange("h (r w) -> r h w", r=P)
             nc.sync.dma_start(out=toeplitz[:], in_=skewed[:, :, 0:CLASS_LEN])
 
-        k_square, norm_ps, mag_t, field_q, short_t, summed, result = {}, {}, {}, {}, {}, {}, {}
+        k_square, norm_ps, norm_sb, mag_t, field_q, short_t, summed, result = {}, {}, {}, {}, {}, {}, {}, {}
 
         def passes(column_block, j):
             cols = slice(BANK * j, BANK * (j + 1))
@@ -242,7 +252,7 @@ def tile_causalwaveletfieldattentionh_pa_kernel(tc, x, Wkv_words, Wkv_scales, bk
             nc.scalar.activation(
                 out=k_square[pair][:, ROWS_PER_BANK * j : ROWS_PER_BANK * (j + 1), :],
                 in_=acc[:].rearrange("p (a q) -> p a q", a=ROWS_PER_BANK),
-                func=ACT.Square,
+                func=ACT.Identity if by_scalar(pair, j) else ACT.Square,
                 bias=bias_col[:, pair : pair + 1],
             )
 
@@ -263,6 +273,7 @@ def tile_causalwaveletfieldattentionh_pa_kernel(tc, x, Wkv_words, Wkv_scales, bk
         def key_norm(pair, t):
             if t == 0:
                 norm_ps[pair] = psum.tile([P, 2 * TOKENS // P], F32, name="norm_ps", tag="bank")
+                norm_sb[pair] = double.tile([P, 2 * TOKENS // P], F32, name="norm_sb")
             squares = k_square[pair][:].rearrange("p a q -> p (a q)")
             nc.tensor.matmul(
                 out=norm_ps[pair][:, 2 * t : 2 * t + 2],
@@ -271,8 +282,25 @@ def tile_causalwaveletfieldattentionh_pa_kernel(tc, x, Wkv_words, Wkv_scales, bk
                 start=True,
                 stop=True,
             )
-            if t == TOKENS // P - 1:
-                nc.scalar.activation(out=mag_q[:, 0 : 2 * TOKENS // P], in_=norm_ps[pair][:], func=ACT.Sqrt)
+
+        def key_norms_by_scalar(pair, j):
+            keys = k_square[pair][:].rearrange("p a q -> p (a q)")
+            turned = psum.tile([P, BANK], F32, name="turned", tag="bank")
+            for i in range(4):
+                nc.tensor.transpose(turned[:, P * i : P * (i + 1)], keys[:, P * (4 * j + i) : P * (4 * j + i + 1)], ident[:])
+            for i in range(2 * 4):
+                nc.scalar.activation(
+                    out=squares_out[:],
+                    in_=turned[:, HEAD_DIM * i : HEAD_DIM * (i + 1)],
+                    func=ACT.Square,
+                    accum_out=norm_sb[pair][:, 2 * 4 * j + i : 2 * 4 * j + i + 1],
+                )
+
+        def roots(pair):
+            for j in range(BANKS):
+                cols = slice(2 * 4 * j, 2 * 4 * (j + 1))
+                source = norm_sb[pair] if by_scalar(pair, j) else norm_ps[pair]
+                nc.scalar.activation(out=mag_q[:, cols], in_=source[:, cols], func=ACT.Sqrt)
 
         def spread_mag(pair):
             turned = psum.tile([P, P], F32, name="turned", tag="bank")
@@ -310,12 +338,13 @@ def tile_causalwaveletfieldattentionh_pa_kernel(tc, x, Wkv_words, Wkv_scales, bk
             shift = short_shifts[i]
             family, m = places[shift]
             weight = short_coef[:, pair, family, m : m + 1]
-            if i == 0:
-                short_t[pair] = double.tile([P, STRIDE, CLASS_LEN], F32, name="short_t")
+            part = i % parts(pair)
+            if i < parts(pair):
+                short_t[pair, part] = shorts.tile([P, STRIDE, CLASS_LEN], F32, name="short_t")
             for row0, row1 in ((shift % STRIDE, STRIDE), (0, shift % STRIDE)):
                 shifted = shifted_field(field_tiles[pair % 3], shift, row0, row1)
-                rows = short_t[pair][:, row0:row1, :]
-                if i == 0:
+                rows = short_t[pair, part][:, row0:row1, :]
+                if i < parts(pair):
                     nc.scalar.activation(out=rows, in_=shifted, func=ACT.Copy, scale=weight)
                 else:
                     nc.vector.scalar_tensor_tensor(out=rows, in0=shifted, scalar=weight, in1=rows, op0=ALU.mult, op1=ALU.add)
@@ -355,15 +384,16 @@ def tile_causalwaveletfieldattentionh_pa_kernel(tc, x, Wkv_words, Wkv_scales, bk
             if j == 0:
                 result[pair] = double.tile([P, BLOCKS, 2, STRIDE, HEAD_DIM], F32, name="result")
             b, group = divmod(j, STRIDE // 4)
-            for i in range(4):
-                nc.tensor.matmul(
-                    out=summed[pair, j][:, i, :, :],
-                    lhsT=short_t[pair][:, 4 * group + i, P * b : P * (b + 1)],
-                    rhs=ident[:].rearrange("p (h e) -> p h e", h=2),
-                    is_transpose=True,
-                    start=False,
-                    stop=(i == 3),
-                )
+            for part in range(parts(pair)):
+                for i in range(4):
+                    nc.tensor.matmul(
+                        out=summed[pair, j][:, i, :, :],
+                        lhsT=short_t[pair, part][:, 4 * group + i, P * b : P * (b + 1)],
+                        rhs=ident[:].rearrange("p (h e) -> p h e", h=2),
+                        is_transpose=True,
+                        start=False,
+                        stop=(part == parts(pair) - 1 and i == 3),
+                    )
             nc.scalar.copy(
                 out=result[pair][:, b, :, 4 * group : 4 * group + 4, :], in_=summed[pair, j][:].rearrange("p a h e -> p h a e")
             )
@@ -385,6 +415,7 @@ def tile_causalwaveletfieldattentionh_pa_kernel(tc, x, Wkv_words, Wkv_scales, bk
                     key_norm(0, t)
         for t in range(4 * (BANKS - 1), 4 * BANKS):
             key_norm(0, t)
+        roots(0)
         waiting = []
         for j in range(BANKS):
             waiting.append(passes(PAIRS, j))
@@ -393,11 +424,12 @@ def tile_causalwaveletfieldattentionh_pa_kernel(tc, x, Wkv_words, Wkv_scales, bk
             read_v(0, j, waiting[j])
         for i in range(-2, PAIRS + 1):
             if live(i):
-                short_shift(i, 0)
+                for t in range(parts(i)):
+                    short_shift(i, t)
             if live(i + 1):
                 make_field(i + 1)
             if live(i):
-                for t in range(1, len(short_shifts)):
+                for t in range(parts(i), len(short_shifts)):
                     short_shift(i, t)
             if live(i + 2) and i + 2 > 0:
                 for j in range(BANKS):
@@ -409,8 +441,9 @@ def tile_causalwaveletfieldattentionh_pa_kernel(tc, x, Wkv_words, Wkv_scales, bk
                 spread_mag(i + 2)
             if i == -1:
                 build_toeplitz()
+            early = live(i) and i >= PAIRS - K_AHEAD
             for j in range(BANKS):
-                norms = list(range(4 * j, 4 * j + 4)) if live(i + K_AHEAD) else []
+                norms = list(range(4 * j, 4 * j + 4)) if live(i + K_AHEAD) and not by_scalar(i + K_AHEAD, j) else []
                 terms = long_sum_terms(j) if live(i - 1) and i - 1 < PAIRS - K_AHEAD else []
                 share = len(norms) // max(len(terms), 1)
                 for n, (half, source) in enumerate(terms):
@@ -419,14 +452,22 @@ def tile_causalwaveletfieldattentionh_pa_kernel(tc, x, Wkv_words, Wkv_scales, bk
                         key_norm(i + K_AHEAD, t)
                     if n == 0 and live(i):
                         turn_field(i, j)
+                    if n == 0 and live(i + K_AHEAD) and by_scalar(i + K_AHEAD, j):
+                        key_norms_by_scalar(i + K_AHEAD, j)
                 if not terms:
+                    if live(i + K_AHEAD) and by_scalar(i + K_AHEAD, j):
+                        key_norms_by_scalar(i + K_AHEAD, j)
                     for t in norms:
                         key_norm(i + K_AHEAD, t)
                     if live(i):
                         turn_field(i, j)
                 if live(i - 1):
                     add_short_part_and_store(i - 1, j)
-            if live(i) and i >= PAIRS - K_AHEAD:
-                for j in range(BANKS):
-                    for half, source in long_sum_terms(j):
-                        long_sum(i, j, half, source)
+                if early and j >= 1:
+                    for half, source in long_sum_terms(j - 1):
+                        long_sum(i, j - 1, half, source)
+            if live(i + K_AHEAD):
+                roots(i + K_AHEAD)
+            if early:
+                for half, source in long_sum_terms(BANKS - 1):
+                    long_sum(i, BANKS - 1, half, source)

@@ -41,8 +41,12 @@ def parts(pair):
     return 2 if pair + K_AHEAD >= PAIRS else 1
 
 
+def by_vector(pair, j):
+    return pair == 1
+
+
 def by_scalar(pair, j):
-    return pair > 0 and (j == 1 or (j == 2 and pair > K_AHEAD))
+    return pair > 1 and (j == 1 or (j == 2 and pair > K_AHEAD))
 
 
 FLOPS = 2 * TOKENS * DIM * 2 * DIM
@@ -249,6 +253,7 @@ def tile_causalwaveletfieldattentionh_pa_kernel(tc, x, Wkv_words, Wkv_scales, bk
         def read_k(pair, j, acc):
             if j == 0:
                 k_square[pair] = single.tile([P, STRIDE, CLASS_LEN], F32, name="k_square")
+                norm_sb[pair] = double.tile([P, 2 * TOKENS // P], F32, name="norm_sb")
             nc.scalar.activation(
                 out=k_square[pair][:, ROWS_PER_BANK * j : ROWS_PER_BANK * (j + 1), :],
                 in_=acc[:].rearrange("p (a q) -> p a q", a=ROWS_PER_BANK),
@@ -271,9 +276,8 @@ def tile_causalwaveletfieldattentionh_pa_kernel(tc, x, Wkv_words, Wkv_scales, bk
             read_v(pair, j, passes(PAIRS + pair, j))
 
         def key_norm(pair, t):
-            if t == 0:
+            if pair not in norm_ps:
                 norm_ps[pair] = psum.tile([P, 2 * TOKENS // P], F32, name="norm_ps", tag="bank")
-                norm_sb[pair] = double.tile([P, 2 * TOKENS // P], F32, name="norm_sb")
             squares = k_square[pair][:].rearrange("p a q -> p (a q)")
             nc.tensor.matmul(
                 out=norm_ps[pair][:, 2 * t : 2 * t + 2],
@@ -296,10 +300,22 @@ def tile_causalwaveletfieldattentionh_pa_kernel(tc, x, Wkv_words, Wkv_scales, bk
                     accum_out=norm_sb[pair][:, 2 * 4 * j + i : 2 * 4 * j + i + 1],
                 )
 
+        def key_norms_by_vector(pair, j):
+            squares = k_square[pair][:].rearrange("p a q -> p (a q)")
+            turned = psum.tile([P, BANK], F32, name="turned", tag="bank")
+            for i in range(4):
+                nc.tensor.transpose(turned[:, P * i : P * (i + 1)], squares[:, P * (4 * j + i) : P * (4 * j + i + 1)], ident[:])
+            nc.vector.tensor_reduce(
+                out=norm_sb[pair][:, 2 * 4 * j : 2 * 4 * (j + 1)],
+                in_=turned[:].rearrange("p (i e) -> p i e", e=HEAD_DIM),
+                axis=AXIS.X,
+                op=ALU.add,
+            )
+
         def roots(pair):
             for j in range(BANKS):
                 cols = slice(2 * 4 * j, 2 * 4 * (j + 1))
-                source = norm_sb[pair] if by_scalar(pair, j) else norm_ps[pair]
+                source = norm_sb[pair] if by_scalar(pair, j) or by_vector(pair, j) else norm_ps[pair]
                 nc.scalar.activation(out=mag_q[:, cols], in_=source[:, cols], func=ACT.Sqrt)
 
         def spread_mag(pair):
@@ -344,7 +360,9 @@ def tile_causalwaveletfieldattentionh_pa_kernel(tc, x, Wkv_words, Wkv_scales, bk
             for row0, row1 in ((shift % STRIDE, STRIDE), (0, shift % STRIDE)):
                 shifted = shifted_field(field_tiles[pair % 3], shift, row0, row1)
                 rows = short_t[pair, part][:, row0:row1, :]
-                if i < parts(pair):
+                if i < parts(pair) and pair == 0:
+                    nc.vector.tensor_scalar_mul(out=rows, in0=shifted, scalar1=weight)
+                elif i < parts(pair):
                     nc.scalar.activation(out=rows, in_=shifted, func=ACT.Copy, scale=weight)
                 else:
                     nc.vector.scalar_tensor_tensor(out=rows, in0=shifted, scalar=weight, in1=rows, op0=ALU.mult, op1=ALU.add)
@@ -416,12 +434,11 @@ def tile_causalwaveletfieldattentionh_pa_kernel(tc, x, Wkv_words, Wkv_scales, bk
         for t in range(4 * (BANKS - 1), 4 * BANKS):
             key_norm(0, t)
         roots(0)
-        waiting = []
-        for j in range(BANKS):
-            waiting.append(passes(PAIRS, j))
+        first = passes(PAIRS, 0)
         spread_mag(0)
-        for j in range(BANKS):
-            read_v(0, j, waiting[j])
+        read_v(0, 0, first)
+        for j in range(1, BANKS):
+            project_v(0, j)
         for i in range(-2, PAIRS + 1):
             if live(i):
                 for t in range(parts(i)):
@@ -443,7 +460,7 @@ def tile_causalwaveletfieldattentionh_pa_kernel(tc, x, Wkv_words, Wkv_scales, bk
                 build_toeplitz()
             early = live(i) and i >= PAIRS - K_AHEAD
             for j in range(BANKS):
-                norms = list(range(4 * j, 4 * j + 4)) if live(i + K_AHEAD) and not by_scalar(i + K_AHEAD, j) else []
+                norms = list(range(4 * j, 4 * j + 4)) if live(i + K_AHEAD) and not by_scalar(i + K_AHEAD, j) and not by_vector(i + K_AHEAD, j) else []
                 terms = long_sum_terms(j) if live(i - 1) and i - 1 < PAIRS - K_AHEAD else []
                 share = len(norms) // max(len(terms), 1)
                 for n, (half, source) in enumerate(terms):
@@ -454,9 +471,13 @@ def tile_causalwaveletfieldattentionh_pa_kernel(tc, x, Wkv_words, Wkv_scales, bk
                         turn_field(i, j)
                     if n == 0 and live(i + K_AHEAD) and by_scalar(i + K_AHEAD, j):
                         key_norms_by_scalar(i + K_AHEAD, j)
+                    if n == 0 and live(i + K_AHEAD) and by_vector(i + K_AHEAD, j):
+                        key_norms_by_vector(i + K_AHEAD, j)
                 if not terms:
                     if live(i + K_AHEAD) and by_scalar(i + K_AHEAD, j):
                         key_norms_by_scalar(i + K_AHEAD, j)
+                    if live(i + K_AHEAD) and by_vector(i + K_AHEAD, j):
+                        key_norms_by_vector(i + K_AHEAD, j)
                     for t in norms:
                         key_norm(i + K_AHEAD, t)
                     if live(i):

@@ -34,19 +34,20 @@ ROWS_PER_BANK = BANK // CLASS_LEN
 BANKS = TOKENS // BANK
 PAD = 8
 PERIOD = CLASS_LEN + P
-K_AHEAD = 3
+EARLY = 5
+
+
+GROUPS = ((0,), (1,), (2, 3), (4, 5), (6, 7))
 
 
 def parts(pair):
-    return 2 if pair + K_AHEAD >= PAIRS else 1
+    return 1 if pair == 0 else 2
 
 
-def by_vector(pair, j):
-    return pair == 1
-
-
-def by_scalar(pair, j):
-    return pair > 1 and (j == 1 or (j == 2 and pair > K_AHEAD))
+def group_of(pair):
+    for group in GROUPS:
+        if pair in group:
+            return group, group.index(pair)
 
 
 FLOPS = 2 * TOKENS * DIM * 2 * DIM
@@ -69,12 +70,15 @@ def tile_causalwaveletfieldattentionh_pa_kernel(tc, x, Wkv_words, Wkv_scales, bk
     short_powers = 1 + max(places[s][1] for s in short_shifts)
     hop = SKIPS[0] // STRIDE
 
+    first_folded = min(group[0] for group in GROUPS if len(group) > 1)
+
     with ExitStack() as ctx:
         const = ctx.enter_context(tc.tile_pool(name="const", bufs=1))
         setup = ctx.enter_context(tc.tile_pool(name="setup", bufs=1))
         x_pool = ctx.enter_context(tc.tile_pool(name="x_pool", bufs=BANKS))
         grouped_pool = ctx.enter_context(tc.tile_pool(name="grouped_pool", bufs=2))
         single = ctx.enter_context(tc.tile_pool(name="single", bufs=1))
+        squares = ctx.enter_context(tc.tile_pool(name="squares", bufs=2))
         double = ctx.enter_context(tc.tile_pool(name="double", bufs=2))
         shorts = ctx.enter_context(tc.tile_pool(name="shorts", bufs=4))
         psum = ctx.enter_context(tc.psum_pool(name="psum", bufs=8))
@@ -85,16 +89,19 @@ def tile_causalwaveletfieldattentionh_pa_kernel(tc, x, Wkv_words, Wkv_scales, bk
         skip_bf = setup.tile([P, len(SKIPS)], BF16, name="skip_bf")
         nc.scalar.dma_start(out=skip_bf[:], in_=skip_w.partition_broadcast(P))
         bias_bf = setup.tile([2 * PAIRS, P], BF16, name="bias_bf")
-        nc.scalar.dma_start(out=bias_bf[:], in_=bkv.rearrange("(t c) -> t c", c=P))
+        bias_view = bkv.rearrange("(t c) -> t c", c=P)
+        nc.scalar.dma_start(out=bias_bf[0:first_folded, :], in_=bias_view[0:first_folded, :])
+        nc.scalar.dma_start(out=bias_bf[PAIRS : 2 * PAIRS, :], in_=bias_view[PAIRS : 2 * PAIRS, :])
+        for group in GROUPS:
+            if len(group) > 1:
+                channels = bkv[P * group[0] : P * (group[-1] + 1)]
+                nc.scalar.dma_start(
+                    out=bias_bf[group[0] : group[-1] + 1, :].rearrange("t (h w) -> t h w", h=2 * len(group)),
+                    in_=channels.rearrange("(h t w) -> t h w", h=2 * len(group), t=len(group)),
+                )
 
         w_scales = const.tile([P, K_PASSES, 2 * DIM], U8, name="w_scales", align_bytes=64)
         nc.vector.memset(w_scales[:].bitcast(I32), 0)
-        for g in range(K_PASSES):
-            for quad in range(4):
-                nc.sync.dma_start(
-                    out=w_scales[32 * quad : 32 * quad + 4, g, :].bitcast(I32),
-                    in_=Wkv_scales[g, 4 * quad : 4 * quad + 4, :].bitcast(I32),
-                )
 
         x_view = x.flatten_outer_dims().rearrange("(b p a) k -> p b a k", b=BLOCKS, p=P, a=STRIDE)
         x_rows = []
@@ -105,14 +112,39 @@ def tile_causalwaveletfieldattentionh_pa_kernel(tc, x, Wkv_words, Wkv_scales, bk
                 columns = slice(2 * P * first, 2 * P * last)
                 nc.sync.dma_start(out=w_words[:, g, columns].bitcast(I32), in_=Wkv_words[g, :, columns].bitcast(I32))
 
-        load_weight_blocks(0, 1)
-        load_weight_blocks(PAIRS, PAIRS + 1)
         for j in range(BANKS):
             rows = x_pool.tile([P, BLOCKS, ROWS_PER_BANK, DIM], BF16, name="x_rows")
-            nc.sync.dma_start(out=rows[:], in_=x_view[:, :, ROWS_PER_BANK * j : ROWS_PER_BANK * (j + 1), :])
+            if j == 0:
+                for a in range(ROWS_PER_BANK):
+                    nc.sync.dma_start(out=rows[:, :, a, :], in_=x_view[:, :, a, :])
+                for g in range(K_PASSES):
+                    for quad in range(4):
+                        nc.sync.dma_start(
+                            out=w_scales[32 * quad : 32 * quad + 4, g, :].bitcast(I32),
+                            in_=Wkv_scales[g, 4 * quad : 4 * quad + 4, :].bitcast(I32),
+                        )
+                load_weight_blocks(0, 1)
+                load_weight_blocks(PAIRS, PAIRS + 1)
+            else:
+                nc.sync.dma_start(out=rows[:], in_=x_view[:, :, ROWS_PER_BANK * j : ROWS_PER_BANK * (j + 1), :])
             x_rows.append(rows)
         load_weight_blocks(1, PAIRS)
         load_weight_blocks(PAIRS + 1, 2 * PAIRS)
+
+        folded_words = const.tile([P, K_PASSES, 2 * P * (PAIRS - first_folded)], U8, name="folded_words", align_bytes=64)
+        folded_scales = const.tile([P, K_PASSES, P * (PAIRS - first_folded)], U8, name="folded_scales", align_bytes=64)
+
+        def fold_weights(group):
+            size = len(group)
+            for g in range(K_PASSES):
+                for width, source, target in ((2, w_words, folded_words), (1, w_scales, folded_scales)):
+                    start = width * P * group[0]
+                    shift = width * P * first_folded
+                    length = width * P * size
+                    nc.gpsimd.tensor_copy(
+                        out=target[:, g, start - shift : start - shift + length].bitcast(U32).rearrange("p (t h w) -> p t h w", t=size, h=2 * size),
+                        in_=source[:, g, start : start + length].bitcast(U32).rearrange("p (h t w) -> p t h w", t=size, h=2 * size),
+                    )
 
         ident = const.tile([P, P], F32, name="ident")
         make_identity(nc, ident[:])
@@ -122,11 +154,6 @@ def tile_causalwaveletfieldattentionh_pa_kernel(tc, x, Wkv_words, Wkv_scales, bk
             nc.gpsimd.memset(field_tile[:, :, 0:PAD], 0.0)
             field_tiles.append(field_tile)
 
-        head_sel = const.tile([P, 2], F32, name="head_sel")
-        nc.gpsimd.memset(head_sel[:], 0.0)
-        nc.gpsimd.memset(head_sel[0:HEAD_DIM, 0:1], 1.0)
-        nc.gpsimd.memset(head_sel[HEAD_DIM:P, 1:2], 1.0)
-        squares_out = const.tile([P, HEAD_DIM], F32, name="squares_out")
         mag_q = const.tile([P, P], F32, name="mag_q")
         nc.gpsimd.memset(mag_q[:], 0.0)
 
@@ -135,10 +162,12 @@ def tile_causalwaveletfieldattentionh_pa_kernel(tc, x, Wkv_words, Wkv_scales, bk
         coef_row = setup.tile([P, HEADS, PERIOD], F32, name="coef_row")
         nc.gpsimd.memset(coef_row[:], 0.0)
         nc.vector.tensor_copy(out=bias_rows[0 : 2 * PAIRS, :], in_=bias_bf[:])
-        bias_ps = psum.tile([P, P], F32, name="bias_ps", tag="bank")
-        nc.tensor.transpose(bias_ps[:], bias_rows[:], ident[:])
         bias_col = const.tile([P, 2 * PAIRS], F32, name="bias_col")
-        nc.vector.tensor_copy(out=bias_col[:], in_=bias_ps[:, 0 : 2 * PAIRS])
+
+        def turn_bias():
+            bias_ps = psum.tile([P, P], F32, name="bias_ps", tag="bank")
+            nc.tensor.transpose(bias_ps[:], bias_rows[:], ident[:])
+            nc.vector.tensor_copy(out=bias_col[:], in_=bias_ps[:, 0 : 2 * PAIRS])
 
         gains = setup.tile([P, SCALES, HEADS], F32, name="gains")
         nc.vector.tensor_copy(out=gains[:].rearrange("p j h -> p (j h)"), in_=gain_bf[:])
@@ -152,14 +181,8 @@ def tile_causalwaveletfieldattentionh_pa_kernel(tc, x, Wkv_words, Wkv_scales, bk
         nc.vector.tensor_copy(out=skip_f32[:], in_=skip_bf[:])
         skip_gate = const.tile([P, len(SKIPS)], F32, name="skip_gate")
         nc.scalar.activation(out=skip_gate[:], in_=skip_f32[:], func=ACT.Sigmoid)
-        total = setup.tile([P, HEADS], F32, name="total")
-        nc.vector.tensor_reduce(out=total[:], in_=gains[:].rearrange("p j h -> p h j"), axis=AXIS.X, op=ALU.add)
-        inverse = setup.tile([P, HEADS], F32, name="inverse")
-        nc.vector.reciprocal(out=inverse[:], in_=total[:])
-        nc.vector.tensor_tensor(
-            out=gains[:], in0=gains[:], in1=inverse[:].unsqueeze(1).to_broadcast([P, SCALES, HEADS]), op=ALU.mult
-        )
-
+        first_root = setup.tile([P, 1], F32, name="first_root")
+        nc.scalar.activation(out=first_root[:], in_=gains[:, 0, 0:1], func=ACT.Sqrt, bias=skip_gate[:, 0:1])
         x_codes = const.tile([P, K_PASSES, TOKENS], U32, name="x_codes", align_bytes=64)
         x_scales = const.tile([P, K_PASSES, TOKENS], U8, name="x_scales", align_bytes=64)
 
@@ -203,29 +226,37 @@ def tile_causalwaveletfieldattentionh_pa_kernel(tc, x, Wkv_words, Wkv_scales, bk
         short_coef = const.tile([P, PAIRS, 2, short_powers], F32, name="short_coef")
         toeplitz = const.tile([P, HEADS, CLASS_LEN], F32, name="toeplitz")
 
-        weights = setup.tile([P, 2, SCALES + 1, HEADS], F32, name="weights")
-        nc.vector.tensor_scalar_mul(out=weights[:, 0, 0:SCALES, :], in0=gains[:], scalar1=D4[2])
-        nc.vector.tensor_scalar_mul(out=weights[:, 1, 0:SCALES, :], in0=gains[:], scalar1=D4[0])
-        nc.vector.tensor_scalar_mul(out=weights[:, 0, SCALES, :], in0=gains[:, SCALES - 1, :], scalar1=D4[1])
-        nc.vector.scalar_tensor_tensor(
-            out=weights[:, 0, 1:SCALES, :],
-            in0=gains[:, 0 : SCALES - 1, :],
-            scalar=D4[1],
-            in1=weights[:, 0, 1:SCALES, :],
-            op0=ALU.mult,
-            op1=ALU.add,
-        )
-        for half in range(2):
-            rows = slice(HEAD_DIM * half, HEAD_DIM * (half + 1))
-            by_pair = weights[rows, :, 0:short_powers, :].rearrange("p f m (c w) -> p c f m w", w=2)
-            nc.vector.tensor_copy(out=short_coef[rows], in_=by_pair[:, :, :, :, half])
-        gain_sum = setup.tile([P, HEADS], F32, name="gain_sum")
-        nc.vector.tensor_reduce(out=gain_sum[:], in_=gains[:].rearrange("p j h -> p h j"), axis=AXIS.X, op=ALU.add)
-        nc.vector.tensor_scalar_mul(out=weights[:, 1, SCALES, :], in0=gain_sum[:], scalar1=D4[3])
-        nc.gpsimd.tensor_copy(out=coef_row[:, :, 0], in_=weights[:, 1, SCALES, :])
-        for shift in long_shifts:
-            family, m = places[shift]
-            nc.gpsimd.tensor_copy(out=coef_row[:, :, shift // STRIDE], in_=weights[:, family, m, :])
+        def make_weights():
+            total = setup.tile([P, HEADS], F32, name="total")
+            nc.vector.tensor_reduce(out=total[:], in_=gains[:].rearrange("p j h -> p h j"), axis=AXIS.X, op=ALU.add)
+            inverse = setup.tile([P, HEADS], F32, name="inverse")
+            nc.vector.reciprocal(out=inverse[:], in_=total[:])
+            nc.vector.tensor_tensor(
+                out=gains[:], in0=gains[:], in1=inverse[:].unsqueeze(1).to_broadcast([P, SCALES, HEADS]), op=ALU.mult
+            )
+            weights = setup.tile([P, 2, SCALES + 1, HEADS], F32, name="weights")
+            nc.vector.tensor_scalar_mul(out=weights[:, 0, 0:SCALES, :], in0=gains[:], scalar1=D4[2])
+            nc.vector.tensor_scalar_mul(out=weights[:, 1, 0:SCALES, :], in0=gains[:], scalar1=D4[0])
+            nc.vector.tensor_scalar_mul(out=weights[:, 0, SCALES, :], in0=gains[:, SCALES - 1, :], scalar1=D4[1])
+            nc.vector.scalar_tensor_tensor(
+                out=weights[:, 0, 1:SCALES, :],
+                in0=gains[:, 0 : SCALES - 1, :],
+                scalar=D4[1],
+                in1=weights[:, 0, 1:SCALES, :],
+                op0=ALU.mult,
+                op1=ALU.add,
+            )
+            for half in range(2):
+                rows = slice(HEAD_DIM * half, HEAD_DIM * (half + 1))
+                by_pair = weights[rows, :, 0:short_powers, :].rearrange("p f m (c w) -> p c f m w", w=2)
+                nc.vector.tensor_copy(out=short_coef[rows], in_=by_pair[:, :, :, :, half])
+            gain_sum = setup.tile([P, HEADS], F32, name="gain_sum")
+            nc.vector.tensor_reduce(out=gain_sum[:], in_=gains[:].rearrange("p j h -> p h j"), axis=AXIS.X, op=ALU.add)
+            nc.vector.tensor_scalar_mul(out=weights[:, 1, SCALES, :], in0=gain_sum[:], scalar1=D4[3])
+            nc.gpsimd.tensor_copy(out=coef_row[:, :, 0], in_=weights[:, 1, SCALES, :])
+            for shift in long_shifts:
+                family, m = places[shift]
+                nc.gpsimd.tensor_copy(out=coef_row[:, :, shift // STRIDE], in_=weights[:, family, m, :])
 
         def build_toeplitz():
             scratch = out_flat[0 : HEADS * P * PERIOD]
@@ -233,16 +264,19 @@ def tile_causalwaveletfieldattentionh_pa_kernel(tc, x, Wkv_words, Wkv_scales, bk
             skewed = scratch.rearrange("(h z) -> h z", h=HEADS)[:, 0 : P * (PERIOD - 1)].rearrange("h (r w) -> r h w", r=P)
             nc.sync.dma_start(out=toeplitz[:], in_=skewed[:, :, 0:CLASS_LEN])
 
-        k_square, norm_ps, norm_sb, mag_t, field_q, short_t, summed, result = {}, {}, {}, {}, {}, {}, {}, {}
+        mag_wide, mag_ps, k_square, norm_sb, parked, mag_t, field_q, short_t, summed, result = {}, {}, {}, {}, {}, {}, {}, {}, {}, {}
 
         def passes(column_block, j):
             cols = slice(BANK * j, BANK * (j + 1))
+            folded = first_folded <= column_block < PAIRS
+            words, scales = (folded_words, folded_scales) if folded else (w_words, w_scales)
+            block = column_block - first_folded if folded else column_block
             acc = psum.tile([P, BANK], F32, name="acc", tag="bank")
             for g in range(K_PASSES):
                 nc.tensor.matmul_mx(
                     out=acc[:],
-                    lhsT=w_words[:, g, 2 * P * column_block : 2 * P * (column_block + 1)].bitcast(FP4X4),
-                    lhsT_scale=w_scales[:, g, P * column_block : P * (column_block + 1)],
+                    lhsT=words[:, g, 2 * P * block : 2 * P * (block + 1)].bitcast(FP4X4),
+                    lhsT_scale=scales[:, g, P * block : P * (block + 1)],
                     rhs=x_codes[:, g, cols].bitcast(FP8X4),
                     rhs_scale=x_scales[:, g, cols],
                     start=(g == 0),
@@ -250,18 +284,16 @@ def tile_causalwaveletfieldattentionh_pa_kernel(tc, x, Wkv_words, Wkv_scales, bk
                 )
             return acc
 
-        def read_k(pair, j, acc):
-            if j == 0:
-                k_square[pair] = single.tile([P, STRIDE, CLASS_LEN], F32, name="k_square")
-                norm_sb[pair] = double.tile([P, 2 * TOKENS // P], F32, name="norm_sb")
-            nc.scalar.activation(
-                out=k_square[pair][:, ROWS_PER_BANK * j : ROWS_PER_BANK * (j + 1), :],
-                in_=acc[:].rearrange("p (a q) -> p a q", a=ROWS_PER_BANK),
-                func=ACT.Identity if by_scalar(pair, j) else ACT.Square,
-                bias=bias_col[:, pair : pair + 1],
-            )
+        def project_k(group, j):
+            k_square[group, j] = squares.tile([P, len(group), BANK], F32, name="k_square")
+            for t, pair in enumerate(group):
+                acc = passes(pair, j)
+                nc.scalar.activation(
+                    out=k_square[group, j][:, t, :], in_=acc[:], func=ACT.Square, bias=bias_col[:, pair : pair + 1]
+                )
 
-        def read_v(pair, j, acc):
+        def project_v(pair, j):
+            acc = passes(PAIRS + pair, j)
             nc.scalar.activation(
                 out=field_tiles[pair % 3][:, ROWS_PER_BANK * j : ROWS_PER_BANK * (j + 1), PAD:],
                 in_=acc[:].rearrange("p (a q) -> p a q", a=ROWS_PER_BANK),
@@ -269,68 +301,63 @@ def tile_causalwaveletfieldattentionh_pa_kernel(tc, x, Wkv_words, Wkv_scales, bk
                 bias=bias_col[:, PAIRS + pair : PAIRS + pair + 1],
             )
 
-        def project_k(pair, j):
-            read_k(pair, j, passes(pair, j))
-
-        def project_v(pair, j):
-            read_v(pair, j, passes(PAIRS + pair, j))
-
-        def key_norm(pair, t):
-            if pair not in norm_ps:
-                norm_ps[pair] = psum.tile([P, 2 * TOKENS // P], F32, name="norm_ps", tag="bank")
-            squares = k_square[pair][:].rearrange("p a q -> p (a q)")
-            nc.tensor.matmul(
-                out=norm_ps[pair][:, 2 * t : 2 * t + 2],
-                lhsT=squares[:, P * t : P * (t + 1)],
-                rhs=head_sel[:],
-                start=True,
-                stop=True,
-            )
-
-        def key_norms_by_scalar(pair, j):
-            keys = k_square[pair][:].rearrange("p a q -> p (a q)")
+        def key_norms(group, j):
+            size = len(group)
+            if j == 0:
+                norm_sb[group] = double.tile([P, TOKENS // P, 2 * size], F32, name="norm_sb")
             turned = psum.tile([P, BANK], F32, name="turned", tag="bank")
             for i in range(4):
-                nc.tensor.transpose(turned[:, P * i : P * (i + 1)], keys[:, P * (4 * j + i) : P * (4 * j + i + 1)], ident[:])
-            for i in range(2 * 4):
-                nc.scalar.activation(
-                    out=squares_out[:],
-                    in_=turned[:, HEAD_DIM * i : HEAD_DIM * (i + 1)],
-                    func=ACT.Square,
-                    accum_out=norm_sb[pair][:, 2 * 4 * j + i : 2 * 4 * j + i + 1],
-                )
-
-        def key_norms_by_vector(pair, j):
-            squares = k_square[pair][:].rearrange("p a q -> p (a q)")
-            turned = psum.tile([P, BANK], F32, name="turned", tag="bank")
-            for i in range(4):
-                nc.tensor.transpose(turned[:, P * i : P * (i + 1)], squares[:, P * (4 * j + i) : P * (4 * j + i + 1)], ident[:])
+                for t in range(size):
+                    nc.tensor.matmul(
+                        out=turned[:, P * i : P * (i + 1)],
+                        lhsT=k_square[group, j][:, t, P * i : P * (i + 1)],
+                        rhs=ident[:],
+                        is_transpose=True,
+                        start=(i == 0 and t == 0),
+                        stop=(i == 3 and t == size - 1),
+                    )
             nc.vector.tensor_reduce(
-                out=norm_sb[pair][:, 2 * 4 * j : 2 * 4 * (j + 1)],
-                in_=turned[:].rearrange("p (i e) -> p i e", e=HEAD_DIM),
+                out=norm_sb[group][:, 4 * j : 4 * (j + 1), :].rearrange("p i h -> p (i h)"),
+                in_=turned[:].rearrange("p (i e) -> p i e", e=HEAD_DIM // size),
                 axis=AXIS.X,
                 op=ALU.add,
             )
 
-        def roots(pair):
-            for j in range(BANKS):
-                cols = slice(2 * 4 * j, 2 * 4 * (j + 1))
-                source = norm_sb[pair] if by_scalar(pair, j) or by_vector(pair, j) else norm_ps[pair]
-                nc.scalar.activation(out=mag_q[:, cols], in_=source[:, cols], func=ACT.Sqrt)
-
-        def spread_mag(pair):
+        def park_mag(group):
+            rows = 2 * len(group) * TOKENS // P
+            nc.scalar.activation(out=mag_q[:, 0:rows], in_=norm_sb[group][:].rearrange("p i h -> p (i h)"), func=ACT.Sqrt)
             turned = psum.tile([P, P], F32, name="turned", tag="bank")
             nc.tensor.transpose(turned[:], mag_q[:], ident[:])
-            mag_rows = single.tile([2 * TOKENS // P, P], F32, name="mag_rows")
-            nc.scalar.copy(out=mag_rows[:], in_=turned[0 : 2 * TOKENS // P, :])
-            parked = out_flat[out_flat.shape[0] - 2 * TOKENS * (pair + 1) : out_flat.shape[0] - 2 * TOKENS * pair]
-            nc.sync.dma_start(out=parked.rearrange("(r q) -> r q", q=P), in_=mag_rows[:])
+            mag_rows = single.tile([P, P], F32, name="mag_rows")
+            nc.scalar.copy(out=mag_rows[0:rows, :], in_=turned[0:rows, :])
+            end = out_flat.shape[0] - 2 * TOKENS * group[0]
+            parked[group] = out_flat[end - rows * P : end]
+            nc.sync.dma_start(out=parked[group].rearrange("(r q) -> r q", q=P), in_=mag_rows[0:rows, :])
+
+        def spread_mag(pair):
+            group, place = group_of(pair)
             mag_t[pair] = double.tile([P, TOKENS], F32, name="mag_t")
             for half in range(2):
                 nc.sync.dma_start(
                     out=mag_t[pair][HEAD_DIM * half : HEAD_DIM * (half + 1), :].rearrange("p (t q) -> p t q", q=P),
-                    in_=parked.rearrange("(t h q) -> h t q", h=2, q=P)[half].partition_broadcast(HEAD_DIM),
+                    in_=parked[group].rearrange("(t h q) -> h t q", h=2 * len(group), q=P)[2 * place + half].partition_broadcast(HEAD_DIM),
                 )
+
+        def wide_roots(group, j):
+            if j == 0:
+                mag_wide[group] = x_pool.tile([P, 2 * TOKENS // P, HEAD_DIM], F32, name="mag_wide", tag="x_rows")
+            cols = slice(2 * 4 * j, 2 * 4 * (j + 1))
+            nc.scalar.activation(
+                out=mag_wide[group][:, cols, :],
+                in_=norm_sb[group][:].rearrange("p i h -> p (i h)")[:, cols].unsqueeze(2).to_broadcast([P, 2 * 4, HEAD_DIM]),
+                func=ACT.Sqrt,
+            )
+
+        def spread_mag_by_tensor(group, j):
+            mag_ps[group, j] = psum.tile([P, BANK], F32, name="mag_ps", tag="bank")
+            wide = mag_wide[group][:].rearrange("p r e -> p (r e)")
+            for i in range(4):
+                nc.tensor.transpose(mag_ps[group, j][:, P * i : P * (i + 1)], wide[:, P * (4 * j + i) : P * (4 * j + i + 1)], ident[:])
 
         def shifted_field(field_t, shift, row0, row1):
             steps, residue = divmod(shift, STRIDE)
@@ -342,12 +369,15 @@ def tile_causalwaveletfieldattentionh_pa_kernel(tc, x, Wkv_words, Wkv_scales, bk
 
         def make_field(pair):
             field_t = field_tiles[pair % 3]
-            nc.vector.tensor_tensor(
-                out=field_t[:, :, PAD:],
-                in0=field_t[:, :, PAD:],
-                in1=mag_t[pair][:].rearrange("p (a q) -> p a q", a=STRIDE),
-                op=ALU.mult,
-            )
+            for j in range(BANKS if pair == 0 else 1):
+                rows = slice(ROWS_PER_BANK * j, ROWS_PER_BANK * (j + 1)) if pair == 0 else slice(0, STRIDE)
+                mag = mag_ps[(0,), j] if pair == 0 else mag_t[pair]
+                nc.vector.tensor_tensor(
+                    out=field_t[:, rows, PAD:],
+                    in0=field_t[:, rows, PAD:],
+                    in1=mag[:].rearrange("p (a q) -> p a q", q=CLASS_LEN),
+                    op=ALU.mult,
+                )
             add_skips(field_t[:, :, PAD:])
 
         def short_shift(pair, i):
@@ -422,23 +452,34 @@ def tile_causalwaveletfieldattentionh_pa_kernel(tc, x, Wkv_words, Wkv_scales, bk
         def live(pair):
             return 0 <= pair < PAIRS
 
+        k_units = {-2: [((1,), j) for j in range(BANKS)], -1: [((2, 3), j) for j in range(BANKS)]}
+        for n, group in enumerate(GROUPS[3:]):
+            for j in range(BANKS):
+                k_units.setdefault(2 * n + j // 2, []).append((group, j))
+
+        head = GROUPS[0]
         quantise_bank(0)
+        turn_bias()
         quantise_bank(1)
         for j in range(BANKS):
-            project_k(0, j)
+            project_k(head, j)
             if j + 2 < BANKS:
                 quantise_bank(j + 2)
             if j >= 1:
-                for t in range(4 * (j - 1), 4 * j):
-                    key_norm(0, t)
-        for t in range(4 * (BANKS - 1), 4 * BANKS):
-            key_norm(0, t)
-        roots(0)
-        first = passes(PAIRS, 0)
-        spread_mag(0)
-        read_v(0, 0, first)
-        for j in range(1, BANKS):
-            project_v(0, j)
+                key_norms(head, j - 1)
+                wide_roots(head, j - 1)
+        project_v(0, 0)
+        key_norms(head, BANKS - 1)
+        wide_roots(head, BANKS - 1)
+        project_v(0, 1)
+        make_weights()
+        for group in GROUPS:
+            if len(group) > 1:
+                fold_weights(group)
+        for j in range(BANKS):
+            spread_mag_by_tensor(head, j)
+            if j < 2:
+                project_v(0, j + 2)
         for i in range(-2, PAIRS + 1):
             if live(i):
                 for t in range(parts(i)):
@@ -451,44 +492,41 @@ def tile_causalwaveletfieldattentionh_pa_kernel(tc, x, Wkv_words, Wkv_scales, bk
             if live(i + 2) and i + 2 > 0:
                 for j in range(BANKS):
                     project_v(i + 2, j)
-            if live(i + K_AHEAD):
-                for j in range(BANKS):
-                    project_k(i + K_AHEAD, j)
-            if live(i + 2) and i + 2 > 0:
                 spread_mag(i + 2)
+            units = k_units.get(i, [])
+            late = []
+            for unit in units:
+                project_k(*unit)
+                if i < 0:
+                    late.append(unit)
+                    if len(late) > 1:
+                        key_norms(*late.pop(0))
+                else:
+                    late.append(unit)
             if i == -1:
                 build_toeplitz()
-            early = live(i) and i >= PAIRS - K_AHEAD
+            early = live(i) and i >= EARLY
             for j in range(BANKS):
-                norms = list(range(4 * j, 4 * j + 4)) if live(i + K_AHEAD) and not by_scalar(i + K_AHEAD, j) and not by_vector(i + K_AHEAD, j) else []
-                terms = long_sum_terms(j) if live(i - 1) and i - 1 < PAIRS - K_AHEAD else []
-                share = len(norms) // max(len(terms), 1)
+                terms = long_sum_terms(j) if live(i - 1) and i - 1 < EARLY else []
                 for n, (half, source) in enumerate(terms):
                     long_sum(i - 1, j, half, source)
-                    for t in norms[share * n : share * (n + 1)]:
-                        key_norm(i + K_AHEAD, t)
                     if n == 0 and live(i):
                         turn_field(i, j)
-                    if n == 0 and live(i + K_AHEAD) and by_scalar(i + K_AHEAD, j):
-                        key_norms_by_scalar(i + K_AHEAD, j)
-                    if n == 0 and live(i + K_AHEAD) and by_vector(i + K_AHEAD, j):
-                        key_norms_by_vector(i + K_AHEAD, j)
+                    if n == 1 and j >= 2 and late:
+                        key_norms(*late.pop(0))
                 if not terms:
-                    if live(i + K_AHEAD) and by_scalar(i + K_AHEAD, j):
-                        key_norms_by_scalar(i + K_AHEAD, j)
-                    if live(i + K_AHEAD) and by_vector(i + K_AHEAD, j):
-                        key_norms_by_vector(i + K_AHEAD, j)
-                    for t in norms:
-                        key_norm(i + K_AHEAD, t)
                     if live(i):
                         turn_field(i, j)
+                    if late:
+                        key_norms(*late.pop(0))
                 if live(i - 1):
                     add_short_part_and_store(i - 1, j)
                 if early and j >= 1:
                     for half, source in long_sum_terms(j - 1):
                         long_sum(i, j - 1, half, source)
-            if live(i + K_AHEAD):
-                roots(i + K_AHEAD)
+            for unit in units:
+                if unit[1] == BANKS - 1:
+                    park_mag(unit[0])
             if early:
                 for half, source in long_sum_terms(BANKS - 1):
                     long_sum(i, BANKS - 1, half, source)

@@ -1,4 +1,5 @@
 from contextlib import ExitStack
+from itertools import product
 
 import concourse.mybir as mybir
 from concourse.masks import make_identity
@@ -37,11 +38,11 @@ PERIOD = CLASS_LEN + P
 EARLY = 5
 
 
-GROUPS = ((0,), (1,), (2, 3), (4, 5), (6, 7))
+GROUPS = ((0,), (1,), (2, 3), (4, 5, 6, 7))
 
 
 def parts(pair):
-    return 1 if pair == 0 else 2
+    return 2 if pair >= 3 else 1
 
 
 def group_of(pair):
@@ -75,14 +76,16 @@ def tile_causalwaveletfieldattentionh_pa_kernel(tc, x, Wkv_words, Wkv_scales, bk
     with ExitStack() as ctx:
         const = ctx.enter_context(tc.tile_pool(name="const", bufs=1))
         setup = ctx.enter_context(tc.tile_pool(name="setup", bufs=1))
-        x_pool = ctx.enter_context(tc.tile_pool(name="x_pool", bufs=BANKS))
+        x_pool = ctx.enter_context(tc.tile_pool(name="x_pool", bufs=2 * BANKS - 1))
         grouped_pool = ctx.enter_context(tc.tile_pool(name="grouped_pool", bufs=2))
         single = ctx.enter_context(tc.tile_pool(name="single", bufs=1))
         squares = ctx.enter_context(tc.tile_pool(name="squares", bufs=2))
         double = ctx.enter_context(tc.tile_pool(name="double", bufs=2))
-        shorts = ctx.enter_context(tc.tile_pool(name="shorts", bufs=4))
         psum = ctx.enter_context(tc.psum_pool(name="psum", bufs=8))
-        ctx.enter_context(tc.manual_schedule(engines={mybir.EngineType.PE, mybir.EngineType.SP}))
+        ctx.enter_context(tc.manual_schedule())
+
+        ident = const.tile([P, P], F32, name="ident")
+        make_identity(nc, ident[:])
 
         gain_bf = setup.tile([P, SCALES * HEADS], BF16, name="gain_bf")
         nc.scalar.dma_start(out=gain_bf[:], in_=scale_gain.rearrange("j h -> (j h)").partition_broadcast(P))
@@ -90,18 +93,23 @@ def tile_causalwaveletfieldattentionh_pa_kernel(tc, x, Wkv_words, Wkv_scales, bk
         nc.scalar.dma_start(out=skip_bf[:], in_=skip_w.partition_broadcast(P))
         bias_bf = setup.tile([2 * PAIRS, P], BF16, name="bias_bf")
         bias_view = bkv.rearrange("(t c) -> t c", c=P)
-        nc.scalar.dma_start(out=bias_bf[0:first_folded, :], in_=bias_view[0:first_folded, :])
-        nc.scalar.dma_start(out=bias_bf[PAIRS : 2 * PAIRS, :], in_=bias_view[PAIRS : 2 * PAIRS, :])
-        for group in GROUPS:
-            if len(group) > 1:
-                channels = bkv[P * group[0] : P * (group[-1] + 1)]
-                nc.scalar.dma_start(
-                    out=bias_bf[group[0] : group[-1] + 1, :].rearrange("t (h w) -> t h w", h=2 * len(group)),
-                    in_=channels.rearrange("(h t w) -> t h w", h=2 * len(group), t=len(group)),
-                )
+
+        def load_bias():
+            nc.sync.dma_start(out=bias_bf[0:first_folded, :], in_=bias_view[0:first_folded, :])
+            nc.sync.dma_start(out=bias_bf[PAIRS : 2 * PAIRS, :], in_=bias_view[PAIRS : 2 * PAIRS, :])
+            for group in GROUPS:
+                if len(group) > 1:
+                    channels = bkv[P * group[0] : P * (group[-1] + 1)]
+                    nc.sync.dma_start(
+                        out=bias_bf[group[0] : group[-1] + 1, :].rearrange("t (h w) -> t h w", h=2 * len(group)),
+                        in_=channels.rearrange("(h t w) -> t h w", h=2 * len(group), t=len(group)),
+                    )
 
         w_scales = const.tile([P, K_PASSES, 2 * DIM], U8, name="w_scales", align_bytes=64)
         nc.vector.memset(w_scales[:].bitcast(I32), 0)
+        first_exp = setup.tile([P, 1], F32, name="first_exp")
+        nc.vector.memset(first_exp[:], 0.0)
+        nc.scalar.activation(out=first_exp[:], in_=first_exp[:], func=ACT.Exp)
 
         x_view = x.flatten_outer_dims().rearrange("(b p a) k -> p b a k", b=BLOCKS, p=P, a=STRIDE)
         x_rows = []
@@ -112,22 +120,23 @@ def tile_causalwaveletfieldattentionh_pa_kernel(tc, x, Wkv_words, Wkv_scales, bk
                 columns = slice(2 * P * first, 2 * P * last)
                 nc.sync.dma_start(out=w_words[:, g, columns].bitcast(I32), in_=Wkv_words[g, :, columns].bitcast(I32))
 
+        def load_x(j, classes):
+            nc.sync.dma_start(out=x_rows[j][:, :, classes.start - ROWS_PER_BANK * j : classes.stop - ROWS_PER_BANK * j, :], in_=x_view[:, :, classes, :])
+
         for j in range(BANKS):
-            rows = x_pool.tile([P, BLOCKS, ROWS_PER_BANK, DIM], BF16, name="x_rows")
-            if j == 0:
-                for a in range(ROWS_PER_BANK):
-                    nc.sync.dma_start(out=rows[:, :, a, :], in_=x_view[:, :, a, :])
-                for g in range(K_PASSES):
-                    for quad in range(4):
-                        nc.sync.dma_start(
-                            out=w_scales[32 * quad : 32 * quad + 4, g, :].bitcast(I32),
-                            in_=Wkv_scales[g, 4 * quad : 4 * quad + 4, :].bitcast(I32),
-                        )
-                load_weight_blocks(0, 1)
-                load_weight_blocks(PAIRS, PAIRS + 1)
-            else:
-                nc.sync.dma_start(out=rows[:], in_=x_view[:, :, ROWS_PER_BANK * j : ROWS_PER_BANK * (j + 1), :])
-            x_rows.append(rows)
+            x_rows.append(x_pool.tile([P, BLOCKS, ROWS_PER_BANK, DIM], BF16, name="x_rows"))
+        for a in range(ROWS_PER_BANK):
+            load_x(0, slice(a, a + 1))
+        for r in range(4):
+            nc.sync.dma_start(
+                out=w_scales[r:P:32, :, :].bitcast(I32), in_=Wkv_scales[:, r:16:4, :].rearrange("g q n -> q g n").bitcast(I32)
+            )
+        load_weight_blocks(0, 1)
+        load_x(1, slice(ROWS_PER_BANK, 2 * ROWS_PER_BANK))
+        load_weight_blocks(PAIRS, PAIRS + 1)
+        load_bias()
+        for j in range(2, BANKS):
+            load_x(j, slice(ROWS_PER_BANK * j, ROWS_PER_BANK * (j + 1)))
         load_weight_blocks(1, PAIRS)
         load_weight_blocks(PAIRS + 1, 2 * PAIRS)
 
@@ -146,8 +155,6 @@ def tile_causalwaveletfieldattentionh_pa_kernel(tc, x, Wkv_words, Wkv_scales, bk
                         in_=source[:, g, start : start + length].bitcast(U32).rearrange("p (h t w) -> p t h w", t=size, h=2 * size),
                     )
 
-        ident = const.tile([P, P], F32, name="ident")
-        make_identity(nc, ident[:])
         field_tiles = []
         for i in range(3):
             field_tile = const.tile([P, STRIDE, PAD + CLASS_LEN], F32, name="field_t%d" % i)
@@ -158,11 +165,17 @@ def tile_causalwaveletfieldattentionh_pa_kernel(tc, x, Wkv_words, Wkv_scales, bk
         nc.gpsimd.memset(mag_q[:], 0.0)
 
         bias_rows = setup.tile([P, P], F32, name="bias_rows")
-        nc.gpsimd.memset(bias_rows[:], 0.0)
+        nc.vector.memset(bias_rows[:], 0.0)
         coef_row = setup.tile([P, HEADS, PERIOD], F32, name="coef_row")
         nc.gpsimd.memset(coef_row[:], 0.0)
-        nc.vector.tensor_copy(out=bias_rows[0 : 2 * PAIRS, :], in_=bias_bf[:])
         bias_col = const.tile([P, 2 * PAIRS], F32, name="bias_col")
+
+        def warm(count):
+            idle = psum.tile([P, 4, P], F32, name="idle", tag="bank")
+            for n in range(count):
+                nc.tensor.matmul(
+                    out=idle[:], lhsT=ident[:], rhs=ident[:].unsqueeze(1).to_broadcast([P, 4, P]), start=True, stop=True
+                )
 
         def turn_bias():
             bias_ps = psum.tile([P, P], F32, name="bias_ps", tag="bank")
@@ -181,8 +194,10 @@ def tile_causalwaveletfieldattentionh_pa_kernel(tc, x, Wkv_words, Wkv_scales, bk
         nc.vector.tensor_copy(out=skip_f32[:], in_=skip_bf[:])
         skip_gate = const.tile([P, len(SKIPS)], F32, name="skip_gate")
         nc.scalar.activation(out=skip_gate[:], in_=skip_f32[:], func=ACT.Sigmoid)
-        first_root = setup.tile([P, 1], F32, name="first_root")
-        nc.scalar.activation(out=first_root[:], in_=gains[:, 0, 0:1], func=ACT.Sqrt, bias=skip_gate[:, 0:1])
+        def load_root_table():
+            first_root = setup.tile([P, 1], F32, name="first_root")
+            nc.scalar.activation(out=first_root[:], in_=gains[:, 0, 0:1], func=ACT.Sqrt, bias=skip_gate[:, 0:1])
+
         x_codes = const.tile([P, K_PASSES, TOKENS], U32, name="x_codes", align_bytes=64)
         x_scales = const.tile([P, K_PASSES, TOKENS], U8, name="x_scales", align_bytes=64)
 
@@ -200,27 +215,33 @@ def tile_causalwaveletfieldattentionh_pa_kernel(tc, x, Wkv_words, Wkv_scales, bk
                                 xt[:, u, P * i : P * (i + 1)], words[:, 256 * g + u : 256 * (g + 1) : 2], ident[:]
                             )
                     dest = grouped_words[:, BANK * half : BANK * (half + 1)].rearrange("p (t u) -> p t u", u=2)
-                    if half == 0:
+                    if half == 0 and g == 0:
                         nc.vector.tensor_copy(out=dest, in_=xt[:].rearrange("p u t -> p t u"))
                     else:
                         nc.scalar.copy(out=dest, in_=xt[:].rearrange("p u t -> p t u"))
                 cols = slice(BANK * j, BANK * (j + 1))
                 nc.vector.quantize_mx(out=x_codes[:, g, cols].bitcast(FP8X4), scales=x_scales[:, g, cols], in_=grouped[:])
 
-        def add_skips(rows):
+        def skip_ops(rows):
             blocks = CLASS_LEN // hop
+
+            def add_block(block, source, i):
+                nc.vector.scalar_tensor_tensor(
+                    out=rows[:, :, hop * block : hop * (block + 1)],
+                    in0=rows[:, :, hop * source : hop * (source + 1)],
+                    scalar=skip_gate[:, i : i + 1],
+                    in1=rows[:, :, hop * block : hop * (block + 1)],
+                    op0=ALU.mult,
+                    op1=ALU.add,
+                )
+
+            ops = []
             for source in range(blocks - 2, -1, -1):
                 for i in range(len(SKIPS)):
                     block = source + SKIPS[i] // SKIPS[0]
                     if block < blocks:
-                        nc.vector.scalar_tensor_tensor(
-                            out=rows[:, :, hop * block : hop * (block + 1)],
-                            in0=rows[:, :, hop * source : hop * (source + 1)],
-                            scalar=skip_gate[:, i : i + 1],
-                            in1=rows[:, :, hop * block : hop * (block + 1)],
-                            op0=ALU.mult,
-                            op1=ALU.add,
-                        )
+                        ops.append((add_block, (block, source, i)))
+            return ops
 
         out_flat = out.rearrange("o h n e -> (o h n e)")
         short_coef = const.tile([P, PAIRS, 2, short_powers], F32, name="short_coef")
@@ -258,13 +279,16 @@ def tile_causalwaveletfieldattentionh_pa_kernel(tc, x, Wkv_words, Wkv_scales, bk
                 family, m = places[shift]
                 nc.gpsimd.tensor_copy(out=coef_row[:, :, shift // STRIDE], in_=weights[:, family, m, :])
 
+        scratch = out_flat[0 : HEADS * P * PERIOD]
+
         def build_toeplitz():
-            scratch = out_flat[0 : HEADS * P * PERIOD]
             nc.sync.dma_start(out=scratch.rearrange("(h r i) -> r h i", h=HEADS, r=P), in_=coef_row[:])
+
+        def load_toeplitz():
             skewed = scratch.rearrange("(h z) -> h z", h=HEADS)[:, 0 : P * (PERIOD - 1)].rearrange("h (r w) -> r h w", r=P)
             nc.sync.dma_start(out=toeplitz[:], in_=skewed[:, :, 0:CLASS_LEN])
 
-        mag_wide, mag_ps, k_square, norm_sb, parked, mag_t, field_q, short_t, summed, result = {}, {}, {}, {}, {}, {}, {}, {}, {}, {}
+        norm_ps, mag_wide, mag_ps, k_square, norm_sb, parked, mag_t, field_q, short_t, summed, result = {}, {}, {}, {}, {}, {}, {}, {}, {}, {}, {}
 
         def passes(column_block, j):
             cols = slice(BANK * j, BANK * (j + 1))
@@ -304,7 +328,7 @@ def tile_causalwaveletfieldattentionh_pa_kernel(tc, x, Wkv_words, Wkv_scales, bk
         def key_norms(group, j):
             size = len(group)
             if j == 0:
-                norm_sb[group] = double.tile([P, TOKENS // P, 2 * size], F32, name="norm_sb")
+                norm_sb[group] = double.tile([P, 2 * size, TOKENS // P], F32, name="norm_sb")
             turned = psum.tile([P, BANK], F32, name="turned", tag="bank")
             for i in range(4):
                 for t in range(size):
@@ -316,16 +340,20 @@ def tile_causalwaveletfieldattentionh_pa_kernel(tc, x, Wkv_words, Wkv_scales, bk
                         start=(i == 0 and t == 0),
                         stop=(i == 3 and t == size - 1),
                     )
+            norm_ps[group, j] = turned
+
+        def add_channels(group, j):
+            size = len(group)
             nc.vector.tensor_reduce(
-                out=norm_sb[group][:, 4 * j : 4 * (j + 1), :].rearrange("p i h -> p (i h)"),
-                in_=turned[:].rearrange("p (i e) -> p i e", e=HEAD_DIM // size),
+                out=norm_sb[group][:, :, 4 * j : 4 * (j + 1)].rearrange("p h i -> p i h"),
+                in_=norm_ps[group, j][:].rearrange("p (i h e) -> p i h e", i=4, h=2 * size),
                 axis=AXIS.X,
                 op=ALU.add,
             )
 
         def park_mag(group):
             rows = 2 * len(group) * TOKENS // P
-            nc.scalar.activation(out=mag_q[:, 0:rows], in_=norm_sb[group][:].rearrange("p i h -> p (i h)"), func=ACT.Sqrt)
+            nc.scalar.activation(out=mag_q[:, 0:rows], in_=norm_sb[group][:].rearrange("p h t -> p (h t)"), func=ACT.Sqrt)
             turned = psum.tile([P, P], F32, name="turned", tag="bank")
             nc.tensor.transpose(turned[:], mag_q[:], ident[:])
             mag_rows = single.tile([P, P], F32, name="mag_rows")
@@ -339,8 +367,8 @@ def tile_causalwaveletfieldattentionh_pa_kernel(tc, x, Wkv_words, Wkv_scales, bk
             mag_t[pair] = double.tile([P, TOKENS], F32, name="mag_t")
             for half in range(2):
                 nc.sync.dma_start(
-                    out=mag_t[pair][HEAD_DIM * half : HEAD_DIM * (half + 1), :].rearrange("p (t q) -> p t q", q=P),
-                    in_=parked[group].rearrange("(t h q) -> h t q", h=2 * len(group), q=P)[2 * place + half].partition_broadcast(HEAD_DIM),
+                    out=mag_t[pair][HEAD_DIM * half : HEAD_DIM * (half + 1), :],
+                    in_=parked[group].rearrange("(h n) -> h n", n=TOKENS)[2 * place + half].partition_broadcast(HEAD_DIM),
                 )
 
         def wide_roots(group, j):
@@ -348,8 +376,8 @@ def tile_causalwaveletfieldattentionh_pa_kernel(tc, x, Wkv_words, Wkv_scales, bk
                 mag_wide[group] = x_pool.tile([P, 2 * TOKENS // P, HEAD_DIM], F32, name="mag_wide", tag="x_rows")
             cols = slice(2 * 4 * j, 2 * 4 * (j + 1))
             nc.scalar.activation(
-                out=mag_wide[group][:, cols, :],
-                in_=norm_sb[group][:].rearrange("p i h -> p (i h)")[:, cols].unsqueeze(2).to_broadcast([P, 2 * 4, HEAD_DIM]),
+                out=mag_wide[group][:, cols, :].rearrange("p (i h) e -> p i h e", h=2),
+                in_=norm_sb[group][:, :, 4 * j : 4 * (j + 1)].rearrange("p h i -> p i h").unsqueeze(3).to_broadcast([P, 4, 2, HEAD_DIM]),
                 func=ACT.Sqrt,
             )
 
@@ -378,24 +406,33 @@ def tile_causalwaveletfieldattentionh_pa_kernel(tc, x, Wkv_words, Wkv_scales, bk
                     in1=mag[:].rearrange("p (a q) -> p a q", q=CLASS_LEN),
                     op=ALU.mult,
                 )
-            add_skips(field_t[:, :, PAD:])
 
-        def short_shift(pair, i):
+        def field_skips(pair):
+            return skip_ops(field_tiles[pair % 3][:, :, PAD:])
+
+        def short_pieces(pair, i):
             shift = short_shifts[i]
             family, m = places[shift]
             weight = short_coef[:, pair, family, m : m + 1]
             part = i % parts(pair)
-            if i < parts(pair):
-                short_t[pair, part] = shorts.tile([P, STRIDE, CLASS_LEN], F32, name="short_t")
-            for row0, row1 in ((shift % STRIDE, STRIDE), (0, shift % STRIDE)):
-                shifted = shifted_field(field_tiles[pair % 3], shift, row0, row1)
-                rows = short_t[pair, part][:, row0:row1, :]
-                if i < parts(pair) and pair == 0:
+            first = i < parts(pair)
+            if first:
+                short_t[pair, part] = x_pool.tile([P, STRIDE, CLASS_LEN], F32, name="short_t", tag="x_rows")
+            blocks = BLOCKS if pair == PAIRS - 1 and i == len(short_shifts) - 1 else 1
+            width = CLASS_LEN // blocks
+
+            def piece(b, row0, row1):
+                shifted = shifted_field(field_tiles[pair % 3], shift, row0, row1)[:, :, width * b : width * (b + 1)]
+                rows = short_t[pair, part][:, row0:row1, width * b : width * (b + 1)]
+                if first and pair == 0:
                     nc.vector.tensor_scalar_mul(out=rows, in0=shifted, scalar1=weight)
-                elif i < parts(pair):
+                elif first:
                     nc.scalar.activation(out=rows, in_=shifted, func=ACT.Copy, scale=weight)
                 else:
                     nc.vector.scalar_tensor_tensor(out=rows, in0=shifted, scalar=weight, in1=rows, op0=ALU.mult, op1=ALU.add)
+
+            halves = ((shift % STRIDE, STRIDE), (0, shift % STRIDE))
+            return [(piece, (b, row0, row1)) for b, (row0, row1) in product(range(blocks), halves)]
 
         def turn_field(pair, j):
             if j == 0:
@@ -452,24 +489,35 @@ def tile_causalwaveletfieldattentionh_pa_kernel(tc, x, Wkv_words, Wkv_scales, bk
         def live(pair):
             return 0 <= pair < PAIRS
 
-        k_units = {-2: [((1,), j) for j in range(BANKS)], -1: [((2, 3), j) for j in range(BANKS)]}
-        for n, group in enumerate(GROUPS[3:]):
-            for j in range(BANKS):
-                k_units.setdefault(2 * n + j // 2, []).append((group, j))
+        def run(pieces, count=99):
+            for n in range(min(count, len(pieces))):
+                piece, place = pieces.pop(0)
+                piece(*place)
 
-        head = GROUPS[0]
+        def starts(pair):
+            return [piece for i in range(parts(pair)) for piece in short_pieces(pair, i)]
+
+        def rest(pair):
+            return [piece for i in range(parts(pair), len(short_shifts)) for piece in short_pieces(pair, i)]
+
+        head, second, third, late_keys = GROUPS
+        warm(2)
         quantise_bank(0)
-        turn_bias()
+        nc.vector.tensor_copy(out=bias_rows[0 : 2 * PAIRS, :], in_=bias_bf[:])
         quantise_bank(1)
+        load_root_table()
+        turn_bias()
         for j in range(BANKS):
             project_k(head, j)
-            if j + 2 < BANKS:
-                quantise_bank(j + 2)
             if j >= 1:
                 key_norms(head, j - 1)
+                add_channels(head, j - 1)
                 wide_roots(head, j - 1)
+            if j + 2 < BANKS:
+                quantise_bank(j + 2)
         project_v(0, 0)
         key_norms(head, BANKS - 1)
+        add_channels(head, BANKS - 1)
         wide_roots(head, BANKS - 1)
         project_v(0, 1)
         make_weights()
@@ -480,31 +528,75 @@ def tile_causalwaveletfieldattentionh_pa_kernel(tc, x, Wkv_words, Wkv_scales, bk
             spread_mag_by_tensor(head, j)
             if j < 2:
                 project_v(0, j + 2)
-        for i in range(-2, PAIRS + 1):
-            if live(i):
-                for t in range(parts(i)):
-                    short_shift(i, t)
+        build_toeplitz()
+        make_field(0)
+
+        skips = field_skips(0)
+        for j in range(BANKS):
+            project_k(second, j)
+            if j >= 1:
+                key_norms(second, j - 1)
+                run(skips, 1)
+                add_channels(second, j - 1)
+        key_norms(second, BANKS - 1)
+        run(skips)
+        add_channels(second, BANKS - 1)
+        run(starts(0))
+        short = rest(0)
+        for j in range(BANKS):
+            project_v(1, j)
+        park_mag(second)
+        spread_mag(1)
+        run(short, 3)
+        for j in range(BANKS):
+            project_k(third, j)
+            if j >= 1:
+                key_norms(third, j - 1)
+                run(short, 1)
+                add_channels(third, j - 1)
+        key_norms(third, BANKS - 1)
+        run(short, 1)
+        add_channels(third, BANKS - 1)
+
+        for i in range(PAIRS + 1):
+            skips = field_skips(i + 1) if live(i + 1) else []
+            fillers = starts(i + 1) if live(i + 1) else []
             if live(i + 1):
                 make_field(i + 1)
-            if live(i):
-                for t in range(parts(i), len(short_shifts)):
-                    short_shift(i, t)
-            if live(i + 2) and i + 2 > 0:
+            if i > 0:
+                short = rest(i) if live(i) else []
+            run(short, 1)
+            run(skips, 1)
+            run(short, 1)
+            run(skips)
+            if live(i + 2):
                 for j in range(BANKS):
                     project_v(i + 2, j)
-                spread_mag(i + 2)
-            units = k_units.get(i, [])
-            late = []
-            for unit in units:
-                project_k(*unit)
-                if i < 0:
-                    late.append(unit)
-                    if len(late) > 1:
-                        key_norms(*late.pop(0))
-                else:
-                    late.append(unit)
-            if i == -1:
-                build_toeplitz()
+                if i != 0 and i != 2:
+                    spread_mag(i + 2)
+            late = [(late_keys, 2 * i), (late_keys, 2 * i + 1)] if i < 2 else []
+            if late:
+                project_k(*late[0])
+            if i == 0:
+                load_toeplitz()
+                park_mag(third)
+                spread_mag(2)
+                turn_field(0, 0)
+                turn_field(0, 1)
+                key_norms(*late[0])
+                run(short, 2)
+                project_k(*late[1])
+                turn_field(0, 2)
+                run(fillers, 1)
+                turn_field(0, 3)
+                run(short)
+                add_channels(*late[0])
+                key_norms(*late[1])
+                run(fillers)
+                add_channels(*late[1])
+                continue
+            if late:
+                project_k(*late[1])
             early = live(i) and i >= EARLY
             for j in range(BANKS):
                 terms = long_sum_terms(j) if live(i - 1) and i - 1 < EARLY else []
@@ -512,21 +604,25 @@ def tile_causalwaveletfieldattentionh_pa_kernel(tc, x, Wkv_words, Wkv_scales, bk
                     long_sum(i - 1, j, half, source)
                     if n == 0 and live(i):
                         turn_field(i, j)
-                    if n == 1 and j >= 2 and late:
-                        key_norms(*late.pop(0))
-                if not terms:
-                    if live(i):
-                        turn_field(i, j)
-                    if late:
-                        key_norms(*late.pop(0))
+                if not terms and live(i):
+                    turn_field(i, j)
+                if late and j in (1, 2):
+                    key_norms(*late[j - 1])
                 if live(i - 1):
                     add_short_part_and_store(i - 1, j)
+                run(short, 2)
+                if i == 2 and j == 0:
+                    park_mag(late_keys)
+                    spread_mag(4)
+                if j >= 1:
+                    run(fillers, 1)
                 if early and j >= 1:
                     for half, source in long_sum_terms(j - 1):
                         long_sum(i, j - 1, half, source)
-            for unit in units:
-                if unit[1] == BANKS - 1:
-                    park_mag(unit[0])
+            run(short)
+            for unit in late:
+                add_channels(*unit)
+            run(fillers)
             if early:
                 for half, source in long_sum_terms(BANKS - 1):
                     long_sum(i, BANKS - 1, half, source)

@@ -42,7 +42,7 @@ GROUPS = ((0,), (1,), (2, 3), (4, 5, 6, 7))
 
 
 def parts(pair):
-    return 2 if pair >= 3 else 1
+    return 2 if pair in (3, 4, 5, 6) else 1
 
 
 def group_of(pair):
@@ -127,12 +127,12 @@ def tile_causalwaveletfieldattentionh_pa_kernel(tc, x, Wkv_words, Wkv_scales, bk
             x_rows.append(x_pool.tile([P, BLOCKS, ROWS_PER_BANK, DIM], BF16, name="x_rows"))
         for a in range(ROWS_PER_BANK):
             load_x(0, slice(a, a + 1))
+        load_x(1, slice(ROWS_PER_BANK, 2 * ROWS_PER_BANK))
         for r in range(4):
             nc.sync.dma_start(
                 out=w_scales[r:P:32, :, :].bitcast(I32), in_=Wkv_scales[:, r:16:4, :].rearrange("g q n -> q g n").bitcast(I32)
             )
         load_weight_blocks(0, 1)
-        load_x(1, slice(ROWS_PER_BANK, 2 * ROWS_PER_BANK))
         load_weight_blocks(PAIRS, PAIRS + 1)
         load_bias()
         for j in range(2, BANKS):
@@ -201,8 +201,8 @@ def tile_causalwaveletfieldattentionh_pa_kernel(tc, x, Wkv_words, Wkv_scales, bk
         x_codes = const.tile([P, K_PASSES, TOKENS], U32, name="x_codes", align_bytes=64)
         x_scales = const.tile([P, K_PASSES, TOKENS], U8, name="x_scales", align_bytes=64)
 
-        def quantise_bank(j):
-            for g in range(K_PASSES):
+        def quantise_bank(j, chosen=range(K_PASSES)):
+            for g in chosen:
                 grouped = grouped_pool.tile([P, 4 * BANK], BF16, name="grouped", align_bytes=64)
                 grouped_words = grouped[:].bitcast(F32)
                 for half in range(2):
@@ -215,7 +215,7 @@ def tile_causalwaveletfieldattentionh_pa_kernel(tc, x, Wkv_words, Wkv_scales, bk
                                 xt[:, u, P * i : P * (i + 1)], words[:, 256 * g + u : 256 * (g + 1) : 2], ident[:]
                             )
                     dest = grouped_words[:, BANK * half : BANK * (half + 1)].rearrange("p (t u) -> p t u", u=2)
-                    if half == 0 and g == 0:
+                    if g == 0:
                         nc.vector.tensor_copy(out=dest, in_=xt[:].rearrange("p u t -> p t u"))
                     else:
                         nc.scalar.copy(out=dest, in_=xt[:].rearrange("p u t -> p t u"))
@@ -351,9 +351,12 @@ def tile_causalwaveletfieldattentionh_pa_kernel(tc, x, Wkv_words, Wkv_scales, bk
                 op=ALU.add,
             )
 
-        def park_mag(group):
+        def take_roots(group):
             rows = 2 * len(group) * TOKENS // P
             nc.scalar.activation(out=mag_q[:, 0:rows], in_=norm_sb[group][:].rearrange("p h t -> p (h t)"), func=ACT.Sqrt)
+
+        def park_mag(group):
+            rows = 2 * len(group) * TOKENS // P
             turned = psum.tile([P, P], F32, name="turned", tag="bank")
             nc.tensor.transpose(turned[:], mag_q[:], ident[:])
             mag_rows = single.tile([P, P], F32, name="mag_rows")
@@ -479,12 +482,19 @@ def tile_causalwaveletfieldattentionh_pa_kernel(tc, x, Wkv_words, Wkv_scales, bk
                         start=False,
                         stop=(part == parts(pair) - 1 and i == 3),
                     )
-            nc.scalar.copy(
-                out=result[pair][:, b, :, 4 * group : 4 * group + 4, :], in_=summed[pair, j][:].rearrange("p a h e -> p h a e")
-            )
-            if group == STRIDE // 4 - 1:
-                out_view = out[0, 2 * pair : 2 * pair + 2].rearrange("h (b p a) e -> b p h (a e)", b=BLOCKS, p=P, a=STRIDE)
-                nc.sync.dma_start(out=out_view[b], in_=result[pair][:, b].rearrange("p h a e -> p h (a e)"))
+            copy = nc.vector.tensor_copy if pair == PAIRS - 1 and group == 0 else nc.scalar.copy
+            copy(out=result[pair][:, b, :, 4 * group : 4 * group + 4, :], in_=summed[pair, j][:].rearrange("p a h e -> p h a e"))
+            out_view = out[0, 2 * pair : 2 * pair + 2].rearrange("h (b p a) e -> b p h (a e)", b=BLOCKS, p=P, a=STRIDE)
+            classes = slice(0, 0)
+            if pair == PAIRS - 1 and b == BLOCKS - 1:
+                classes = slice(4 * group, 4 * group + 4)
+            elif group == STRIDE // 4 - 1:
+                classes = slice(0, STRIDE)
+            if classes.stop:
+                nc.sync.dma_start(
+                    out=out_view[b][:, :, HEAD_DIM * classes.start : HEAD_DIM * classes.stop],
+                    in_=result[pair][:, b, :, classes, :].rearrange("p h a e -> p h (a e)"),
+                )
 
         def live(pair):
             return 0 <= pair < PAIRS
@@ -501,12 +511,15 @@ def tile_causalwaveletfieldattentionh_pa_kernel(tc, x, Wkv_words, Wkv_scales, bk
             return [piece for i in range(parts(pair), len(short_shifts)) for piece in short_pieces(pair, i)]
 
         head, second, third, late_keys = GROUPS
+        load_root_table()
         warm(2)
         quantise_bank(0)
         nc.vector.tensor_copy(out=bias_rows[0 : 2 * PAIRS, :], in_=bias_bf[:])
         quantise_bank(1)
-        load_root_table()
         turn_bias()
+        for group in GROUPS:
+            if len(group) > 1:
+                fold_weights(group)
         for j in range(BANKS):
             project_k(head, j)
             if j >= 1:
@@ -514,20 +527,17 @@ def tile_causalwaveletfieldattentionh_pa_kernel(tc, x, Wkv_words, Wkv_scales, bk
                 add_channels(head, j - 1)
                 wide_roots(head, j - 1)
             if j + 2 < BANKS:
-                quantise_bank(j + 2)
-        project_v(0, 0)
+                quantise_bank(j + 2, [0])
+                project_v(0, j)
+                quantise_bank(j + 2, [1])
+        project_v(0, 2)
         key_norms(head, BANKS - 1)
         add_channels(head, BANKS - 1)
         wide_roots(head, BANKS - 1)
-        project_v(0, 1)
+        project_v(0, 3)
         make_weights()
-        for group in GROUPS:
-            if len(group) > 1:
-                fold_weights(group)
         for j in range(BANKS):
             spread_mag_by_tensor(head, j)
-            if j < 2:
-                project_v(0, j + 2)
         build_toeplitz()
         make_field(0)
 
@@ -544,6 +554,8 @@ def tile_causalwaveletfieldattentionh_pa_kernel(tc, x, Wkv_words, Wkv_scales, bk
         run(starts(0))
         short = rest(0)
         for j in range(BANKS):
+            if j == 2:
+                take_roots(second)
             project_v(1, j)
         park_mag(second)
         spread_mag(1)
@@ -558,6 +570,7 @@ def tile_causalwaveletfieldattentionh_pa_kernel(tc, x, Wkv_words, Wkv_scales, bk
         run(short, 1)
         add_channels(third, BANKS - 1)
 
+        pending = []
         for i in range(PAIRS + 1):
             skips = field_skips(i + 1) if live(i + 1) else []
             fillers = starts(i + 1) if live(i + 1) else []
@@ -569,18 +582,24 @@ def tile_causalwaveletfieldattentionh_pa_kernel(tc, x, Wkv_words, Wkv_scales, bk
             run(skips, 1)
             run(short, 1)
             run(skips)
+            for unit in pending:
+                add_channels(*unit)
+            pending = []
             if live(i + 2):
                 for j in range(BANKS):
                     project_v(i + 2, j)
-                if i != 0 and i != 2:
+                if i == 2:
+                    take_roots(late_keys)
+                if i == 0:
+                    take_roots(third)
+                    park_mag(third)
+                if i != 2:
                     spread_mag(i + 2)
             late = [(late_keys, 2 * i), (late_keys, 2 * i + 1)] if i < 2 else []
             if late:
                 project_k(*late[0])
             if i == 0:
                 load_toeplitz()
-                park_mag(third)
-                spread_mag(2)
                 turn_field(0, 0)
                 turn_field(0, 1)
                 key_norms(*late[0])
@@ -593,7 +612,7 @@ def tile_causalwaveletfieldattentionh_pa_kernel(tc, x, Wkv_words, Wkv_scales, bk
                 add_channels(*late[0])
                 key_norms(*late[1])
                 run(fillers)
-                add_channels(*late[1])
+                pending = late[1:]
                 continue
             if late:
                 project_k(*late[1])
@@ -614,7 +633,7 @@ def tile_causalwaveletfieldattentionh_pa_kernel(tc, x, Wkv_words, Wkv_scales, bk
                 if i == 2 and j == 0:
                     park_mag(late_keys)
                     spread_mag(4)
-                if j >= 1:
+                if j >= 2:
                     run(fillers, 1)
                 if early and j >= 1:
                     for half, source in long_sum_terms(j - 1):

@@ -24,6 +24,7 @@ PAIRS = HEADS // 2
 SCALES = 10
 D4 = (0.4829629131445341, 0.8365163037378079, 0.2241438680420134, -0.1294095225512604)
 SKIPS = (512, 1024)
+EXP_LIMIT = 80.0
 K_PASS = 512
 K_PASSES = DIM // K_PASS
 BANK = 512
@@ -191,12 +192,13 @@ def tile_causalwaveletfieldattentionh_pa_kernel(tc, x, Wkv_words, Wkv_scales, bk
         )
         nc.scalar.activation(out=gains[:], in_=gains[:], func=ACT.Exp)
         skip_f32 = setup.tile([P, len(SKIPS)], F32, name="skip_f32")
-        nc.vector.tensor_copy(out=skip_f32[:], in_=skip_bf[:])
+        nc.vector.tensor_scalar(out=skip_f32[:], in0=skip_bf[:], scalar1=-1.0, scalar2=EXP_LIMIT, op0=ALU.mult, op1=ALU.min)
+        skip_exp = setup.tile([P, len(SKIPS)], F32, name="skip_exp")
+        nc.scalar.activation(out=skip_exp[:], in_=skip_f32[:], func=ACT.Exp)
         skip_gate = const.tile([P, len(SKIPS)], F32, name="skip_gate")
-        nc.scalar.activation(out=skip_gate[:], in_=skip_f32[:], func=ACT.Sigmoid)
         def load_root_table():
             first_root = setup.tile([P, 1], F32, name="first_root")
-            nc.scalar.activation(out=first_root[:], in_=gains[:, 0, 0:1], func=ACT.Sqrt, bias=skip_gate[:, 0:1])
+            nc.scalar.activation(out=first_root[:], in_=gains[:, 0, 0:1], func=ACT.Sqrt, bias=skip_exp[:, 0:1])
 
         x_codes = const.tile([P, K_PASSES, TOKENS], U32, name="x_codes", align_bytes=64)
         x_scales = const.tile([P, K_PASSES, TOKENS], U8, name="x_scales", align_bytes=64)
@@ -247,15 +249,22 @@ def tile_causalwaveletfieldattentionh_pa_kernel(tc, x, Wkv_words, Wkv_scales, bk
         short_coef = const.tile([P, PAIRS, 2, short_powers], F32, name="short_coef")
         toeplitz = const.tile([P, HEADS, CLASS_LEN], F32, name="toeplitz")
 
-        def make_weights():
-            total = setup.tile([P, HEADS], F32, name="total")
+        weights = setup.tile([P, 2, SCALES + 1, HEADS], F32, name="weights")
+        total = setup.tile([P, HEADS], F32, name="total")
+        inverse = setup.tile([P, HEADS], F32, name="inverse")
+
+        def weigh_skips():
             nc.vector.tensor_reduce(out=total[:], in_=gains[:].rearrange("p j h -> p h j"), axis=AXIS.X, op=ALU.add)
-            inverse = setup.tile([P, HEADS], F32, name="inverse")
+            nc.vector.tensor_scalar(out=skip_exp[:], in0=skip_exp[:], scalar1=1.0, scalar2=None, op0=ALU.add)
             nc.vector.reciprocal(out=inverse[:], in_=total[:])
+            nc.vector.reciprocal(out=skip_gate[:], in_=skip_exp[:])
+
+        def divide_gains():
             nc.vector.tensor_tensor(
                 out=gains[:], in0=gains[:], in1=inverse[:].unsqueeze(1).to_broadcast([P, SCALES, HEADS]), op=ALU.mult
             )
-            weights = setup.tile([P, 2, SCALES + 1, HEADS], F32, name="weights")
+
+        def weigh_taps():
             nc.vector.tensor_scalar_mul(out=weights[:, 0, 0:SCALES, :], in0=gains[:], scalar1=D4[2])
             nc.vector.tensor_scalar_mul(out=weights[:, 1, 0:SCALES, :], in0=gains[:], scalar1=D4[0])
             nc.vector.tensor_scalar_mul(out=weights[:, 0, SCALES, :], in0=gains[:, SCALES - 1, :], scalar1=D4[1])
@@ -267,13 +276,15 @@ def tile_causalwaveletfieldattentionh_pa_kernel(tc, x, Wkv_words, Wkv_scales, bk
                 op0=ALU.mult,
                 op1=ALU.add,
             )
+            nc.vector.tensor_scalar(
+                out=weights[:, 1, SCALES, :], in0=gains[:, 0, :], scalar1=0.0, scalar2=D4[3], op0=ALU.mult, op1=ALU.add
+            )
+
+        def place_weights():
             for half in range(2):
                 rows = slice(HEAD_DIM * half, HEAD_DIM * (half + 1))
                 by_pair = weights[rows, :, 0:short_powers, :].rearrange("p f m (c w) -> p c f m w", w=2)
                 nc.vector.tensor_copy(out=short_coef[rows], in_=by_pair[:, :, :, :, half])
-            gain_sum = setup.tile([P, HEADS], F32, name="gain_sum")
-            nc.vector.tensor_reduce(out=gain_sum[:], in_=gains[:].rearrange("p j h -> p h j"), axis=AXIS.X, op=ALU.add)
-            nc.vector.tensor_scalar_mul(out=weights[:, 1, SCALES, :], in0=gain_sum[:], scalar1=D4[3])
             nc.gpsimd.tensor_copy(out=coef_row[:, :, 0], in_=weights[:, 1, SCALES, :])
             for shift in long_shifts:
                 family, m = places[shift]
@@ -398,17 +409,20 @@ def tile_causalwaveletfieldattentionh_pa_kernel(tc, x, Wkv_words, Wkv_scales, bk
                 source, back = row0 - residue + STRIDE, steps + 1
             return field_t[:, source : source + row1 - row0, PAD - back : PAD - back + CLASS_LEN]
 
-        def make_field(pair):
+        def multiply(pair, rows, mag):
             field_t = field_tiles[pair % 3]
-            for j in range(BANKS if pair == 0 else 1):
-                rows = slice(ROWS_PER_BANK * j, ROWS_PER_BANK * (j + 1)) if pair == 0 else slice(0, STRIDE)
-                mag = mag_ps[(0,), j] if pair == 0 else mag_t[pair]
-                nc.vector.tensor_tensor(
-                    out=field_t[:, rows, PAD:],
-                    in0=field_t[:, rows, PAD:],
-                    in1=mag[:].rearrange("p (a q) -> p a q", q=CLASS_LEN),
-                    op=ALU.mult,
-                )
+            nc.vector.tensor_tensor(
+                out=field_t[:, rows, PAD:],
+                in0=field_t[:, rows, PAD:],
+                in1=mag[:].rearrange("p (a q) -> p a q", q=CLASS_LEN),
+                op=ALU.mult,
+            )
+
+        def make_field(pair):
+            multiply(pair, slice(0, STRIDE), mag_t[pair])
+
+        def make_first_field(j):
+            multiply(0, slice(ROWS_PER_BANK * j, ROWS_PER_BANK * (j + 1)), mag_ps[GROUPS[0], j])
 
         def field_skips(pair):
             return skip_ops(field_tiles[pair % 3][:, :, PAD:])
@@ -427,9 +441,7 @@ def tile_causalwaveletfieldattentionh_pa_kernel(tc, x, Wkv_words, Wkv_scales, bk
             def piece(b, row0, row1):
                 shifted = shifted_field(field_tiles[pair % 3], shift, row0, row1)[:, :, width * b : width * (b + 1)]
                 rows = short_t[pair, part][:, row0:row1, width * b : width * (b + 1)]
-                if first and pair == 0:
-                    nc.vector.tensor_scalar_mul(out=rows, in0=shifted, scalar1=weight)
-                elif first:
+                if first:
                     nc.scalar.activation(out=rows, in_=shifted, func=ACT.Copy, scale=weight)
                 else:
                     nc.vector.scalar_tensor_tensor(out=rows, in0=shifted, scalar=weight, in1=rows, op0=ALU.mult, op1=ALU.add)
@@ -512,11 +524,13 @@ def tile_causalwaveletfieldattentionh_pa_kernel(tc, x, Wkv_words, Wkv_scales, bk
 
         head, second, third, late_keys = GROUPS
         load_root_table()
-        warm(2)
+        warm(1)
         quantise_bank(0)
         nc.vector.tensor_copy(out=bias_rows[0 : 2 * PAIRS, :], in_=bias_bf[:])
-        quantise_bank(1)
+        quantise_bank(1, [0])
         turn_bias()
+        quantise_bank(1, [1])
+        weigh_skips()
         for group in GROUPS:
             if len(group) > 1:
                 fold_weights(group)
@@ -526,32 +540,41 @@ def tile_causalwaveletfieldattentionh_pa_kernel(tc, x, Wkv_words, Wkv_scales, bk
                 key_norms(head, j - 1)
                 add_channels(head, j - 1)
                 wide_roots(head, j - 1)
+            if j >= 2:
+                spread_mag_by_tensor(head, j - 2)
+                make_first_field(j - 2)
             if j + 2 < BANKS:
                 quantise_bank(j + 2, [0])
+                if j == 0:
+                    divide_gains()
+                else:
+                    place_weights()
                 project_v(0, j)
                 quantise_bank(j + 2, [1])
+                if j == 0:
+                    weigh_taps()
+                else:
+                    build_toeplitz()
         project_v(0, 2)
         key_norms(head, BANKS - 1)
         add_channels(head, BANKS - 1)
         wide_roots(head, BANKS - 1)
         project_v(0, 3)
-        make_weights()
-        for j in range(BANKS):
+        for j in range(2, BANKS):
             spread_mag_by_tensor(head, j)
-        build_toeplitz()
-        make_field(0)
+            make_first_field(j)
 
         skips = field_skips(0)
         for j in range(BANKS):
             project_k(second, j)
+            run(skips, 2)
             if j >= 1:
                 key_norms(second, j - 1)
-                run(skips, 1)
-                add_channels(second, j - 1)
-        key_norms(second, BANKS - 1)
-        run(skips)
-        add_channels(second, BANKS - 1)
         run(starts(0))
+        for j in range(BANKS - 1):
+            add_channels(second, j)
+        key_norms(second, BANKS - 1)
+        add_channels(second, BANKS - 1)
         short = rest(0)
         for j in range(BANKS):
             if j == 2:

@@ -43,7 +43,7 @@ GROUPS = ((0,), (1,), (2, 3), (4, 5, 6, 7))
 
 
 def parts(pair):
-    return 2 if pair in (3, 4, 5, 6) else 1
+    return 2 if 2 <= pair <= 6 else 1
 
 
 def group_of(pair):
@@ -527,9 +527,8 @@ def tile_causalwaveletfieldattentionh_pa_kernel(tc, x, Wkv_words, Wkv_scales, bk
         warm(1)
         quantise_bank(0)
         nc.vector.tensor_copy(out=bias_rows[0 : 2 * PAIRS, :], in_=bias_bf[:])
-        quantise_bank(1, [0])
+        quantise_bank(1)
         turn_bias()
-        quantise_bank(1, [1])
         weigh_skips()
         for group in GROUPS:
             if len(group) > 1:
@@ -576,19 +575,21 @@ def tile_causalwaveletfieldattentionh_pa_kernel(tc, x, Wkv_words, Wkv_scales, bk
         key_norms(second, BANKS - 1)
         add_channels(second, BANKS - 1)
         short = rest(0)
-        for j in range(BANKS):
-            if j == 2:
-                take_roots(second)
-            project_v(1, j)
-        park_mag(second)
-        spread_mag(1)
-        run(short, 3)
+        run(short, 2)
         for j in range(BANKS):
             project_k(third, j)
+            if j == 0:
+                take_roots(second)
+            if j == 1:
+                park_mag(second)
+                spread_mag(1)
             if j >= 1:
                 key_norms(third, j - 1)
                 run(short, 1)
                 add_channels(third, j - 1)
+            if j >= 2:
+                project_v(1, 2 * j - 4)
+                project_v(1, 2 * j - 3)
         key_norms(third, BANKS - 1)
         run(short, 1)
         add_channels(third, BANKS - 1)
@@ -608,15 +609,17 @@ def tile_causalwaveletfieldattentionh_pa_kernel(tc, x, Wkv_words, Wkv_scales, bk
             for unit in pending:
                 add_channels(*unit)
             pending = []
+            if i == 0:
+                take_roots(third)
+            if i == 2:
+                take_roots(late_keys)
             if live(i + 2):
                 for j in range(BANKS):
                     project_v(i + 2, j)
-                if i == 2:
-                    take_roots(late_keys)
-                if i == 0:
-                    take_roots(third)
-                    park_mag(third)
-                if i != 2:
+                    if i == 0 and j == 1:
+                        park_mag(third)
+                        spread_mag(2)
+                if i != 0 and i != 2:
                     spread_mag(i + 2)
             late = [(late_keys, 2 * i), (late_keys, 2 * i + 1)] if i < 2 else []
             if late:

@@ -172,10 +172,10 @@ def tile_causalwaveletfieldattentionh_pa_kernel(tc, x, Wkv_words, Wkv_scales, bk
         bias_col = const.tile([P, 2 * PAIRS], F32, name="bias_col")
 
         def warm(count):
-            idle = psum.tile([P, 4, P], F32, name="idle", tag="bank")
+            idle = psum.tile([P, 2, P], F32, name="idle", tag="bank")
             for n in range(count):
                 nc.tensor.matmul(
-                    out=idle[:], lhsT=ident[:], rhs=ident[:].unsqueeze(1).to_broadcast([P, 4, P]), start=True, stop=True
+                    out=idle[:], lhsT=ident[:], rhs=ident[:].unsqueeze(1).to_broadcast([P, 2, P]), start=True, stop=True
                 )
 
         def turn_bias():
@@ -524,10 +524,14 @@ def tile_causalwaveletfieldattentionh_pa_kernel(tc, x, Wkv_words, Wkv_scales, bk
 
         head, second, third, late_keys = GROUPS
         load_root_table()
+        warm(4)
+        quantise_bank(0, [0])
         warm(1)
-        quantise_bank(0)
+        quantise_bank(0, [1])
+        warm(1)
         nc.vector.tensor_copy(out=bias_rows[0 : 2 * PAIRS, :], in_=bias_bf[:])
-        quantise_bank(1)
+        quantise_bank(1, [0])
+        quantise_bank(1, [1])
         turn_bias()
         weigh_skips()
         for group in GROUPS:

@@ -43,7 +43,7 @@ GROUPS = ((0,), (1,), (2, 3), (4, 5, 6, 7))
 
 
 def parts(pair):
-    return 2 if 2 <= pair <= 6 else 1
+    return 2 if 3 <= pair <= 6 else 1
 
 
 def group_of(pair):

from contextlib import ExitStack
from itertools import product

import concourse.mybir as mybir
from concourse.masks import make_identity

F32 = mybir.dt.float32
BF16 = mybir.dt.bfloat16
I32 = mybir.dt.int32
U32 = mybir.dt.uint32
U8 = mybir.dt.uint8
FP8X4 = mybir.dt.float8_e4m3fn_x4
FP4X4 = mybir.dt.float4_e2m1fn_x4
ALU = mybir.AluOpType
ACT = mybir.ActivationFunctionType
AXIS = mybir.AxisListType

P = 128
TOKENS = 2048
DIM = 1024
HEADS = 16
HEAD_DIM = 64
PAIRS = HEADS // 2
SCALES = 10
D4 = (0.4829629131445341, 0.8365163037378079, 0.2241438680420134, -0.1294095225512604)
SKIPS = (512, 1024)
EXP_LIMIT = 80.0
K_PASS = 512
K_PASSES = DIM // K_PASS
BANK = 512

STRIDE = 8
CLASS_LEN = TOKENS // STRIDE
BLOCKS = CLASS_LEN // P
ROWS_PER_BANK = BANK // CLASS_LEN
BANKS = TOKENS // BANK
PAD = 8
PERIOD = CLASS_LEN + P
EARLY = 5


GROUPS = ((0,), (1,), (2, 3), (4, 5, 6, 7))


def parts(pair):
    return 2 if 3 <= pair <= 6 else 1


def group_of(pair):
    for group in GROUPS:
        if pair in group:
            return group, group.index(pair)


FLOPS = 2 * TOKENS * DIM * 2 * DIM


def tap_places():
    places = {}
    for m in range(SCALES + 1):
        places[2**m] = (0, m)
    for m in range(SCALES):
        places[3 * 2**m] = (1, m)
    return places


def tile_causalwaveletfieldattentionh_pa_kernel(tc, x, Wkv_words, Wkv_scales, bkv, scale_gain, skip_w, out):
    nc = tc.nc
    places = tap_places()
    long_shifts = [s for s in sorted(places) if s % STRIDE == 0]
    short_shifts = sorted([s for s in places if s % STRIDE != 0], key=lambda s: (s % STRIDE, s))
    short_powers = 1 + max(places[s][1] for s in short_shifts)
    hop = SKIPS[0] // STRIDE

    first_folded = min(group[0] for group in GROUPS if len(group) > 1)

    with ExitStack() as ctx:
        const = ctx.enter_context(tc.tile_pool(name="const", bufs=1))
        setup = ctx.enter_context(tc.tile_pool(name="setup", bufs=1))
        x_pool = ctx.enter_context(tc.tile_pool(name="x_pool", bufs=2 * BANKS - 1))
        grouped_pool = ctx.enter_context(tc.tile_pool(name="grouped_pool", bufs=2))
        single = ctx.enter_context(tc.tile_pool(name="single", bufs=1))
        squares = ctx.enter_context(tc.tile_pool(name="squares", bufs=2))
        double = ctx.enter_context(tc.tile_pool(name="double", bufs=2))
        psum = ctx.enter_context(tc.psum_pool(name="psum", bufs=8))
        ctx.enter_context(tc.manual_schedule())

        ident = const.tile([P, P], F32, name="ident")
        make_identity(nc, ident[:])

        gain_bf = setup.tile([P, SCALES * HEADS], BF16, name="gain_bf")
        nc.scalar.dma_start(out=gain_bf[:], in_=scale_gain.rearrange("j h -> (j h)").partition_broadcast(P))
        skip_bf = setup.tile([P, len(SKIPS)], BF16, name="skip_bf")
        nc.scalar.dma_start(out=skip_bf[:], in_=skip_w.partition_broadcast(P))
        bias_bf = setup.tile([2 * PAIRS, P], BF16, name="bias_bf")
        bias_view = bkv.rearrange("(t c) -> t c", c=P)

        def load_bias():
            nc.sync.dma_start(out=bias_bf[0:first_folded, :], in_=bias_view[0:first_folded, :])
            nc.sync.dma_start(out=bias_bf[PAIRS : 2 * PAIRS, :], in_=bias_view[PAIRS : 2 * PAIRS, :])
            for group in GROUPS:
                if len(group) > 1:
                    channels = bkv[P * group[0] : P * (group[-1] + 1)]
                    nc.sync.dma_start(
                        out=bias_bf[group[0] : group[-1] + 1, :].rearrange("t (h w) -> t h w", h=2 * len(group)),
                        in_=channels.rearrange("(h t w) -> t h w", h=2 * len(group), t=len(group)),
                    )

        w_scales = const.tile([P, K_PASSES, 2 * DIM], U8, name="w_scales", align_bytes=64)
        nc.vector.memset(w_scales[:].bitcast(I32), 0)
        first_exp = setup.tile([P, 1], F32, name="first_exp")
        nc.vector.memset(first_exp[:], 0.0)
        nc.scalar.activation(out=first_exp[:], in_=first_exp[:], func=ACT.Exp)

        x_view = x.flatten_outer_dims().rearrange("(b p a) k -> p b a k", b=BLOCKS, p=P, a=STRIDE)
        x_rows = []
        w_words = const.tile([P, K_PASSES, 4 * DIM], U8, name="w_words", align_bytes=64)

        def load_weight_blocks(first, last):
            for g in range(K_PASSES):
                columns = slice(2 * P * first, 2 * P * last)
                nc.sync.dma_start(out=w_words[:, g, columns].bitcast(I32), in_=Wkv_words[g, :, columns].bitcast(I32))

        def load_x(j, classes):
            nc.sync.dma_start(out=x_rows[j][:, :, classes.start - ROWS_PER_BANK * j : classes.stop - ROWS_PER_BANK * j, :], in_=x_view[:, :, classes, :])

        for j in range(BANKS):
            x_rows.append(x_pool.tile([P, BLOCKS, ROWS_PER_BANK, DIM], BF16, name="x_rows"))
        for a in range(ROWS_PER_BANK):
            load_x(0, slice(a, a + 1))
        load_x(1, slice(ROWS_PER_BANK, 2 * ROWS_PER_BANK))
        for r in range(4):
            nc.sync.dma_start(
                out=w_scales[r:P:32, :, :].bitcast(I32), in_=Wkv_scales[:, r:16:4, :].rearrange("g q n -> q g n").bitcast(I32)
            )
        load_weight_blocks(0, 1)
        load_weight_blocks(PAIRS, PAIRS + 1)
        load_bias()
        for j in range(2, BANKS):
            load_x(j, slice(ROWS_PER_BANK * j, ROWS_PER_BANK * (j + 1)))
        load_weight_blocks(1, PAIRS)
        load_weight_blocks(PAIRS + 1, 2 * PAIRS)

        folded_words = const.tile([P, K_PASSES, 2 * P * (PAIRS - first_folded)], U8, name="folded_words", align_bytes=64)
        folded_scales = const.tile([P, K_PASSES, P * (PAIRS - first_folded)], U8, name="folded_scales", align_bytes=64)

        def fold_weights(group):
            size = len(group)
            for g in range(K_PASSES):
                for width, source, target in ((2, w_words, folded_words), (1, w_scales, folded_scales)):
                    start = width * P * group[0]
                    shift = width * P * first_folded
                    length = width * P * size
                    nc.gpsimd.tensor_copy(
                        out=target[:, g, start - shift : start - shift + length].bitcast(U32).rearrange("p (t h w) -> p t h w", t=size, h=2 * size),
                        in_=source[:, g, start : start + length].bitcast(U32).rearrange("p (h t w) -> p t h w", t=size, h=2 * size),
                    )

        field_tiles = []
        for i in range(3):
            field_tile = const.tile([P, STRIDE, PAD + CLASS_LEN], F32, name="field_t%d" % i)
            nc.gpsimd.memset(field_tile[:, :, 0:PAD], 0.0)
            field_tiles.append(field_tile)

        mag_q = const.tile([P, P], F32, name="mag_q")
        nc.gpsimd.memset(mag_q[:], 0.0)

        bias_rows = setup.tile([P, P], F32, name="bias_rows")
        nc.vector.memset(bias_rows[:], 0.0)
        coef_row = setup.tile([P, HEADS, PERIOD], F32, name="coef_row")
        nc.gpsimd.memset(coef_row[:], 0.0)
        bias_col = const.tile([P, 2 * PAIRS], F32, name="bias_col")

        def warm(count):
            idle = psum.tile([P, 2, P], F32, name="idle", tag="bank")
            for n in range(count):
                nc.tensor.matmul(
                    out=idle[:], lhsT=ident[:], rhs=ident[:].unsqueeze(1).to_broadcast([P, 2, P]), start=True, stop=True
                )

        def turn_bias():
            bias_ps = psum.tile([P, P], F32, name="bias_ps", tag="bank")
            nc.tensor.transpose(bias_ps[:], bias_rows[:], ident[:])
            nc.vector.tensor_copy(out=bias_col[:], in_=bias_ps[:, 0 : 2 * PAIRS])

        gains = setup.tile([P, SCALES, HEADS], F32, name="gains")
        nc.vector.tensor_copy(out=gains[:].rearrange("p j h -> p (j h)"), in_=gain_bf[:])
        top = setup.tile([P, HEADS], F32, name="top")
        nc.vector.tensor_reduce(out=top[:], in_=gains[:].rearrange("p j h -> p h j"), axis=AXIS.X, op=ALU.max)
        nc.vector.tensor_tensor(
            out=gains[:], in0=gains[:], in1=top[:].unsqueeze(1).to_broadcast([P, SCALES, HEADS]), op=ALU.subtract
        )
        nc.scalar.activation(out=gains[:], in_=gains[:], func=ACT.Exp)
        skip_f32 = setup.tile([P, len(SKIPS)], F32, name="skip_f32")
        nc.vector.tensor_scalar(out=skip_f32[:], in0=skip_bf[:], scalar1=-1.0, scalar2=EXP_LIMIT, op0=ALU.mult, op1=ALU.min)
        skip_exp = setup.tile([P, len(SKIPS)], F32, name="skip_exp")
        nc.scalar.activation(out=skip_exp[:], in_=skip_f32[:], func=ACT.Exp)
        skip_gate = const.tile([P, len(SKIPS)], F32, name="skip_gate")
        def load_root_table():
            first_root = setup.tile([P, 1], F32, name="first_root")
            nc.scalar.activation(out=first_root[:], in_=gains[:, 0, 0:1], func=ACT.Sqrt, bias=skip_exp[:, 0:1])

        x_codes = const.tile([P, K_PASSES, TOKENS], U32, name="x_codes", align_bytes=64)
        x_scales = const.tile([P, K_PASSES, TOKENS], U8, name="x_scales", align_bytes=64)

        def quantise_bank(j, chosen=range(K_PASSES)):
            for g in chosen:
                grouped = grouped_pool.tile([P, 4 * BANK], BF16, name="grouped", align_bytes=64)
                grouped_words = grouped[:].bitcast(F32)
                for half in range(2):
                    xt = psum.tile([P, 2, BANK // 2], F32, name="xt", tag="bank")
                    for i in range(2):
                        a_local, b = divmod(2 * half + i, BLOCKS)
                        words = x_rows[j][:, b, a_local, :].bitcast(F32)
                        for u in range(2):
                            nc.tensor.transpose(
                                xt[:, u, P * i : P * (i + 1)], words[:, 256 * g + u : 256 * (g + 1) : 2], ident[:]
                            )
                    dest = grouped_words[:, BANK * half : BANK * (half + 1)].rearrange("p (t u) -> p t u", u=2)
                    if g == 0:
                        nc.vector.tensor_copy(out=dest, in_=xt[:].rearrange("p u t -> p t u"))
                    else:
                        nc.scalar.copy(out=dest, in_=xt[:].rearrange("p u t -> p t u"))
                cols = slice(BANK * j, BANK * (j + 1))
                nc.vector.quantize_mx(out=x_codes[:, g, cols].bitcast(FP8X4), scales=x_scales[:, g, cols], in_=grouped[:])

        def skip_ops(rows):
            blocks = CLASS_LEN // hop

            def add_block(block, source, i):
                nc.vector.scalar_tensor_tensor(
                    out=rows[:, :, hop * block : hop * (block + 1)],
                    in0=rows[:, :, hop * source : hop * (source + 1)],
                    scalar=skip_gate[:, i : i + 1],
                    in1=rows[:, :, hop * block : hop * (block + 1)],
                    op0=ALU.mult,
                    op1=ALU.add,
                )

            ops = []
            for source in range(blocks - 2, -1, -1):
                for i in range(len(SKIPS)):
                    block = source + SKIPS[i] // SKIPS[0]
                    if block < blocks:
                        ops.append((add_block, (block, source, i)))
            return ops

        out_flat = out.rearrange("o h n e -> (o h n e)")
        short_coef = const.tile([P, PAIRS, 2, short_powers], F32, name="short_coef")
        toeplitz = const.tile([P, HEADS, CLASS_LEN], F32, name="toeplitz")

        weights = setup.tile([P, 2, SCALES + 1, HEADS], F32, name="weights")
        total = setup.tile([P, HEADS], F32, name="total")
        inverse = setup.tile([P, HEADS], F32, name="inverse")

        def weigh_skips():
            nc.vector.tensor_reduce(out=total[:], in_=gains[:].rearrange("p j h -> p h j"), axis=AXIS.X, op=ALU.add)
            nc.vector.tensor_scalar(out=skip_exp[:], in0=skip_exp[:], scalar1=1.0, scalar2=None, op0=ALU.add)
            nc.vector.reciprocal(out=inverse[:], in_=total[:])
            nc.vector.reciprocal(out=skip_gate[:], in_=skip_exp[:])

        def divide_gains():
            nc.vector.tensor_tensor(
                out=gains[:], in0=gains[:], in1=inverse[:].unsqueeze(1).to_broadcast([P, SCALES, HEADS]), op=ALU.mult
            )

        def weigh_taps():
            nc.vector.tensor_scalar_mul(out=weights[:, 0, 0:SCALES, :], in0=gains[:], scalar1=D4[2])
            nc.vector.tensor_scalar_mul(out=weights[:, 1, 0:SCALES, :], in0=gains[:], scalar1=D4[0])
            nc.vector.tensor_scalar_mul(out=weights[:, 0, SCALES, :], in0=gains[:, SCALES - 1, :], scalar1=D4[1])
            nc.vector.scalar_tensor_tensor(
                out=weights[:, 0, 1:SCALES, :],
                in0=gains[:, 0 : SCALES - 1, :],
                scalar=D4[1],
                in1=weights[:, 0, 1:SCALES, :],
                op0=ALU.mult,
                op1=ALU.add,
            )
            nc.vector.tensor_scalar(
                out=weights[:, 1, SCALES, :], in0=gains[:, 0, :], scalar1=0.0, scalar2=D4[3], op0=ALU.mult, op1=ALU.add
            )

        def place_weights():
            for half in range(2):
                rows = slice(HEAD_DIM * half, HEAD_DIM * (half + 1))
                by_pair = weights[rows, :, 0:short_powers, :].rearrange("p f m (c w) -> p c f m w", w=2)
                nc.vector.tensor_copy(out=short_coef[rows], in_=by_pair[:, :, :, :, half])
            nc.gpsimd.tensor_copy(out=coef_row[:, :, 0], in_=weights[:, 1, SCALES, :])
            for shift in long_shifts:
                family, m = places[shift]
                nc.gpsimd.tensor_copy(out=coef_row[:, :, shift // STRIDE], in_=weights[:, family, m, :])

        scratch = out_flat[0 : HEADS * P * PERIOD]

        def build_toeplitz():
            nc.sync.dma_start(out=scratch.rearrange("(h r i) -> r h i", h=HEADS, r=P), in_=coef_row[:])

        def load_toeplitz():
            skewed = scratch.rearrange("(h z) -> h z", h=HEADS)[:, 0 : P * (PERIOD - 1)].rearrange("h (r w) -> r h w", r=P)
            nc.sync.dma_start(out=toeplitz[:], in_=skewed[:, :, 0:CLASS_LEN])

        norm_ps, mag_wide, mag_ps, k_square, norm_sb, parked, mag_t, field_q, short_t, summed, result = {}, {}, {}, {}, {}, {}, {}, {}, {}, {}, {}

        def passes(column_block, j):
            cols = slice(BANK * j, BANK * (j + 1))
            folded = first_folded <= column_block < PAIRS
            words, scales = (folded_words, folded_scales) if folded else (w_words, w_scales)
            block = column_block - first_folded if folded else column_block
            acc = psum.tile([P, BANK], F32, name="acc", tag="bank")
            for g in range(K_PASSES):
                nc.tensor.matmul_mx(
                    out=acc[:],
                    lhsT=words[:, g, 2 * P * block : 2 * P * (block + 1)].bitcast(FP4X4),
                    lhsT_scale=scales[:, g, P * block : P * (block + 1)],
                    rhs=x_codes[:, g, cols].bitcast(FP8X4),
                    rhs_scale=x_scales[:, g, cols],
                    start=(g == 0),
                    stop=(g == K_PASSES - 1),
                )
            return acc

        def project_k(group, j):
            k_square[group, j] = squares.tile([P, len(group), BANK], F32, name="k_square")
            for t, pair in enumerate(group):
                acc = passes(pair, j)
                nc.scalar.activation(
                    out=k_square[group, j][:, t, :], in_=acc[:], func=ACT.Square, bias=bias_col[:, pair : pair + 1]
                )

        def project_v(pair, j):
            acc = passes(PAIRS + pair, j)
            nc.scalar.activation(
                out=field_tiles[pair % 3][:, ROWS_PER_BANK * j : ROWS_PER_BANK * (j + 1), PAD:],
                in_=acc[:].rearrange("p (a q) -> p a q", a=ROWS_PER_BANK),
                func=ACT.Identity,
                bias=bias_col[:, PAIRS + pair : PAIRS + pair + 1],
            )

        def key_norms(group, j):
            size = len(group)
            if j == 0:
                norm_sb[group] = double.tile([P, 2 * size, TOKENS // P], F32, name="norm_sb")
            turned = psum.tile([P, BANK], F32, name="turned", tag="bank")
            for i in range(4):
                for t in range(size):
                    nc.tensor.matmul(
                        out=turned[:, P * i : P * (i + 1)],
                        lhsT=k_square[group, j][:, t, P * i : P * (i + 1)],
                        rhs=ident[:],
                        is_transpose=True,
                        start=(i == 0 and t == 0),
                        stop=(i == 3 and t == size - 1),
                    )
            norm_ps[group, j] = turned

        def add_channels(group, j):
            size = len(group)
            nc.vector.tensor_reduce(
                out=norm_sb[group][:, :, 4 * j : 4 * (j + 1)].rearrange("p h i -> p i h"),
                in_=norm_ps[group, j][:].rearrange("p (i h e) -> p i h e", i=4, h=2 * size),
                axis=AXIS.X,
                op=ALU.add,
            )

        def take_roots(group):
            rows = 2 * len(group) * TOKENS // P
            nc.scalar.activation(out=mag_q[:, 0:rows], in_=norm_sb[group][:].rearrange("p h t -> p (h t)"), func=ACT.Sqrt)

        def park_mag(group):
            rows = 2 * len(group) * TOKENS // P
            turned = psum.tile([P, P], F32, name="turned", tag="bank")
            nc.tensor.transpose(turned[:], mag_q[:], ident[:])
            mag_rows = single.tile([P, P], F32, name="mag_rows")
            nc.scalar.copy(out=mag_rows[0:rows, :], in_=turned[0:rows, :])
            end = out_flat.shape[0] - 2 * TOKENS * group[0]
            parked[group] = out_flat[end - rows * P : end]
            nc.sync.dma_start(out=parked[group].rearrange("(r q) -> r q", q=P), in_=mag_rows[0:rows, :])

        def spread_mag(pair):
            group, place = group_of(pair)
            mag_t[pair] = double.tile([P, TOKENS], F32, name="mag_t")
            for half in range(2):
                nc.sync.dma_start(
                    out=mag_t[pair][HEAD_DIM * half : HEAD_DIM * (half + 1), :],
                    in_=parked[group].rearrange("(h n) -> h n", n=TOKENS)[2 * place + half].partition_broadcast(HEAD_DIM),
                )

        def wide_roots(group, j):
            if j == 0:
                mag_wide[group] = x_pool.tile([P, 2 * TOKENS // P, HEAD_DIM], F32, name="mag_wide", tag="x_rows")
            cols = slice(2 * 4 * j, 2 * 4 * (j + 1))
            nc.scalar.activation(
                out=mag_wide[group][:, cols, :].rearrange("p (i h) e -> p i h e", h=2),
                in_=norm_sb[group][:, :, 4 * j : 4 * (j + 1)].rearrange("p h i -> p i h").unsqueeze(3).to_broadcast([P, 4, 2, HEAD_DIM]),
                func=ACT.Sqrt,
            )

        def spread_mag_by_tensor(group, j):
            mag_ps[group, j] = psum.tile([P, BANK], F32, name="mag_ps", tag="bank")
            wide = mag_wide[group][:].rearrange("p r e -> p (r e)")
            for i in range(4):
                nc.tensor.transpose(mag_ps[group, j][:, P * i : P * (i + 1)], wide[:, P * (4 * j + i) : P * (4 * j + i + 1)], ident[:])

        def shifted_field(field_t, shift, row0, row1):
            steps, residue = divmod(shift, STRIDE)
            if row0 >= residue:
                source, back = row0 - residue, steps
            else:
                source, back = row0 - residue + STRIDE, steps + 1
            return field_t[:, source : source + row1 - row0, PAD - back : PAD - back + CLASS_LEN]

        def multiply(pair, rows, mag):
            field_t = field_tiles[pair % 3]
            nc.vector.tensor_tensor(
                out=field_t[:, rows, PAD:],
                in0=field_t[:, rows, PAD:],
                in1=mag[:].rearrange("p (a q) -> p a q", q=CLASS_LEN),
                op=ALU.mult,
            )

        def make_field(pair):
            multiply(pair, slice(0, STRIDE), mag_t[pair])

        def make_first_field(j):
            multiply(0, slice(ROWS_PER_BANK * j, ROWS_PER_BANK * (j + 1)), mag_ps[GROUPS[0], j])

        def field_skips(pair):
            return skip_ops(field_tiles[pair % 3][:, :, PAD:])

        def short_pieces(pair, i):
            shift = short_shifts[i]
            family, m = places[shift]
            weight = short_coef[:, pair, family, m : m + 1]
            part = i % parts(pair)
            first = i < parts(pair)
            if first:
                short_t[pair, part] = x_pool.tile([P, STRIDE, CLASS_LEN], F32, name="short_t", tag="x_rows")
            blocks = BLOCKS if pair == PAIRS - 1 and i == len(short_shifts) - 1 else 1
            width = CLASS_LEN // blocks

            def piece(b, row0, row1):
                shifted = shifted_field(field_tiles[pair % 3], shift, row0, row1)[:, :, width * b : width * (b + 1)]
                rows = short_t[pair, part][:, row0:row1, width * b : width * (b + 1)]
                if first:
                    nc.scalar.activation(out=rows, in_=shifted, func=ACT.Copy, scale=weight)
                else:
                    nc.vector.scalar_tensor_tensor(out=rows, in0=shifted, scalar=weight, in1=rows, op0=ALU.mult, op1=ALU.add)

            halves = ((shift % STRIDE, STRIDE), (0, shift % STRIDE))
            return [(piece, (b, row0, row1)) for b, (row0, row1) in product(range(blocks), halves)]

        def turn_field(pair, j):
            if j == 0:
                field_q[pair] = double.tile([P, BLOCKS, 2, STRIDE, HEAD_DIM], F32, name="field_q")
            b, group = divmod(j, STRIDE // 4)
            turned = psum.tile([P, BANK], F32, name="turned", tag="bank")
            for i in range(4):
                nc.tensor.transpose(
                    turned[:, P * i : P * (i + 1)],
                    field_tiles[pair % 3][:, 4 * group + i, PAD + P * b : PAD + P * (b + 1)],
                    ident[:],
                )
            nc.scalar.copy(
                out=field_q[pair][:, b, :, 4 * group : 4 * group + 4, :],
                in_=turned[:].rearrange("p (a h e) -> p h a e", a=4, h=2),
            )

        def long_sum_terms(j):
            return [(half, source) for half in range(2) for source in range(j // (STRIDE // 4) + 1)]

        def long_sum(pair, j, half, source):
            b, group = divmod(j, STRIDE // 4)
            if half == 0 and source == 0:
                summed[pair, j] = psum.tile([P, 4, 2, HEAD_DIM], F32, name="summed", tag="bank")
            nc.tensor.matmul(
                out=summed[pair, j][:, :, half, :],
                lhsT=toeplitz[:, 2 * pair + half, P * (b - source) : P * (b - source + 1)],
                rhs=field_q[pair][:, source, half, 4 * group : 4 * group + 4, :],
                start=(half == 0 and source == 0),
                stop=False,
            )

        def add_short_part_and_store(pair, j):
            if j == 0:
                result[pair] = double.tile([P, BLOCKS, 2, STRIDE, HEAD_DIM], F32, name="result")
            b, group = divmod(j, STRIDE // 4)
            for part in range(parts(pair)):
                for i in range(4):
                    nc.tensor.matmul(
                        out=summed[pair, j][:, i, :, :],
                        lhsT=short_t[pair, part][:, 4 * group + i, P * b : P * (b + 1)],
                        rhs=ident[:].rearrange("p (h e) -> p h e", h=2),
                        is_transpose=True,
                        start=False,
                        stop=(part == parts(pair) - 1 and i == 3),
                    )
            copy = nc.vector.tensor_copy if pair == PAIRS - 1 and group == 0 else nc.scalar.copy
            copy(out=result[pair][:, b, :, 4 * group : 4 * group + 4, :], in_=summed[pair, j][:].rearrange("p a h e -> p h a e"))
            out_view = out[0, 2 * pair : 2 * pair + 2].rearrange("h (b p a) e -> b p h (a e)", b=BLOCKS, p=P, a=STRIDE)
            classes = slice(0, 0)
            if pair == PAIRS - 1 and b == BLOCKS - 1:
                classes = slice(4 * group, 4 * group + 4)
            elif group == STRIDE // 4 - 1:
                classes = slice(0, STRIDE)
            if classes.stop:
                nc.sync.dma_start(
                    out=out_view[b][:, :, HEAD_DIM * classes.start : HEAD_DIM * classes.stop],
                    in_=result[pair][:, b, :, classes, :].rearrange("p h a e -> p h (a e)"),
                )

        def live(pair):
            return 0 <= pair < PAIRS

        def run(pieces, count=99):
            for n in range(min(count, len(pieces))):
                piece, place = pieces.pop(0)
                piece(*place)

        def starts(pair):
            return [piece for i in range(parts(pair)) for piece in short_pieces(pair, i)]

        def rest(pair):
            return [piece for i in range(parts(pair), len(short_shifts)) for piece in short_pieces(pair, i)]

        head, second, third, late_keys = GROUPS
        load_root_table()
        warm(4)
        quantise_bank(0, [0])
        warm(1)
        quantise_bank(0, [1])
        warm(1)
        nc.vector.tensor_copy(out=bias_rows[0 : 2 * PAIRS, :], in_=bias_bf[:])
        quantise_bank(1, [0])
        quantise_bank(1, [1])
        turn_bias()
        weigh_skips()
        for group in GROUPS:
            if len(group) > 1:
                fold_weights(group)
        for j in range(BANKS):
            project_k(head, j)
            if j >= 1:
                key_norms(head, j - 1)
                add_channels(head, j - 1)
                wide_roots(head, j - 1)
            if j >= 2:
                spread_mag_by_tensor(head, j - 2)
                make_first_field(j - 2)
            if j + 2 < BANKS:
                quantise_bank(j + 2, [0])
                if j == 0:
                    divide_gains()
                else:
                    place_weights()
                project_v(0, j)
                quantise_bank(j + 2, [1])
                if j == 0:
                    weigh_taps()
                else:
                    build_toeplitz()
        project_v(0, 2)
        key_norms(head, BANKS - 1)
        add_channels(head, BANKS - 1)
        wide_roots(head, BANKS - 1)
        project_v(0, 3)
        for j in range(2, BANKS):
            spread_mag_by_tensor(head, j)
            make_first_field(j)

        skips = field_skips(0)
        for j in range(BANKS):
            project_k(second, j)
            run(skips, 2)
            if j >= 1:
                key_norms(second, j - 1)
        run(starts(0))
        for j in range(BANKS - 1):
            add_channels(second, j)
        key_norms(second, BANKS - 1)
        add_channels(second, BANKS - 1)
        short = rest(0)
        run(short, 2)
        for j in range(BANKS):
            project_k(third, j)
            if j == 0:
                take_roots(second)
            if j == 1:
                park_mag(second)
                spread_mag(1)
            if j >= 1:
                key_norms(third, j - 1)
                run(short, 1)
                add_channels(third, j - 1)
            if j >= 2:
                project_v(1, 2 * j - 4)
                project_v(1, 2 * j - 3)
        key_norms(third, BANKS - 1)
        run(short, 1)
        add_channels(third, BANKS - 1)

        pending = []
        for i in range(PAIRS + 1):
            skips = field_skips(i + 1) if live(i + 1) else []
            fillers = starts(i + 1) if live(i + 1) else []
            if live(i + 1):
                make_field(i + 1)
            if i > 0:
                short = rest(i) if live(i) else []
            run(short, 1)
            run(skips, 1)
            run(short, 1)
            run(skips)
            for unit in pending:
                add_channels(*unit)
            pending = []
            if i == 0:
                take_roots(third)
            if i == 2:
                take_roots(late_keys)
            if live(i + 2):
                for j in range(BANKS):
                    project_v(i + 2, j)
                    if i == 0 and j == 1:
                        park_mag(third)
                        spread_mag(2)
                if i != 0 and i != 2:
                    spread_mag(i + 2)
            late = [(late_keys, 2 * i), (late_keys, 2 * i + 1)] if i < 2 else []
            if late:
                project_k(*late[0])
            if i == 0:
                load_toeplitz()
                turn_field(0, 0)
                turn_field(0, 1)
                key_norms(*late[0])
                run(short, 2)
                project_k(*late[1])
                turn_field(0, 2)
                run(fillers, 1)
                turn_field(0, 3)
                run(short)
                add_channels(*late[0])
                key_norms(*late[1])
                run(fillers)
                pending = late[1:]
                continue
            if late:
                project_k(*late[1])
            early = live(i) and i >= EARLY
            for j in range(BANKS):
                terms = long_sum_terms(j) if live(i - 1) and i - 1 < EARLY else []
                for n, (half, source) in enumerate(terms):
                    long_sum(i - 1, j, half, source)
                    if n == 0 and live(i):
                        turn_field(i, j)
                if not terms and live(i):
                    turn_field(i, j)
                if late and j in (1, 2):
                    key_norms(*late[j - 1])
                if live(i - 1):
                    add_short_part_and_store(i - 1, j)
                run(short, 2)
                if i == 2 and j == 0:
                    park_mag(late_keys)
                    spread_mag(4)
                if j >= 2:
                    run(fillers, 1)
                if early and j >= 1:
                    for half, source in long_sum_terms(j - 1):
                        long_sum(i, j - 1, half, source)
            run(short)
            for unit in late:
                add_channels(*unit)
            run(fillers)
            if early:
                for half, source in long_sum_terms(BANKS - 1):
                    long_sum(i, BANKS - 1, half, source)
